import numpy as np
import ml_dtypes


def mxq(x, axis, fmt="e4m3"):
    dtype, down = {"e4m3": (ml_dtypes.float8_e4m3fn, 7), "e5m2": (ml_dtypes.float8_e5m2, 14)}[fmt]
    v = np.moveaxis(np.asarray(x, np.float32).astype(ml_dtypes.bfloat16).astype(np.float64), axis, -1)
    blocks = v.reshape(v.shape[:-1] + (-1, 32))
    amax = np.abs(blocks).max(-1, keepdims=True)
    byte = np.maximum(np.where(amax > 0, np.frexp(amax)[1] - 1 + 127, 0) - down, 1)
    scale = np.exp2(byte - 127.0)
    codes = (blocks / scale).astype(np.float32).astype(dtype).astype(np.float64)
    return np.moveaxis((codes * scale).reshape(v.shape), -1, axis)


WIDE = False


def mx_kscale(k):
    if not WIDE:
        return np.ones(k)
    levels = np.array([10, -10, 5, -5, 0])
    if k % 512:
        return np.exp2(np.random.permutation(np.resize(levels, k // 32))).repeat(32)
    a = np.empty((k // 512, 16))
    for p in range(k // 512):
        a[p, :8] = np.random.permutation(np.resize(levels, 8))
        for g in range(8):
            far = levels[np.abs(levels - a[p, g]) >= 10]
            a[p, g + 8] = far[np.random.randint(len(far))]
    return np.exp2(a.ravel()).repeat(32)


BF16 = ml_dtypes.bfloat16


def bf(x):
    return np.asarray(x, np.float32).astype(BF16)


def f64(x):
    return np.asarray(x).astype(np.float64)


B, IN_C, OUT_C, HM, HN, NL = 4096, 512, 256, 1024, 4, 3


def rmsnorm2d(v):
    for d in (-2, -1):
        v = v - v.mean(d, keepdims=True)
        v = v / np.maximum(np.sqrt(np.mean(v * v, d, keepdims=True)), 1e-8)
    return v


def setup_inputs():
    s = mx_kscale(HM)
    g = np.random.standard_normal((B, HN))
    e = np.exp(g - g.max(-1, keepdims=True))
    return {"h_pre": bf(1.5 * np.random.standard_normal((B, HN, HM)) * s),
            "W_mo": bf(np.random.standard_normal((HN, HM, OUT_C)) / np.sqrt(HM) / s[None, :, None]),
            "weights_n": bf(e / e.sum(-1, keepdims=True)),
            "leak_n": bf(np.random.uniform(-2.0, 2.0, HN))}


def reference(h_pre, W_mo, weights_n, leak_n):
    h = f64(h_pre)
    h = np.where(h < 0, h * f64(leak_n)[:, None], h)
    y = (mxq(h, 2, "e4m3").transpose(1, 0, 2) @ mxq(f64(W_mo), 1, "e4m3")).transpose(1, 0, 2)
    y = y * f64(weights_n)[..., None]
    return rmsnorm2d(y).mean(-2)

@@ -1,0 +1,455 @@
+from contextlib import ExitStack
+
+import concourse.mybir as mybir
+from concourse.masks import make_identity
+
+F32 = mybir.dt.float32
+BF16 = mybir.dt.bfloat16
+U32 = mybir.dt.uint32
+U8 = mybir.dt.uint8
+FP8X4 = mybir.dt.float8_e4m3fn_x4
+ALU = mybir.AluOpType
+ACT = mybir.ActivationFunctionType
+AX = mybir.AxisListType
+
+P = 128
+B, HN, HM, OC = 4096, 4, 1024, 256
+NT = B // P
+NS = NT * HN
+GROUP = 4
+NG = NT // GROUP
+FLOPS = 2 * B * HN * HM * OC
+
+PIN = True
+XY_BUFS = 8
+AHEAD = 3
+ORDER = [
+    ("wr0", 3),
+    ("qs", 21),
+    ("usq1", 28),
+    ("wr2", 4),
+    ("wr3", 4),
+    ("usq0", 31),
+    ("nmb", 18),
+    ("T", (5, 5, 5, 5)),
+    ("wr5", 4),
+    ("quant", (9, 8, 9, 8)),
+    ("wr4", 6),
+    ("wq3", 8),
+    ("flip", (0, 1, 0, 1)),
+    ("wr6", 5),
+    ("ce0", 18),
+    ("u3", 23),
+    ("wq2", 7),
+    ("wr1", 3),
+    ("wq1", 6),
+    ("L", (7, 6, 7, 6)),
+    ("usq3", 25),
+    ("wq0", 5),
+    ("u2", 23),
+    ("mx", (10, 9, 10, 9)),
+    ("u0", 23),
+    ("usq2", 26),
+    ("weigh", (11, 11, 11, 11)),
+    ("sq0", 19),
+    ("r", 22),
+    ("wr7", 6),
+    ("max", (7, 7, 7, 7)),
+    ("rb", 22),
+    ("nm", 16),
+    ("sum", 15),
+    ("u1", 23),
+]
+W_ON_SCALAR = (1, 3, 5, 7)
+FIN_BASE = 44
+ADVANCED = ("flip", "T", "L", "max", "quant")
+ADV_FROM = 96
+ADV_EVERY = 4
+ADV_MAX = 0
+GROUPS = [(4 * i, 4) for i in range(7)] + [(28, 3), (31, 1)]
+TAIL_FROM = 24
+USQ_T0 = 27
+USQ_T1 = 29
+USQ_T2 = 25
+USQ_T3 = 25
+FIN_T0 = 27
+FIN_T1 = 27
+FIN_T2 = 30
+
+
+def l_on_vector(t, n):
+    return n == 3 and t % 4 != 3
+
+
+def tile_tensormoe_pb_t_kernel(tc, h_pre, W_mo, weights_n, leak_n, out):
+    nc = tc.nc
+    with ExitStack() as ctx:
+        if PIN:
+            ctx.enter_context(tc.manual_schedule())
+        const = ctx.enter_context(tc.tile_pool(name="const", bufs=1))
+        work = ctx.enter_context(tc.tile_pool(name="work", bufs=2))
+        xpsum = ctx.enter_context(tc.psum_pool(name="xpsum", bufs=XY_BUFS))
+        mpsum = xpsum
+
+        h_view = h_pre.rearrange("(p t) n m -> p t (n m)", t=NT)
+        out_view = out.rearrange("(p t) o -> p t o", t=NT)
+
+        lkb = const.tile([P, HN], BF16)
+        nc.sync.dma_start(out=lkb[:], in_=leak_n.partition_broadcast(P))
+        wtb = const.tile([P, NT * HN], BF16)
+        nc.sync.dma_start(out=wtb[:], in_=weights_n.rearrange("(p t) n -> p (t n)", t=NT))
+
+        H = {}
+        X = {}
+        L = {}
+        G = {}
+        Q = {}
+        Y = {}
+        Z = {}
+        C = {}
+        C2 = {}
+        MA = {}
+        MB = {}
+        TT = {}
+        U = {}
+        FIN = {}
+        UC = {}
+
+        def load(t, pieces):
+            hsb = work.tile([P, HN * HM], BF16, name="hsb", bufs=6)
+            w = HN * HM // pieces
+            for i in range(pieces):
+                nc.sync.dma_start(out=hsb[:, i * w : (i + 1) * w], in_=h_view[:, t, i * w : (i + 1) * w])
+            H[t] = hsb
+
+        load(0, HN)
+        wraw = const.tile([P, 16 * 512], BF16)
+        nc.sync.dma_start(
+            out=wraw[:].rearrange("p (a r) -> p a r", a=8),
+            in_=W_mo.rearrange("n (g p t) o -> p (n g) (t o)", g=2, p=P, t=4),
+        )
+        for t in range(1, AHEAD):
+            load(t, 1)
+
+        ident = const.tile([P, P], F32)
+        make_identity(nc, ident[:])
+
+        one = const.tile([P, 1], F32)
+        nc.vector.memset(one[:], 1.0)
+        warm = const.tile([P, 1], F32)
+        nc.scalar.activation(out=warm[:], in_=one[:], func=ACT.Abs_reciprocal_sqrt)
+
+        lk = const.tile([P, HN], F32)
+        nc.vector.tensor_copy(out=lk[:], in_=lkb[:])
+        sg = const.tile([P, HN], F32)
+        nc.vector.tensor_scalar(out=sg[:], in0=lk[:], scalar1=1.0, scalar2=-2.0, op0=ALU.is_gt, op1=ALU.mult)
+        nc.vector.tensor_scalar_add(out=sg[:], in0=sg[:], scalar1=1.0)
+        wp = const.tile([P, NT, HN], F32)
+        nc.vector.tensor_tensor(
+            out=wp[:],
+            in0=wtb[:].rearrange("p (t n) -> p t n", n=HN),
+            in1=sg[:].unsqueeze(1).to_broadcast([P, NT, HN]),
+            op=ALU.mult,
+        )
+        wgrp = const.tile([P, 8192], BF16, align_bytes=64)
+        wcodes = const.tile([P, 2048], U32, align_bytes=64)
+        wscales = const.tile([P, 2048], U8, align_bytes=64)
+        su = const.tile([P, NT, HN], F32)
+        sq = const.tile([P, NT, HN], F32)
+
+        wsrc = wraw[:].rearrange("p (a t o) -> p a o t", a=8, t=4, o=OC)
+        wdst = wgrp[:].rearrange("p (a o t) -> p a o t", a=8, t=4, o=OC)
+
+        def w_regroup(a):
+            if a in W_ON_SCALAR:
+                nc.scalar.copy(out=wdst[:, a], in_=wsrc[:, a])
+            else:
+                nc.vector.tensor_copy(out=wdst[:, a], in_=wsrc[:, a])
+
+        def w_quantise(n):
+            nc.vector.quantize_mx(
+                out=wcodes[:, n * 512 : (n + 1) * 512].bitcast(FP8X4),
+                scales=wscales[:, n * 512 : (n + 1) * 512],
+                in_=wgrp[:, n * 2048 : (n + 1) * 2048],
+            )
+
+        def flip(s):
+            t, n = divmod(s, HN)
+            sl = H[t][:, n * HM : (n + 1) * HM]
+            nc.vector.tensor_scalar(out=sl, in0=sl, scalar1=sg[:, n : n + 1], scalar2=None, op0=ALU.mult)
+
+        def transposes(s):
+            t, n = divmod(s, HN)
+            hw = H[t][:].bitcast(F32)
+            xt = xpsum.tile([P, 512], F32, name="xt", tag="xy")
+            for u in range(2):
+                for g in range(2):
+                    j = u * 2 + g
+                    c0 = n * 512 + g * 256
+                    nc.tensor.transpose(xt[:, j * P : (j + 1) * P], hw[:, c0 + u : c0 + 256 : 2], ident[:])
+            X[s] = xt
+            if n == HN - 1:
+                H.pop(t)
+
+        def leak_times(s):
+            t, n = divmod(s, HN)
+            xb = X[s][:].bitcast(BF16)
+            lt = work.tile([P, HM], BF16, name="lt", bufs=4)
+            if l_on_vector(t, n):
+                nc.vector.tensor_scalar(out=lt[:], in0=xb, scalar1=lk[:, n : n + 1], scalar2=None, op0=ALU.mult)
+            else:
+                nc.scalar.activation(out=lt[:], in_=xb, func=ACT.Copy, scale=lk[:, n : n + 1])
+            L[s] = lt
+
+        def take_max(s):
+            xb = X.pop(s)[:].bitcast(BF16)
+            lt = L.pop(s)
+            grp = work.tile([P, HM], BF16, name="grp", bufs=4, align_bytes=64)
+            nc.vector.tensor_tensor(
+                out=grp[:].rearrange("p (w u e) -> p w u e", u=2, e=2),
+                in0=lt[:].rearrange("p (u w e) -> p w u e", u=2, e=2),
+                in1=xb.rearrange("p (u w e) -> p w u e", u=2, e=2),
+                op=ALU.max,
+            )
+            G[s] = grp
+
+        def quantise(s):
+            grp = G.pop(s)
+            codes = work.tile([P, 256], U32, name="codes", bufs=8, align_bytes=64)
+            scales = work.tile([P, 256], U8, name="scales", bufs=8, align_bytes=64)
+            nc.vector.quantize_mx(out=codes[:].bitcast(FP8X4), scales=scales[:], in_=grp[:])
+            Q[s] = (codes, scales)
+
+        def mx(s):
+            t, n = divmod(s, HN)
+            codes, scales = Q.pop(s)
+            if n % 2 == 0:
+                y = xpsum.tile([P, 2, OC], F32, name="y", tag="xy")
+                Y[s // 2] = y
+            y = Y[s // 2]
+            for g in range(2):
+                a = n * 2 + g
+                nc.tensor.matmul_mx(
+                    out=y[:, n % 2, :],
+                    lhsT=codes[:, g * P : (g + 1) * P].bitcast(FP8X4),
+                    lhsT_scale=scales[:, g * P : (g + 1) * P],
+                    rhs=wcodes[:, a * OC : (a + 1) * OC].bitcast(FP8X4),
+                    rhs_scale=wscales[:, a * OC : (a + 1) * OC],
+                    start=(g == 0),
+                    stop=(g == 1),
+                )
+
+        def weigh(s):
+            t, n = divmod(s, HN)
+            if n == 0:
+                z = work.tile([P, HN, OC], F32, name="z", bufs=3)
+                Z[t] = z
+            y = Y[s // 2]
+            nc.scalar.activation(out=Z[t][:, n, :], in_=y[:, n % 2, :], func=ACT.Copy, scale=wp[:, t, n : n + 1])
+            if n % 2 == 1:
+                Y.pop(s // 2)
+
+        def sum_over_experts(src, tagname):
+            m = mpsum.tile([P, 512], F32, name=tagname, tag="xy")
+            for hf in range(2):
+                for n in range(HN):
+                    nc.tensor.matmul(
+                        out=m[:, hf * P : (hf + 1) * P],
+                        lhsT=src[:, n, hf * P : (hf + 1) * P],
+                        rhs=ident[:],
+                        start=(n == 0),
+                        stop=(n == HN - 1),
+                        is_transpose=True,
+                    )
+            return m
+
+        def back(m, src_t):
+            for hf in range(2):
+                nc.tensor.transpose(m[:, 256 + hf * P : 256 + (hf + 1) * P], src_t[:, hf * P : (hf + 1) * P], ident[:])
+
+        def e_sum(t):
+            MA[t] = sum_over_experts(Z[t], "mA")
+
+        def e_nm(t):
+            nmt = work.tile([P, OC], F32, name="nmt")
+            nc.scalar.activation(out=nmt[:], in_=MA[t][:, 0:256], func=ACT.Copy, scale=-0.25)
+            TT[t] = nmt
+
+        def e_nmback(t):
+            back(MA[t], TT.pop(t))
+
+        def e_centre(t):
+            c = work.tile([P, HN, OC], F32, name="c", bufs=3)
+            nm = MA.pop(t)[:, 256:512]
+            nc.vector.tensor_tensor(
+                out=c[:], in0=Z.pop(t)[:], in1=nm.unsqueeze(1).to_broadcast([P, HN, OC]), op=ALU.add
+            )
+            C[t] = c
+
+        def e_square(t):
+            c2 = work.tile([P, HN, OC], F32, name="c2")
+            nc.scalar.activation(out=c2[:], in_=C[t][:], func=ACT.Square)
+            C2[t] = c2
+
+        def e_q(t):
+            MB[t] = sum_over_experts(C2.pop(t), "mB")
+
+        def e_r(t):
+            rt = work.tile([P, OC], F32, name="rt")
+            nc.scalar.activation(out=rt[:], in_=MB[t][:, 0:256], func=ACT.Abs_reciprocal_sqrt, scale=0.25)
+            TT[t] = rt
+
+        def e_rback(t):
+            back(MB[t], TT.pop(t))
+
+        def e_u(t, n):
+            if t not in U:
+                u = work.tile([P, HN, OC], F32, name="u", bufs=10)
+                U[t] = u
+                UC[t] = 0
+            nc.vector.scalar_tensor_tensor(
+                out=U[t][:, n, :], in0=MB[t][:, 256:512], scalar=1.0e8, in1=C[t][:, n, :], op0=ALU.min, op1=ALU.mult,
+                accum_out=su[:, t, n : n + 1],
+            )
+            UC[t] += 1
+            if UC[t] == HN:
+                MB.pop(t)
+                C.pop(t)
+
+        def e_usq(t, n):
+            junk = work.tile([P, OC], F32, name="junk")
+            nc.scalar.activation(out=junk[:], in_=U[t][:, n, :], func=ACT.Square, accum_out=sq[:, t, n : n + 1])
+
+        def fin(gi, step):
+            t0, size = GROUPS[gi]
+            ts = slice(t0, t0 + size)
+
+            def small(name):
+                return work.tile([P, size, HN], F32, name=name)
+
+            if step == 0:
+                mu = small("mu")
+                nc.vector.tensor_scalar_mul(out=mu[:], in0=su[:, ts, :], scalar1=1.0 / OC)
+                FIN[gi] = {"mu": mu}
+            f = FIN[gi]
+            if step == 1:
+                m2 = small("m2")
+                nc.vector.tensor_tensor(out=m2[:], in0=f["mu"][:], in1=f["mu"][:], op=ALU.mult)
+                f["m2"] = m2
+            if step == 2:
+                var = small("var")
+                nc.vector.scalar_tensor_tensor(
+                    out=var[:], in0=sq[:, ts, :], scalar=1.0 / OC, in1=f["m2"][:], op0=ALU.mult, op1=ALU.subtract
+                )
+                f["var"] = var
+            if step == 3:
+                a = small("a")
+                nc.scalar.activation(out=a[:], in_=f["var"][:], func=ACT.Abs_reciprocal_sqrt)
+                f["a"] = a
+            if step == 4:
+                a4 = small("a4")
+                nc.vector.tensor_scalar(out=a4[:], in0=f["a"][:], scalar1=1.0e8, scalar2=0.25, op0=ALU.min, op1=ALU.mult)
+                f["a4"] = a4
+            if step == 5:
+                am = small("am")
+                nc.vector.scalar_tensor_tensor(
+                    out=am[:], in0=f["mu"][:], scalar=-1.0, in1=f["a4"][:], op0=ALU.mult, op1=ALU.mult
+                )
+                f["am"] = am
+                dl = work.tile([P, size, 3], F32, name="dl")
+                nc.vector.tensor_tensor(
+                    out=dl[:], in0=f["a4"][:, :, 0:3], in1=f["a4"][:, :, 3:4].to_broadcast([P, size, 3]), op=ALU.subtract
+                )
+                f["dl"] = dl
+            if step == 6:
+                nk = work.tile([P, size], F32, name="nk")
+                nc.vector.tensor_reduce(out=nk[:], in_=f["am"][:], axis=AX.X, op=ALU.add)
+                f["nk"] = nk
+                ob = work.tile([P, size, OC], F32, name="ob")
+                f["ob"] = ob
+
+        def fin_first(gi, k):
+            f = FIN[gi]
+            f0 = work.tile([P, OC], F32, name="f0")
+            if GROUPS[gi][1] < GROUP:
+                nc.vector.tensor_scalar(
+                    out=f0[:], in0=U[GROUPS[gi][0] + k][:, 0, :], scalar1=f["dl"][:, k, 0:1], scalar2=f["nk"][:, k : k + 1],
+                    op0=ALU.mult, op1=ALU.add,
+                )
+            else:
+                nc.scalar.activation(
+                    out=f0[:], in_=U[GROUPS[gi][0] + k][:, 0, :], func=ACT.Identity,
+                    scale=f["dl"][:, k, 0:1], bias=f["nk"][:, k : k + 1],
+                )
+            f[("f0", k)] = f0
+
+        def fin_rest(gi, k):
+            f = FIN[gi]
+            u = U.pop(GROUPS[gi][0] + k)
+            f1 = work.tile([P, OC], F32, name="f1")
+            nc.vector.scalar_tensor_tensor(
+                out=f1[:], in0=u[:, 1, :], scalar=f["dl"][:, k, 1:2], in1=f[("f0", k)][:], op0=ALU.mult, op1=ALU.add
+            )
+            nc.vector.scalar_tensor_tensor(
+                out=f["ob"][:, k, :], in0=u[:, 2, :], scalar=f["dl"][:, k, 2:3], in1=f1[:], op0=ALU.mult, op1=ALU.add
+            )
+
+        def fin_store(gi):
+            f = FIN.pop(gi)
+            t0, size = GROUPS[gi]
+            nc.sync.dma_start(out=out_view[:, t0 : t0 + size, :], in_=f["ob"][:])
+
+        bank_stage = {
+            "flip": flip, "T": transposes, "L": leak_times, "max": take_max, "quant": quantise, "mx": mx, "weigh": weigh,
+        }
+        tile_stage = {
+            "sum": e_sum, "nm": e_nm, "nmb": e_nmback, "ce0": e_centre, "sq0": e_square, "qs": e_q, "r": e_r, "rb": e_rback,
+        }
+
+        events = {}
+
+        def at(step, rank, sub, fn, args):
+            if step not in events:
+                events[step] = []
+            events[step].append((rank, sub, len(events[step]), fn, args))
+
+        def advance(s):
+            return min(ADV_MAX, max(0, (s - ADV_FROM) // ADV_EVERY))
+
+        for rank, (name, lag) in enumerate(ORDER):
+            if name in bank_stage:
+                for s in range(NS):
+                    adv = advance(s) if name in ADVANCED else 0
+                    at(s + lag[s % HN] - adv, rank, s, bank_stage[name], (s,))
+            elif name[0:2] == "wr":
+                at(lag, rank, 0, w_regroup, (int(name[2]),))
+            elif name[0:2] == "wq":
+                at(lag, rank, 0, w_quantise, (int(name[2]),))
+            elif name in tile_stage:
+                for t in range(NT):
+                    at(HN * t + lag, rank, t, tile_stage[name], (t,))
+            elif name[0:3] == "usq":
+                n = int(name[3])
+                for t in range(NT):
+                    at(HN * t + (lag if t < TAIL_FROM else (USQ_T0, USQ_T1, USQ_T2, USQ_T3)[n]), rank, t, e_usq, (t, n))
+            else:
+                for t in range(NT):
+                    at(HN * t + lag, rank, t, e_u, (t, int(name[1])))
+        flip_lag = [lag for name, lag in ORDER if name == "flip"][0]
+        for t in range(AHEAD, NT):
+            at(HN * t + flip_lag[0] - advance(HN * t) - HN * AHEAD, -1, t, load, (t, 1))
+        after = len(ORDER)
+        for gi in range(len(GROUPS)):
+            t0, size = GROUPS[gi]
+            base = HN * (t0 + size - GROUP) + FIN_BASE
+            if t0 >= TAIL_FROM:
+                base = HN * (t0 + size - 1) + (FIN_T0, FIN_T1, FIN_T2)[gi - len(GROUPS) + 3]
+            for step in range(7):
+                at(base + step, after, gi, fin, (gi, step))
+            for k in range(size):
+                at(base + 7 + k, after + 1, gi, fin_first, (gi, k))
+                at(base + 8 + k, after + 2, gi, fin_rest, (gi, k))
+            at(base + 9 + size, after + 3, gi, fin_store, (gi,))
+        for step in sorted(events):
+            for rank, sub, k, fn, args in sorted(events[step], key=lambda ev: ev[0:3]):
+                fn(*args)

@@ -17,79 +17,26 @@ B, HN, HM, OC = 4096, 4, 1024, 256
 NT = B // P
 NS = NT * HN
 GROUP = 4
-NG = NT // GROUP
 FLOPS = 2 * B * HN * HM * OC
 
-PIN = True
-XY_BUFS = 8
+AT_PSUM = (0, 1, 2, 3)
+NZ = HN - len(AT_PSUM)
 AHEAD = 3
-ORDER = [
-    ("wr0", 3),
-    ("qs", 21),
-    ("usq1", 28),
-    ("wr2", 4),
-    ("wr3", 4),
-    ("usq0", 31),
-    ("nmb", 18),
-    ("T", (5, 5, 5, 5)),
-    ("wr5", 4),
-    ("quant", (9, 8, 9, 8)),
-    ("wr4", 6),
-    ("wq3", 8),
-    ("flip", (0, 1, 0, 1)),
-    ("wr6", 5),
-    ("ce0", 18),
-    ("u3", 23),
-    ("wq2", 7),
-    ("wr1", 3),
-    ("wq1", 6),
-    ("L", (7, 6, 7, 6)),
-    ("usq3", 25),
-    ("wq0", 5),
-    ("u2", 23),
-    ("mx", (10, 9, 10, 9)),
-    ("u0", 23),
-    ("usq2", 26),
-    ("weigh", (11, 11, 11, 11)),
-    ("sq0", 19),
-    ("r", 22),
-    ("wr7", 6),
-    ("max", (7, 7, 7, 7)),
-    ("rb", 22),
-    ("nm", 16),
-    ("sum", 15),
-    ("u1", 23),
-]
-W_ON_SCALAR = (1, 3, 5, 7)
-FIN_BASE = 44
-ADVANCED = ("flip", "T", "L", "max", "quant")
-ADV_FROM = 96
-ADV_EVERY = 4
-ADV_MAX = 0
-GROUPS = [(4 * i, 4) for i in range(7)] + [(28, 3), (31, 1)]
-TAIL_FROM = 24
-USQ_T0 = 27
-USQ_T1 = 29
-USQ_T2 = 25
-USQ_T3 = 25
-FIN_T0 = 27
-FIN_T1 = 27
-FIN_T2 = 30
 
 
 def l_on_vector(t, n):
-    return n == 3 and t % 4 != 3
+    return n == 3 and t % 3 != 0
 
 
 def tile_tensormoe_pb_t_kernel(tc, h_pre, W_mo, weights_n, leak_n, out):
     nc = tc.nc
     with ExitStack() as ctx:
-        if PIN:
-            ctx.enter_context(tc.manual_schedule())
+        ctx.enter_context(tc.manual_schedule())
         const = ctx.enter_context(tc.tile_pool(name="const", bufs=1))
         work = ctx.enter_context(tc.tile_pool(name="work", bufs=2))
-        xpsum = ctx.enter_context(tc.psum_pool(name="xpsum", bufs=XY_BUFS))
-        mpsum = xpsum
+        xpsum = ctx.enter_context(tc.psum_pool(name="xpsum", bufs=4))
+        ypsum = ctx.enter_context(tc.psum_pool(name="ypsum", bufs=2))
+        mpsum = ctx.enter_context(tc.psum_pool(name="mpsum", bufs=2))
 
         h_view = h_pre.rearrange("(p t) n m -> p t (n m)", t=NT)
         out_view = out.rearrange("(p t) o -> p t o", t=NT)
@@ -99,35 +46,31 @@ def tile_tensormoe_pb_t_kernel(tc, h_pre, W_mo, weights_n, leak_n, out):
         wtb = const.tile([P, NT * HN], BF16)
         nc.sync.dma_start(out=wtb[:], in_=weights_n.rearrange("(p t) n -> p (t n)", t=NT))
 
-        H = {}
-        X = {}
-        L = {}
-        G = {}
-        Q = {}
-        Y = {}
-        Z = {}
-        C = {}
-        C2 = {}
-        MA = {}
-        MB = {}
-        TT = {}
-        U = {}
-        FIN = {}
-        UC = {}
+        DT, NEG, H, X, LT, G, Q, Y, Z, C, C2, MA, MB, TT, U, FIN = {}, {}, {}, {}, {}, {}, {}, {}, {}, {}, {}, {}, {}, {}, {}, {}
 
         def load(t, pieces):
-            hsb = work.tile([P, HN * HM], BF16, name="hsb", bufs=6)
+            hsb = work.tile([P, HN * HM], BF16, name="hsb", bufs=AHEAD + 3)
             w = HN * HM // pieces
             for i in range(pieces):
                 nc.sync.dma_start(out=hsb[:, i * w : (i + 1) * w], in_=h_view[:, t, i * w : (i + 1) * w])
             H[t] = hsb
 
-        load(0, HN)
-        wraw = const.tile([P, 16 * 512], BF16)
-        nc.sync.dma_start(
-            out=wraw[:].rearrange("p (a r) -> p a r", a=8),
-            in_=W_mo.rearrange("n (g p t) o -> p (n g) (t o)", g=2, p=P, t=4),
-        )
+        wraw = const.tile([P, 8 * 1024], BF16)
+        w_view = W_mo.rearrange("n (g p j) o -> p (n g) (j o)", g=2, p=P, j=4)
+
+        def load_w(n):
+            for g in range(2):
+                a = 2 * n + g
+                nc.sync.dma_start(
+                    out=wraw[:, a * 1024 : (a + 1) * 1024],
+                    in_=w_view[:, a, :],
+                )
+
+        hsb0 = work.tile([P, HN * HM], BF16, name="hsb", bufs=AHEAD + 3)
+        H[0] = hsb0
+        for n in range(HN):
+            nc.sync.dma_start(out=hsb0[:, n * HM : (n + 1) * HM], in_=h_view[:, 0, n * HM : (n + 1) * HM])
+            load_w(n)
         for t in range(1, AHEAD):
             load(t, 1)
 
@@ -144,6 +87,8 @@ def tile_tensormoe_pb_t_kernel(tc, h_pre, W_mo, weights_n, leak_n, out):
         sg = const.tile([P, HN], F32)
         nc.vector.tensor_scalar(out=sg[:], in0=lk[:], scalar1=1.0, scalar2=-2.0, op0=ALU.is_gt, op1=ALU.mult)
         nc.vector.tensor_scalar_add(out=sg[:], in0=sg[:], scalar1=1.0)
+        sl = const.tile([P, HN], F32)
+        nc.vector.tensor_tensor(out=sl[:], in0=sg[:], in1=lk[:], op=ALU.mult)
         wp = const.tile([P, NT, HN], F32)
         nc.vector.tensor_tensor(
             out=wp[:],
@@ -157,11 +102,11 @@ def tile_tensormoe_pb_t_kernel(tc, h_pre, W_mo, weights_n, leak_n, out):
         su = const.tile([P, NT, HN], F32)
         sq = const.tile([P, NT, HN], F32)
 
-        wsrc = wraw[:].rearrange("p (a t o) -> p a o t", a=8, t=4, o=OC)
-        wdst = wgrp[:].rearrange("p (a o t) -> p a o t", a=8, t=4, o=OC)
+        wsrc = wraw[:].rearrange("p (a j o) -> p a o j", a=8, j=4, o=OC)
+        wdst = wgrp[:].rearrange("p (a o j) -> p a o j", a=8, j=4, o=OC)
 
         def w_regroup(a):
-            if a in W_ON_SCALAR:
+            if a % 2 == 1:
                 nc.scalar.copy(out=wdst[:, a], in_=wsrc[:, a])
             else:
                 nc.vector.tensor_copy(out=wdst[:, a], in_=wsrc[:, a])
@@ -175,69 +120,76 @@ def tile_tensormoe_pb_t_kernel(tc, h_pre, W_mo, weights_n, leak_n, out):
 
         def flip(s):
             t, n = divmod(s, HN)
-            sl = H[t][:, n * HM : (n + 1) * HM]
-            nc.vector.tensor_scalar(out=sl, in0=sl, scalar1=sg[:, n : n + 1], scalar2=None, op0=ALU.mult)
+            x = H[t][:, n * HM : (n + 1) * HM]
+            nc.vector.tensor_scalar(out=x, in0=x, scalar1=sg[:, n : n + 1], scalar2=None, op0=ALU.mult)
 
         def transposes(s):
             t, n = divmod(s, HN)
             hw = H[t][:].bitcast(F32)
-            xt = xpsum.tile([P, 512], F32, name="xt", tag="xy")
+            xt = xpsum.tile([P, 512], F32, name="xt")
             for u in range(2):
                 for g in range(2):
                     j = u * 2 + g
                     c0 = n * 512 + g * 256
                     nc.tensor.transpose(xt[:, j * P : (j + 1) * P], hw[:, c0 + u : c0 + 256 : 2], ident[:])
             X[s] = xt
-            if n == HN - 1:
-                H.pop(t)
 
-        def leak_times(s):
+        def pair_half(s):
+            if s // 2 not in G:
+                grp = work.tile([P, 2 * HM], BF16, name="grp", bufs=3, align_bytes=64)
+                G[s // 2] = grp
+            return G[s // 2][:, (s % 2) * HM : (s % 2 + 1) * HM]
+
+        def leave(s):
             t, n = divmod(s, HN)
-            xb = X[s][:].bitcast(BF16)
-            lt = work.tile([P, HM], BF16, name="lt", bufs=4)
-            if l_on_vector(t, n):
-                nc.vector.tensor_scalar(out=lt[:], in0=xb, scalar1=lk[:, n : n + 1], scalar2=None, op0=ALU.mult)
+            if n in AT_PSUM:
+                lt = work.tile([P, HM], BF16, name="lt", bufs=4)
+                if l_on_vector(t, n):
+                    nc.vector.tensor_scalar(out=lt[:], in0=X[s][:].bitcast(BF16), scalar1=lk[:, n : n + 1], scalar2=None, op0=ALU.mult)
+                else:
+                    nc.scalar.activation(out=lt[:], in_=X[s][:].bitcast(BF16), func=ACT.Copy, scale=lk[:, n : n + 1])
+                LT[s] = lt
             else:
-                nc.scalar.activation(out=lt[:], in_=xb, func=ACT.Copy, scale=lk[:, n : n + 1])
-            L[s] = lt
+                nc.scalar.copy(
+                    out=pair_half(s).bitcast(F32).rearrange("p (w u) -> p w u", u=2),
+                    in_=X.pop(s)[:].rearrange("p (u w) -> p w u", u=2),
+                )
 
-        def take_max(s):
-            xb = X.pop(s)[:].bitcast(BF16)
-            lt = L.pop(s)
-            grp = work.tile([P, HM], BF16, name="grp", bufs=4, align_bytes=64)
+        def rectify_psum(s):
+            t, n = divmod(s, HN)
+            if n not in AT_PSUM:
+                return
             nc.vector.tensor_tensor(
-                out=grp[:].rearrange("p (w u e) -> p w u e", u=2, e=2),
-                in0=lt[:].rearrange("p (u w e) -> p w u e", u=2, e=2),
-                in1=xb.rearrange("p (u w e) -> p w u e", u=2, e=2),
+                out=pair_half(s).rearrange("p (w u e) -> p w u e", u=2, e=2),
+                in0=LT.pop(s)[:].rearrange("p (u w e) -> p w u e", u=2, e=2),
+                in1=X.pop(s)[:].bitcast(BF16).rearrange("p (u w e) -> p w u e", u=2, e=2),
                 op=ALU.max,
             )
-            G[s] = grp
 
-        def quantise(s):
-            grp = G.pop(s)
-            codes = work.tile([P, 256], U32, name="codes", bufs=8, align_bytes=64)
-            scales = work.tile([P, 256], U8, name="scales", bufs=8, align_bytes=64)
+        def quantise(q):
+            grp = G.pop(q)
+            codes = work.tile([P, 512], U32, name="codes", bufs=4, align_bytes=64)
+            scales = work.tile([P, 512], U8, name="scales", bufs=4, align_bytes=64)
             nc.vector.quantize_mx(out=codes[:].bitcast(FP8X4), scales=scales[:], in_=grp[:])
-            Q[s] = (codes, scales)
+            Q[q] = (codes, scales)
 
-        def mx(s):
-            t, n = divmod(s, HN)
-            codes, scales = Q.pop(s)
-            if n % 2 == 0:
-                y = xpsum.tile([P, 2, OC], F32, name="y", tag="xy")
-                Y[s // 2] = y
-            y = Y[s // 2]
-            for g in range(2):
-                a = n * 2 + g
-                nc.tensor.matmul_mx(
-                    out=y[:, n % 2, :],
-                    lhsT=codes[:, g * P : (g + 1) * P].bitcast(FP8X4),
-                    lhsT_scale=scales[:, g * P : (g + 1) * P],
-                    rhs=wcodes[:, a * OC : (a + 1) * OC].bitcast(FP8X4),
-                    rhs_scale=wscales[:, a * OC : (a + 1) * OC],
-                    start=(g == 0),
-                    stop=(g == 1),
-                )
+        def mx(q):
+            codes, scales = Q.pop(q)
+            y = ypsum.tile([P, 2, OC], F32, name="y")
+            Y[q] = y
+            for i in range(2):
+                for g in range(2):
+                    a = (q % 2) * 4 + i * 2 + g
+                    c0 = (i * 2 + g) * P
+                    nc.tensor.matmul_mx(
+                        out=y[:, i, :],
+                        lhsT=codes[:, c0 : c0 + P].bitcast(FP8X4),
+                        lhsT_scale=scales[:, c0 : c0 + P],
+                        rhs=wcodes[:, a * OC : (a + 1) * OC].bitcast(FP8X4),
+                        rhs_scale=wscales[:, a * OC : (a + 1) * OC],
+                        start=(g == 0),
+                        stop=(g == 1),
+                    )
 
         def weigh(s):
             t, n = divmod(s, HN)
@@ -249,8 +201,8 @@ def tile_tensormoe_pb_t_kernel(tc, h_pre, W_mo, weights_n, leak_n, out):
             if n % 2 == 1:
                 Y.pop(s // 2)
 
-        def sum_over_experts(src, tagname):
-            m = mpsum.tile([P, 512], F32, name=tagname, tag="xy")
+        def sum_over_experts(src, name):
+            m = mpsum.tile([P, 512], F32, name=name, tag="m")
             for hf in range(2):
                 for n in range(HN):
                     nc.tensor.matmul(
@@ -298,39 +250,63 @@ def tile_tensormoe_pb_t_kernel(tc, h_pre, W_mo, weights_n, leak_n, out):
             rt = work.tile([P, OC], F32, name="rt")
             nc.scalar.activation(out=rt[:], in_=MB[t][:, 0:256], func=ACT.Abs_reciprocal_sqrt, scale=0.25)
             TT[t] = rt
+            dt = work.tile([P, OC], F32, name="dt")
+            nc.scalar.activation(out=dt[:], in_=MB[t][:, 0:256], func=ACT.Relu, scale=-0.25e16, bias=one[:])
+            DT[t] = dt
 
         def e_rback(t):
             back(MB[t], TT.pop(t))
+            dt = DT.pop(t)
+            for hf in range(2):
+                nc.tensor.matmul(
+                    out=MB[t][:, 0:1], lhsT=dt[:, hf * P : (hf + 1) * P], rhs=one[:], start=(hf == 0), stop=(hf == 1)
+                )
 
-        def e_u(t, n):
-            if t not in U:
-                u = work.tile([P, HN, OC], F32, name="u", bufs=10)
-                U[t] = u
-                UC[t] = 0
-            nc.vector.scalar_tensor_tensor(
-                out=U[t][:, n, :], in0=MB[t][:, 256:512], scalar=1.0e8, in1=C[t][:, n, :], op0=ALU.min, op1=ALU.mult,
-                accum_out=su[:, t, n : n + 1],
-            )
-            UC[t] += 1
-            if UC[t] == HN:
-                MB.pop(t)
-                C.pop(t)
+        def e_lack(t):
+            nc.scalar.activation(out=sq[:, t, 3:4], in_=MB[t][:, 0:1], func=ACT.Copy, scale=-4.0)
 
-        def e_usq(t, n):
+        def e_u(t):
+            u = work.tile([P, HN - 1, OC], F32, name="u", bufs=10)
+            U[t] = u
+            for n in range(HN - 1):
+                nc.vector.scalar_tensor_tensor(
+                    out=u[:, n, :], in0=MB[t][:, 256:512], scalar=1.0e8, in1=C[t][:, n, :], op0=ALU.min, op1=ALU.mult,
+                    accum_out=su[:, t, n : n + 1],
+                )
+            MB.pop(t)
+            C.pop(t)
+
+        def e_usq(s):
+            t, n = divmod(s, HN)
+            if n == HN - 1:
+                return
             junk = work.tile([P, OC], F32, name="junk")
             nc.scalar.activation(out=junk[:], in_=U[t][:, n, :], func=ACT.Square, accum_out=sq[:, t, n : n + 1])
 
         def fin(gi, step):
-            t0, size = GROUPS[gi]
-            ts = slice(t0, t0 + size)
+            ts = slice(gi * GROUP, (gi + 1) * GROUP)
 
             def small(name):
-                return work.tile([P, size, HN], F32, name=name)
+                return work.tile([P, GROUP, HN], F32, name=name)
 
+            if step == -2:
+                rs = work.tile([P, GROUP], F32, name="rs")
+                nc.vector.tensor_reduce(out=rs[:], in_=su[:, ts, 0:3], axis=AX.X, op=ALU.add)
+                rq = work.tile([P, GROUP], F32, name="rq")
+                nc.vector.tensor_reduce(out=rq[:], in_=sq[:, ts, 0:3], axis=AX.X, op=ALU.add)
+                FIN[gi] = {"rs": rs, "rq": rq}
+                return
+            if step == -1:
+                f = FIN[gi]
+                nc.vector.tensor_scalar_mul(out=su[:, ts, 3], in0=f["rs"][:], scalar1=-1.0)
+                nc.vector.scalar_tensor_tensor(
+                    out=sq[:, ts, 3], in0=sq[:, ts, 3], scalar=4.0 * OC, in1=f["rq"][:], op0=ALU.add, op1=ALU.subtract
+                )
+                return
             if step == 0:
                 mu = small("mu")
                 nc.vector.tensor_scalar_mul(out=mu[:], in0=su[:, ts, :], scalar1=1.0 / OC)
-                FIN[gi] = {"mu": mu}
+                FIN[gi]["mu"] = mu
             f = FIN[gi]
             if step == 1:
                 m2 = small("m2")
@@ -356,100 +332,99 @@ def tile_tensormoe_pb_t_kernel(tc, h_pre, W_mo, weights_n, leak_n, out):
                     out=am[:], in0=f["mu"][:], scalar=-1.0, in1=f["a4"][:], op0=ALU.mult, op1=ALU.mult
                 )
                 f["am"] = am
-                dl = work.tile([P, size, 3], F32, name="dl")
+                dl = work.tile([P, GROUP, 3], F32, name="dl")
                 nc.vector.tensor_tensor(
-                    out=dl[:], in0=f["a4"][:, :, 0:3], in1=f["a4"][:, :, 3:4].to_broadcast([P, size, 3]), op=ALU.subtract
+                    out=dl[:], in0=f["a4"][:, :, 0:3], in1=f["a4"][:, :, 3:4].to_broadcast([P, GROUP, 3]), op=ALU.subtract
                 )
                 f["dl"] = dl
             if step == 6:
-                nk = work.tile([P, size], F32, name="nk")
+                nk = work.tile([P, GROUP], F32, name="nk")
                 nc.vector.tensor_reduce(out=nk[:], in_=f["am"][:], axis=AX.X, op=ALU.add)
                 f["nk"] = nk
-                ob = work.tile([P, size, OC], F32, name="ob")
+                ob = work.tile([P, GROUP, OC], F32, name="ob")
                 f["ob"] = ob
 
         def fin_first(gi, k):
             f = FIN[gi]
             f0 = work.tile([P, OC], F32, name="f0")
-            if GROUPS[gi][1] < GROUP:
-                nc.vector.tensor_scalar(
-                    out=f0[:], in0=U[GROUPS[gi][0] + k][:, 0, :], scalar1=f["dl"][:, k, 0:1], scalar2=f["nk"][:, k : k + 1],
-                    op0=ALU.mult, op1=ALU.add,
-                )
-            else:
-                nc.scalar.activation(
-                    out=f0[:], in_=U[GROUPS[gi][0] + k][:, 0, :], func=ACT.Identity,
-                    scale=f["dl"][:, k, 0:1], bias=f["nk"][:, k : k + 1],
-                )
+            nc.vector.tensor_scalar(
+                out=f0[:], in0=U[gi * GROUP + k][:, 0, :], scalar1=f["dl"][:, k, 0:1], scalar2=f["nk"][:, k : k + 1],
+                op0=ALU.mult, op1=ALU.add,
+            )
             f[("f0", k)] = f0
 
-        def fin_rest(gi, k):
+        def fin_second(gi, k):
             f = FIN[gi]
-            u = U.pop(GROUPS[gi][0] + k)
             f1 = work.tile([P, OC], F32, name="f1")
             nc.vector.scalar_tensor_tensor(
-                out=f1[:], in0=u[:, 1, :], scalar=f["dl"][:, k, 1:2], in1=f[("f0", k)][:], op0=ALU.mult, op1=ALU.add
+                out=f1[:], in0=U[gi * GROUP + k][:, 1, :], scalar=f["dl"][:, k, 1:2], in1=f[("f0", k)][:],
+                op0=ALU.mult, op1=ALU.add,
             )
+            f[("f1", k)] = f1
+
+        def fin_third(gi, k):
+            f = FIN[gi]
             nc.vector.scalar_tensor_tensor(
-                out=f["ob"][:, k, :], in0=u[:, 2, :], scalar=f["dl"][:, k, 2:3], in1=f1[:], op0=ALU.mult, op1=ALU.add
+                out=f["ob"][:, k, :], in0=U.pop(gi * GROUP + k)[:, 2, :], scalar=f["dl"][:, k, 2:3], in1=f[("f1", k)][:],
+                op0=ALU.mult, op1=ALU.add,
             )
 
         def fin_store(gi):
             f = FIN.pop(gi)
-            t0, size = GROUPS[gi]
-            nc.sync.dma_start(out=out_view[:, t0 : t0 + size, :], in_=f["ob"][:])
+            nc.sync.dma_start(out=out_view[:, gi * GROUP : (gi + 1) * GROUP, :], in_=f["ob"][:])
 
-        bank_stage = {
-            "flip": flip, "T": transposes, "L": leak_times, "max": take_max, "quant": quantise, "mx": mx, "weigh": weigh,
-        }
-        tile_stage = {
-            "sum": e_sum, "nm": e_nm, "nmb": e_nmback, "ce0": e_centre, "sq0": e_square, "qs": e_q, "r": e_r, "rb": e_rback,
-        }
-
-        events = {}
-
-        def at(step, rank, sub, fn, args):
-            if step not in events:
-                events[step] = []
-            events[step].append((rank, sub, len(events[step]), fn, args))
-
-        def advance(s):
-            return min(ADV_MAX, max(0, (s - ADV_FROM) // ADV_EVERY))
-
-        for rank, (name, lag) in enumerate(ORDER):
-            if name in bank_stage:
-                for s in range(NS):
-                    adv = advance(s) if name in ADVANCED else 0
-                    at(s + lag[s % HN] - adv, rank, s, bank_stage[name], (s,))
-            elif name[0:2] == "wr":
-                at(lag, rank, 0, w_regroup, (int(name[2]),))
-            elif name[0:2] == "wq":
-                at(lag, rank, 0, w_quantise, (int(name[2]),))
-            elif name in tile_stage:
-                for t in range(NT):
-                    at(HN * t + lag, rank, t, tile_stage[name], (t,))
-            elif name[0:3] == "usq":
-                n = int(name[3])
-                for t in range(NT):
-                    at(HN * t + (lag if t < TAIL_FROM else (USQ_T0, USQ_T1, USQ_T2, USQ_T3)[n]), rank, t, e_usq, (t, n))
-            else:
-                for t in range(NT):
-                    at(HN * t + lag, rank, t, e_u, (t, int(name[1])))
-        flip_lag = [lag for name, lag in ORDER if name == "flip"][0]
-        for t in range(AHEAD, NT):
-            at(HN * t + flip_lag[0] - advance(HN * t) - HN * AHEAD, -1, t, load, (t, 1))
-        after = len(ORDER)
-        for gi in range(len(GROUPS)):
-            t0, size = GROUPS[gi]
-            base = HN * (t0 + size - GROUP) + FIN_BASE
-            if t0 >= TAIL_FROM:
-                base = HN * (t0 + size - 1) + (FIN_T0, FIN_T1, FIN_T2)[gi - len(GROUPS) + 3]
-            for step in range(7):
-                at(base + step, after, gi, fin, (gi, step))
-            for k in range(size):
-                at(base + 7 + k, after + 1, gi, fin_first, (gi, k))
-                at(base + 8 + k, after + 2, gi, fin_rest, (gi, k))
-            at(base + 9 + size, after + 3, gi, fin_store, (gi,))
-        for step in sorted(events):
-            for rank, sub, k, fn, args in sorted(events[step], key=lambda ev: ev[0:3]):
-                fn(*args)
+        BANK, TILE, PAIR = 0, 1, 2
+        stages = [
+            (e_usq, 21, BANK),
+            (e_lack, 20, TILE),
+            (e_u, 20, TILE),
+            (e_rback, 19, TILE),
+            (e_r, 18, TILE),
+            (e_q, 17, TILE),
+            (e_square, 16, TILE),
+            (e_centre, 15, TILE),
+            (e_nmback, 14, TILE),
+            (e_nm, 13, TILE),
+            (e_sum, 12, TILE),
+            (weigh, 8, BANK),
+            (mx, 7, PAIR),
+            (quantise, 6, PAIR),
+            (rectify_psum, 4, BANK),
+            (leave, 3, BANK),
+            (transposes, 2, BANK),
+            (flip, 0, BANK),
+        ]
+        FIN_LAG = 26
+        last = HN * (NT - 1) + FIN_LAG + 9 + GROUP
+        for k in range(last + 1):
+            for gi in range(NT // GROUP):
+                d = k - (HN * (gi * GROUP + GROUP - 1) + FIN_LAG)
+                if d == 9 + GROUP:
+                    fin_store(gi)
+                if 9 <= d < 9 + GROUP:
+                    fin_third(gi, d - 9)
+                if 8 <= d < 8 + GROUP:
+                    fin_second(gi, d - 8)
+                if 7 <= d < 7 + GROUP:
+                    fin_first(gi, d - 7)
+                if -2 <= d < 7:
+                    fin(gi, d)
+            for fn, lag, kind in stages:
+                if kind == BANK:
+                    for n in range(HN):
+                        d = k - (lag if isinstance(lag, int) else lag[n])
+                        if d % HN == n and 0 <= d < NS:
+                            fn(d)
+                    continue
+                d = k - lag
+                if kind == TILE and d % HN == 0 and 0 <= d // HN < NT:
+                    fn(d // HN)
+                if kind == PAIR and d % 2 == 0 and 0 <= d // 2 < NS // 2:
+                    fn(d // 2)
+            if k < HN:
+                w_regroup(2 * k)
+                w_regroup(2 * k + 1)
+            if 2 <= k < 2 + HN:
+                w_quantise(k - 2)
+            if k % HN == 0 and k // HN + AHEAD < NT:
+                load(k // HN + AHEAD, 1)

@@ -21,11 +21,11 @@ FLOPS = 2 * B * HN * HM * OC
 
 AT_PSUM = (0, 1, 2, 3)
 NZ = HN - len(AT_PSUM)
-AHEAD = 3
+AHEAD = 4
 
 
 def l_on_vector(t, n):
-    return n == 3 and t % 3 != 0
+    return n == 3 and t % 4 == 0
 
 
 def tile_tensormoe_pb_t_kernel(tc, h_pre, W_mo, weights_n, leak_n, out):
@@ -240,7 +240,7 @@ def tile_tensormoe_pb_t_kernel(tc, h_pre, W_mo, weights_n, leak_n, out):
 
         def e_square(t):
             c2 = work.tile([P, HN, OC], F32, name="c2")
-            nc.scalar.activation(out=c2[:], in_=C[t][:], func=ACT.Square)
+            nc.gpsimd.tensor_tensor(out=c2[:], in0=C[t][:], in1=C[t][:], op=ALU.mult)
             C2[t] = c2
 
         def e_q(t):
@@ -347,7 +347,7 @@ def tile_tensormoe_pb_t_kernel(tc, h_pre, W_mo, weights_n, leak_n, out):
         def fin_first(gi, k):
             f = FIN[gi]
             f0 = work.tile([P, OC], F32, name="f0")
-            nc.vector.tensor_scalar(
+            nc.gpsimd.tensor_scalar(
                 out=f0[:], in0=U[gi * GROUP + k][:, 0, :], scalar1=f["dl"][:, k, 0:1], scalar2=f["nk"][:, k : k + 1],
                 op0=ALU.mult, op1=ALU.add,
             )
@@ -373,58 +373,90 @@ def tile_tensormoe_pb_t_kernel(tc, h_pre, W_mo, weights_n, leak_n, out):
             f = FIN.pop(gi)
             nc.sync.dma_start(out=out_view[:, gi * GROUP : (gi + 1) * GROUP, :], in_=f["ob"][:])
 
-        BANK, TILE, PAIR = 0, 1, 2
-        stages = [
-            (e_usq, 21, BANK),
-            (e_lack, 20, TILE),
-            (e_u, 20, TILE),
-            (e_rback, 19, TILE),
-            (e_r, 18, TILE),
-            (e_q, 17, TILE),
-            (e_square, 16, TILE),
-            (e_centre, 15, TILE),
-            (e_nmback, 14, TILE),
-            (e_nm, 13, TILE),
-            (e_sum, 12, TILE),
-            (weigh, 8, BANK),
-            (mx, 7, PAIR),
-            (quantise, 6, PAIR),
-            (rectify_psum, 4, BANK),
-            (leave, 3, BANK),
-            (transposes, 2, BANK),
-            (flip, 0, BANK),
-        ]
-        FIN_LAG = 26
-        last = HN * (NT - 1) + FIN_LAG + 9 + GROUP
-        for k in range(last + 1):
+        def ok(t):
+            return 0 <= t < NT
+
+        def usq_tile(t):
+            for n in range(HN - 1):
+                e_usq(HN * t + n)
+
+        for j in range(-2, NT + 9):
+            if ok(j + AHEAD) and j + AHEAD >= AHEAD:
+                load(j + AHEAD, 1)
             for gi in range(NT // GROUP):
-                d = k - (HN * (gi * GROUP + GROUP - 1) + FIN_LAG)
-                if d == 9 + GROUP:
+                d = j - (gi * GROUP + GROUP - 1 + 4)
+                if d == 1:
+                    fin(gi, 3)
+            for n in range(HN):
+                if ok(j) and l_on_vector(j, n):
+                    leave(HN * j + n)
+            if ok(j - 2):
+                e_centre(j - 2)
+                e_square(j - 2)
+            for gi in range(NT // GROUP):
+                d = j - (gi * GROUP + GROUP - 1 + 4)
+                if 2 <= d < 2 + GROUP:
+                    fin_first(gi, d - 2)
+            if ok(j - 3):
+                e_lack(j - 3)
+            if ok(j - 4):
+                usq_tile(j - 4)
+            if ok(j - 1):
+                for n in range(HN):
+                    weigh(HN * (j - 1) + n)
+            for n in range(HN):
+                if n == 2 and ok(j - 3):
+                    e_u(j - 3)
+                if ok(j):
+                    rectify_psum(HN * j + n)
+                if ok(j + 1):
+                    transposes(HN * (j + 1) + n)
+                    if not l_on_vector(j + 1, n):
+                        leave(HN * (j + 1) + n)
+                if n == 1 and ok(j - 1):
+                    e_sum(j - 1)
+                    e_nm(j - 1)
+                if n == 1 and ok(j - 2):
+                    e_q(j - 2)
+                    e_r(j - 2)
+            small = []
+            for gi in range(NT // GROUP):
+                d = j - (gi * GROUP + GROUP - 1 + 4)
+                if 2 <= d < 2 + GROUP:
+                    small.append((fin_second, gi, d - 2))
+                if d == 0:
+                    small.extend([(fin, gi, step) for step in range(-2, 3)])
+                if d == 1:
+                    small.extend([(fin, gi, step) for step in range(4, 7)])
+            for gi in range(NT // GROUP):
+                d = j - (gi * GROUP + GROUP - 1 + 4)
+                if 2 <= d < 2 + GROUP:
+                    small.append((fin_third, gi, d - 2))
+            for i in range(2):
+                if ok(j):
+                    quantise(2 * j + i)
+                    mx(2 * j + i)
+                if i == 0 and ok(j - 1):
+                    e_nmback(j - 1)
+                if i == 0 and ok(j - 2):
+                    e_rback(j - 2)
+                if small:
+                    fn, gi, arg = small.pop(0)
+                    fn(gi, arg)
+                for n in (2 * i, 2 * i + 1):
+                    if ok(j + 2):
+                        flip(HN * (j + 2) + n)
+                    if small:
+                        fn, gi, arg = small.pop(0)
+                        fn(gi, arg)
+            for fn, gi, arg in small:
+                fn(gi, arg)
+            if j == -2:
+                for a in range(8):
+                    w_regroup(a)
+            if j == -1:
+                for n in range(HN):
+                    w_quantise(n)
+            for gi in range(NT // GROUP):
+                if j - (gi * GROUP + GROUP - 1 + 4) == 1 + GROUP:
                     fin_store(gi)
-                if 9 <= d < 9 + GROUP:
-                    fin_third(gi, d - 9)
-                if 8 <= d < 8 + GROUP:
-                    fin_second(gi, d - 8)
-                if 7 <= d < 7 + GROUP:
-                    fin_first(gi, d - 7)
-                if -2 <= d < 7:
-                    fin(gi, d)
-            for fn, lag, kind in stages:
-                if kind == BANK:
-                    for n in range(HN):
-                        d = k - (lag if isinstance(lag, int) else lag[n])
-                        if d % HN == n and 0 <= d < NS:
-                            fn(d)
-                    continue
-                d = k - lag
-                if kind == TILE and d % HN == 0 and 0 <= d // HN < NT:
-                    fn(d // HN)
-                if kind == PAIR and d % 2 == 0 and 0 <= d // 2 < NS // 2:
-                    fn(d // 2)
-            if k < HN:
-                w_regroup(2 * k)
-                w_regroup(2 * k + 1)
-            if 2 <= k < 2 + HN:
-                w_quantise(k - 2)
-            if k % HN == 0 and k // HN + AHEAD < NT:
-                load(k // HN + AHEAD, 1)

@@ -15,17 +15,18 @@ AX = mybir.AxisListType
 P = 128
 B, HN, HM, OC = 4096, 4, 1024, 256
 NT = B // P
-NS = NT * HN
+PASSES = HM // (4 * P)
+WORDS = HM // 2
 GROUP = 4
+NG = NT // GROUP
 FLOPS = 2 * B * HN * HM * OC
 
-AT_PSUM = (0, 1, 2, 3)
-NZ = HN - len(AT_PSUM)
 AHEAD = 4
+STATS = 4
 
 
-def l_on_vector(t, n):
-    return n == 3 and t % 4 == 0
+def slope_on_vector(t, n):
+    return n == HN - 1 and t % 4 == 0
 
 
 def tile_tensormoe_pb_t_kernel(tc, h_pre, W_mo, weights_n, leak_n, out):
@@ -34,429 +35,413 @@ def tile_tensormoe_pb_t_kernel(tc, h_pre, W_mo, weights_n, leak_n, out):
         ctx.enter_context(tc.manual_schedule())
         const = ctx.enter_context(tc.tile_pool(name="const", bufs=1))
         work = ctx.enter_context(tc.tile_pool(name="work", bufs=2))
-        xpsum = ctx.enter_context(tc.psum_pool(name="xpsum", bufs=4))
-        ypsum = ctx.enter_context(tc.psum_pool(name="ypsum", bufs=2))
-        mpsum = ctx.enter_context(tc.psum_pool(name="mpsum", bufs=2))
+        bank_pool = ctx.enter_context(tc.psum_pool(name="bank_pool", bufs=HN))
+        prod_pool = ctx.enter_context(tc.psum_pool(name="prod_pool", bufs=2))
+        sum_pool = ctx.enter_context(tc.psum_pool(name="sum_pool", bufs=2))
 
         h_view = h_pre.rearrange("(p t) n m -> p t (n m)", t=NT)
         out_view = out.rearrange("(p t) o -> p t o", t=NT)
+        w_view = W_mo.rearrange("n (g p j) o -> p (n g) (j o)", g=PASSES, p=P, j=4)
 
-        lkb = const.tile([P, HN], BF16)
-        nc.sync.dma_start(out=lkb[:], in_=leak_n.partition_broadcast(P))
-        wtb = const.tile([P, NT * HN], BF16)
-        nc.sync.dma_start(out=wtb[:], in_=weights_n.rearrange("(p t) n -> p (t n)", t=NT))
+        leak_bf = const.tile([P, HN], BF16)
+        nc.sync.dma_start(out=leak_bf[:], in_=leak_n.partition_broadcast(P))
+        weights_bf = const.tile([P, NT * HN], BF16)
+        nc.sync.dma_start(out=weights_bf[:], in_=weights_n.rearrange("(p t) n -> p (t n)", t=NT))
 
-        DT, NEG, H, X, LT, G, Q, Y, Z, C, C2, MA, MB, TT, U, FIN = {}, {}, {}, {}, {}, {}, {}, {}, {}, {}, {}, {}, {}, {}, {}, {}
+        rows, bank, sloped, rect, quantised, prod, weighted, centred, squares = {}, {}, {}, {}, {}, {}, {}, {}, {}
+        mean_sum, square_sum, turned, lacking, normed, stats = {}, {}, {}, {}, {}, {}
 
-        def load(t, pieces):
-            hsb = work.tile([P, HN * HM], BF16, name="hsb", bufs=AHEAD + 3)
-            w = HN * HM // pieces
-            for i in range(pieces):
-                nc.sync.dma_start(out=hsb[:, i * w : (i + 1) * w], in_=h_view[:, t, i * w : (i + 1) * w])
-            H[t] = hsb
+        def new_rows(t):
+            rows[t] = work.tile([P, HN * HM], BF16, name="rows", bufs=AHEAD + 3)
 
-        wraw = const.tile([P, 8 * 1024], BF16)
-        w_view = W_mo.rearrange("n (g p j) o -> p (n g) (j o)", g=2, p=P, j=4)
+        def load(t):
+            new_rows(t)
+            nc.sync.dma_start(out=rows[t][:], in_=h_view[:, t, :])
 
-        def load_w(n):
-            for g in range(2):
-                a = 2 * n + g
-                nc.sync.dma_start(
-                    out=wraw[:, a * 1024 : (a + 1) * 1024],
-                    in_=w_view[:, a, :],
-                )
-
-        hsb0 = work.tile([P, HN * HM], BF16, name="hsb", bufs=AHEAD + 3)
-        H[0] = hsb0
+        w_raw = const.tile([P, HN * PASSES * 4 * OC], BF16)
+        new_rows(0)
         for n in range(HN):
-            nc.sync.dma_start(out=hsb0[:, n * HM : (n + 1) * HM], in_=h_view[:, 0, n * HM : (n + 1) * HM])
-            load_w(n)
+            nc.sync.dma_start(out=rows[0][:, n * HM : (n + 1) * HM], in_=h_view[:, 0, n * HM : (n + 1) * HM])
+            for a in range(n * PASSES, (n + 1) * PASSES):
+                nc.sync.dma_start(out=w_raw[:, a * 4 * OC : (a + 1) * 4 * OC], in_=w_view[:, a, :])
         for t in range(1, AHEAD):
-            load(t, 1)
+            load(t)
 
         ident = const.tile([P, P], F32)
         make_identity(nc, ident[:])
-
         one = const.tile([P, 1], F32)
         nc.vector.memset(one[:], 1.0)
         warm = const.tile([P, 1], F32)
         nc.scalar.activation(out=warm[:], in_=one[:], func=ACT.Abs_reciprocal_sqrt)
 
-        lk = const.tile([P, HN], F32)
-        nc.vector.tensor_copy(out=lk[:], in_=lkb[:])
-        sg = const.tile([P, HN], F32)
-        nc.vector.tensor_scalar(out=sg[:], in0=lk[:], scalar1=1.0, scalar2=-2.0, op0=ALU.is_gt, op1=ALU.mult)
-        nc.vector.tensor_scalar_add(out=sg[:], in0=sg[:], scalar1=1.0)
-        sl = const.tile([P, HN], F32)
-        nc.vector.tensor_tensor(out=sl[:], in0=sg[:], in1=lk[:], op=ALU.mult)
-        wp = const.tile([P, NT, HN], F32)
+        leak = const.tile([P, HN], F32)
+        nc.vector.tensor_copy(out=leak[:], in_=leak_bf[:])
+        sign = const.tile([P, HN], F32)
+        nc.vector.tensor_scalar(out=sign[:], in0=leak[:], scalar1=1.0, scalar2=-2.0, op0=ALU.is_gt, op1=ALU.mult)
+        nc.vector.tensor_scalar_add(out=sign[:], in0=sign[:], scalar1=1.0)
+        signed_weights = const.tile([P, NT, HN], F32)
         nc.vector.tensor_tensor(
-            out=wp[:],
-            in0=wtb[:].rearrange("p (t n) -> p t n", n=HN),
-            in1=sg[:].unsqueeze(1).to_broadcast([P, NT, HN]),
+            out=signed_weights[:],
+            in0=weights_bf[:].rearrange("p (t n) -> p t n", n=HN),
+            in1=sign[:].unsqueeze(1).to_broadcast([P, NT, HN]),
             op=ALU.mult,
         )
-        wgrp = const.tile([P, 8192], BF16, align_bytes=64)
-        wcodes = const.tile([P, 2048], U32, align_bytes=64)
-        wscales = const.tile([P, 2048], U8, align_bytes=64)
-        su = const.tile([P, NT, HN], F32)
-        sq = const.tile([P, NT, HN], F32)
 
-        wsrc = wraw[:].rearrange("p (a j o) -> p a o j", a=8, j=4, o=OC)
-        wdst = wgrp[:].rearrange("p (a o j) -> p a o j", a=8, j=4, o=OC)
+        w_grouped = const.tile([P, HN * PASSES * OC * 4], BF16, align_bytes=64)
+        w_codes = const.tile([P, HN * PASSES * OC], U32, align_bytes=64)
+        w_scales = const.tile([P, HN * PASSES * OC], U8, align_bytes=64)
+        w_from = w_raw[:].rearrange("p (a j o) -> p a o j", a=HN * PASSES, j=4, o=OC)
+        w_to = w_grouped[:].rearrange("p (a o j) -> p a o j", a=HN * PASSES, j=4, o=OC)
 
-        def w_regroup(a):
+        def regroup_w(a):
             if a % 2 == 1:
-                nc.scalar.copy(out=wdst[:, a], in_=wsrc[:, a])
+                nc.scalar.copy(out=w_to[:, a], in_=w_from[:, a])
             else:
-                nc.vector.tensor_copy(out=wdst[:, a], in_=wsrc[:, a])
+                nc.vector.tensor_copy(out=w_to[:, a], in_=w_from[:, a])
 
-        def w_quantise(n):
+        def quantise_w(n):
+            cols = slice(n * PASSES * OC, (n + 1) * PASSES * OC)
             nc.vector.quantize_mx(
-                out=wcodes[:, n * 512 : (n + 1) * 512].bitcast(FP8X4),
-                scales=wscales[:, n * 512 : (n + 1) * 512],
-                in_=wgrp[:, n * 2048 : (n + 1) * 2048],
+                out=w_codes[:, cols].bitcast(FP8X4),
+                scales=w_scales[:, cols],
+                in_=w_grouped[:, n * PASSES * OC * 4 : (n + 1) * PASSES * OC * 4],
             )
+
+        row_sum = const.tile([P, NT, HN], F32)
+        row_squares = const.tile([P, NT, HN], F32)
 
         def flip(s):
             t, n = divmod(s, HN)
-            x = H[t][:, n * HM : (n + 1) * HM]
-            nc.vector.tensor_scalar(out=x, in0=x, scalar1=sg[:, n : n + 1], scalar2=None, op0=ALU.mult)
+            x = rows[t][:, n * HM : (n + 1) * HM]
+            nc.vector.tensor_scalar(out=x, in0=x, scalar1=sign[:, n : n + 1], scalar2=None, op0=ALU.mult)
 
         def transposes(s):
             t, n = divmod(s, HN)
-            hw = H[t][:].bitcast(F32)
-            xt = xpsum.tile([P, 512], F32, name="xt")
+            words = rows[t][:].bitcast(F32)
+            bank[s] = bank_pool.tile([P, WORDS], F32, name="bank")
             for u in range(2):
-                for g in range(2):
-                    j = u * 2 + g
-                    c0 = n * 512 + g * 256
-                    nc.tensor.transpose(xt[:, j * P : (j + 1) * P], hw[:, c0 + u : c0 + 256 : 2], ident[:])
-            X[s] = xt
+                for g in range(PASSES):
+                    first = n * WORDS + g * 2 * P
+                    at = (u * PASSES + g) * P
+                    nc.tensor.transpose(bank[s][:, at : at + P], words[:, first + u : first + 2 * P : 2], ident[:])
 
-        def pair_half(s):
-            if s // 2 not in G:
-                grp = work.tile([P, 2 * HM], BF16, name="grp", bufs=3, align_bytes=64)
-                G[s // 2] = grp
-            return G[s // 2][:, (s % 2) * HM : (s % 2 + 1) * HM]
-
-        def leave(s):
+        def slope(s):
             t, n = divmod(s, HN)
-            if n in AT_PSUM:
-                lt = work.tile([P, HM], BF16, name="lt", bufs=4)
-                if l_on_vector(t, n):
-                    nc.vector.tensor_scalar(out=lt[:], in0=X[s][:].bitcast(BF16), scalar1=lk[:, n : n + 1], scalar2=None, op0=ALU.mult)
-                else:
-                    nc.scalar.activation(out=lt[:], in_=X[s][:].bitcast(BF16), func=ACT.Copy, scale=lk[:, n : n + 1])
-                LT[s] = lt
+            sloped[s] = work.tile([P, HM], BF16, name="sloped", bufs=HN)
+            x = bank[s][:].bitcast(BF16)
+            if slope_on_vector(t, n):
+                nc.vector.tensor_scalar(out=sloped[s][:], in0=x, scalar1=leak[:, n : n + 1], scalar2=None, op0=ALU.mult)
             else:
-                nc.scalar.copy(
-                    out=pair_half(s).bitcast(F32).rearrange("p (w u) -> p w u", u=2),
-                    in_=X.pop(s)[:].rearrange("p (u w) -> p w u", u=2),
-                )
+                nc.scalar.activation(out=sloped[s][:], in_=x, func=ACT.Copy, scale=leak[:, n : n + 1])
 
-        def rectify_psum(s):
-            t, n = divmod(s, HN)
-            if n not in AT_PSUM:
-                return
+        def rectify(s):
+            q = s // 2
+            if s % 2 == 0:
+                rect[q] = work.tile([P, 2 * HM], BF16, name="rect", bufs=3, align_bytes=64)
             nc.vector.tensor_tensor(
-                out=pair_half(s).rearrange("p (w u e) -> p w u e", u=2, e=2),
-                in0=LT.pop(s)[:].rearrange("p (u w e) -> p w u e", u=2, e=2),
-                in1=X.pop(s)[:].bitcast(BF16).rearrange("p (u w e) -> p w u e", u=2, e=2),
+                out=rect[q][:, (s % 2) * HM : (s % 2 + 1) * HM].rearrange("p (w u e) -> p w u e", u=2, e=2),
+                in0=sloped.pop(s)[:].rearrange("p (u w e) -> p w u e", u=2, e=2),
+                in1=bank.pop(s)[:].bitcast(BF16).rearrange("p (u w e) -> p w u e", u=2, e=2),
                 op=ALU.max,
             )
 
         def quantise(q):
-            grp = G.pop(q)
-            codes = work.tile([P, 512], U32, name="codes", bufs=4, align_bytes=64)
-            scales = work.tile([P, 512], U8, name="scales", bufs=4, align_bytes=64)
-            nc.vector.quantize_mx(out=codes[:].bitcast(FP8X4), scales=scales[:], in_=grp[:])
-            Q[q] = (codes, scales)
+            codes = work.tile([P, HM // 2], U32, name="codes", bufs=4, align_bytes=64)
+            scales = work.tile([P, HM // 2], U8, name="scales", bufs=4, align_bytes=64)
+            nc.vector.quantize_mx(out=codes[:].bitcast(FP8X4), scales=scales[:], in_=rect.pop(q)[:])
+            quantised[q] = (codes, scales)
 
-        def mx(q):
-            codes, scales = Q.pop(q)
-            y = ypsum.tile([P, 2, OC], F32, name="y")
-            Y[q] = y
+        def multiply(q):
+            codes, scales = quantised.pop(q)
+            prod[q] = prod_pool.tile([P, 2, OC], F32, name="prod")
             for i in range(2):
-                for g in range(2):
-                    a = (q % 2) * 4 + i * 2 + g
-                    c0 = (i * 2 + g) * P
+                for g in range(PASSES):
+                    h_cols = slice((i * PASSES + g) * P, (i * PASSES + g + 1) * P)
+                    a = ((q % 2) * 2 + i) * PASSES + g
+                    w_cols = slice(a * OC, (a + 1) * OC)
                     nc.tensor.matmul_mx(
-                        out=y[:, i, :],
-                        lhsT=codes[:, c0 : c0 + P].bitcast(FP8X4),
-                        lhsT_scale=scales[:, c0 : c0 + P],
-                        rhs=wcodes[:, a * OC : (a + 1) * OC].bitcast(FP8X4),
-                        rhs_scale=wscales[:, a * OC : (a + 1) * OC],
+                        out=prod[q][:, i, :],
+                        lhsT=codes[:, h_cols].bitcast(FP8X4),
+                        lhsT_scale=scales[:, h_cols],
+                        rhs=w_codes[:, w_cols].bitcast(FP8X4),
+                        rhs_scale=w_scales[:, w_cols],
                         start=(g == 0),
-                        stop=(g == 1),
+                        stop=(g == PASSES - 1),
                     )
 
-        def weigh(s):
-            t, n = divmod(s, HN)
-            if n == 0:
-                z = work.tile([P, HN, OC], F32, name="z", bufs=3)
-                Z[t] = z
-            y = Y[s // 2]
-            nc.scalar.activation(out=Z[t][:, n, :], in_=y[:, n % 2, :], func=ACT.Copy, scale=wp[:, t, n : n + 1])
-            if n % 2 == 1:
-                Y.pop(s // 2)
+        def weigh(t):
+            weighted[t] = work.tile([P, HN, OC], F32, name="weighted", bufs=3)
+            for n in range(HN):
+                nc.scalar.activation(
+                    out=weighted[t][:, n, :], in_=prod[2 * t + n // 2][:, n % 2, :], func=ACT.Copy,
+                    scale=signed_weights[:, t, n : n + 1],
+                )
+            prod.pop(2 * t)
+            prod.pop(2 * t + 1)
 
-        def sum_over_experts(src, name):
-            m = mpsum.tile([P, 512], F32, name=name, tag="m")
-            for hf in range(2):
+        def sum_over_experts(terms):
+            total = sum_pool.tile([P, 2 * OC], F32, name="total")
+            for half in range(OC // P):
                 for n in range(HN):
                     nc.tensor.matmul(
-                        out=m[:, hf * P : (hf + 1) * P],
-                        lhsT=src[:, n, hf * P : (hf + 1) * P],
+                        out=total[:, half * P : (half + 1) * P],
+                        lhsT=terms[:, n, half * P : (half + 1) * P],
                         rhs=ident[:],
                         start=(n == 0),
                         stop=(n == HN - 1),
                         is_transpose=True,
                     )
-            return m
+            return total
 
-        def back(m, src_t):
-            for hf in range(2):
-                nc.tensor.transpose(m[:, 256 + hf * P : 256 + (hf + 1) * P], src_t[:, hf * P : (hf + 1) * P], ident[:])
-
-        def e_sum(t):
-            MA[t] = sum_over_experts(Z[t], "mA")
-
-        def e_nm(t):
-            nmt = work.tile([P, OC], F32, name="nmt")
-            nc.scalar.activation(out=nmt[:], in_=MA[t][:, 0:256], func=ACT.Copy, scale=-0.25)
-            TT[t] = nmt
-
-        def e_nmback(t):
-            back(MA[t], TT.pop(t))
-
-        def e_centre(t):
-            c = work.tile([P, HN, OC], F32, name="c", bufs=3)
-            nm = MA.pop(t)[:, 256:512]
-            nc.vector.tensor_tensor(
-                out=c[:], in0=Z.pop(t)[:], in1=nm.unsqueeze(1).to_broadcast([P, HN, OC]), op=ALU.add
-            )
-            C[t] = c
-
-        def e_square(t):
-            c2 = work.tile([P, HN, OC], F32, name="c2")
-            nc.gpsimd.tensor_tensor(out=c2[:], in0=C[t][:], in1=C[t][:], op=ALU.mult)
-            C2[t] = c2
-
-        def e_q(t):
-            MB[t] = sum_over_experts(C2.pop(t), "mB")
-
-        def e_r(t):
-            rt = work.tile([P, OC], F32, name="rt")
-            nc.scalar.activation(out=rt[:], in_=MB[t][:, 0:256], func=ACT.Abs_reciprocal_sqrt, scale=0.25)
-            TT[t] = rt
-            dt = work.tile([P, OC], F32, name="dt")
-            nc.scalar.activation(out=dt[:], in_=MB[t][:, 0:256], func=ACT.Relu, scale=-0.25e16, bias=one[:])
-            DT[t] = dt
-
-        def e_rback(t):
-            back(MB[t], TT.pop(t))
-            dt = DT.pop(t)
-            for hf in range(2):
-                nc.tensor.matmul(
-                    out=MB[t][:, 0:1], lhsT=dt[:, hf * P : (hf + 1) * P], rhs=one[:], start=(hf == 0), stop=(hf == 1)
+        def turn_back(total, t):
+            made = turned.pop(t)
+            for half in range(OC // P):
+                nc.tensor.transpose(
+                    total[:, OC + half * P : OC + (half + 1) * P], made[:, half * P : (half + 1) * P], ident[:]
                 )
 
-        def e_lack(t):
-            nc.scalar.activation(out=sq[:, t, 3:4], in_=MB[t][:, 0:1], func=ACT.Copy, scale=-4.0)
+        def sum_weighted(t):
+            mean_sum[t] = sum_over_experts(weighted[t])
 
-        def e_u(t):
-            u = work.tile([P, HN - 1, OC], F32, name="u", bufs=10)
-            U[t] = u
+        def negative_mean(t):
+            turned[t] = work.tile([P, OC], F32, name="neg_mean")
+            nc.scalar.activation(out=turned[t][:], in_=mean_sum[t][:, 0:OC], func=ACT.Copy, scale=-1.0 / HN)
+
+        def mean_back(t):
+            turn_back(mean_sum[t], t)
+
+        def centre(t):
+            centred[t] = work.tile([P, HN, OC], F32, name="centred", bufs=3)
+            nc.vector.tensor_tensor(
+                out=centred[t][:],
+                in0=weighted.pop(t)[:],
+                in1=mean_sum.pop(t)[:, OC : 2 * OC].unsqueeze(1).to_broadcast([P, HN, OC]),
+                op=ALU.add,
+            )
+
+        def square(t):
+            squares[t] = work.tile([P, HN, OC], F32, name="squares")
+            nc.gpsimd.tensor_tensor(out=squares[t][:], in0=centred[t][:], in1=centred[t][:], op=ALU.mult)
+
+        def sum_squares(t):
+            square_sum[t] = sum_over_experts(squares.pop(t))
+
+        def rsqrt(t):
+            turned[t] = work.tile([P, OC], F32, name="rsqrt")
+            nc.scalar.activation(
+                out=turned[t][:], in_=square_sum[t][:, 0:OC], func=ACT.Abs_reciprocal_sqrt, scale=1.0 / HN
+            )
+            lacking[t] = work.tile([P, OC], F32, name="lacking")
+            nc.scalar.activation(
+                out=lacking[t][:], in_=square_sum[t][:, 0:OC], func=ACT.Relu, scale=-1.0e16 / HN, bias=one[:]
+            )
+
+        def rsqrt_back(t):
+            turn_back(square_sum[t], t)
+            short = lacking.pop(t)
+            for half in range(OC // P):
+                nc.tensor.matmul(
+                    out=square_sum[t][:, 0:1], lhsT=short[:, half * P : (half + 1) * P], rhs=one[:],
+                    start=(half == 0), stop=(half == OC // P - 1),
+                )
+
+        def fetch_lack(t):
+            nc.scalar.activation(
+                out=row_squares[:, t, HN - 1 : HN], in_=square_sum[t][:, 0:1], func=ACT.Copy, scale=-1.0 * HN
+            )
+
+        def normalise(t):
+            normed[t] = work.tile([P, HN - 1, OC], F32, name="normed", bufs=10)
             for n in range(HN - 1):
                 nc.vector.scalar_tensor_tensor(
-                    out=u[:, n, :], in0=MB[t][:, 256:512], scalar=1.0e8, in1=C[t][:, n, :], op0=ALU.min, op1=ALU.mult,
-                    accum_out=su[:, t, n : n + 1],
+                    out=normed[t][:, n, :], in0=square_sum[t][:, OC : 2 * OC], scalar=1.0e8, in1=centred[t][:, n, :],
+                    op0=ALU.min, op1=ALU.mult, accum_out=row_sum[:, t, n : n + 1],
                 )
-            MB.pop(t)
-            C.pop(t)
+            square_sum.pop(t)
+            centred.pop(t)
 
-        def e_usq(s):
-            t, n = divmod(s, HN)
-            if n == HN - 1:
-                return
-            junk = work.tile([P, OC], F32, name="junk")
-            nc.scalar.activation(out=junk[:], in_=U[t][:, n, :], func=ACT.Square, accum_out=sq[:, t, n : n + 1])
-
-        def fin(gi, step):
-            ts = slice(gi * GROUP, (gi + 1) * GROUP)
-
-            def small(name):
-                return work.tile([P, GROUP, HN], F32, name=name)
-
-            if step == -2:
-                rs = work.tile([P, GROUP], F32, name="rs")
-                nc.vector.tensor_reduce(out=rs[:], in_=su[:, ts, 0:3], axis=AX.X, op=ALU.add)
-                rq = work.tile([P, GROUP], F32, name="rq")
-                nc.vector.tensor_reduce(out=rq[:], in_=sq[:, ts, 0:3], axis=AX.X, op=ALU.add)
-                FIN[gi] = {"rs": rs, "rq": rq}
-                return
-            if step == -1:
-                f = FIN[gi]
-                nc.vector.tensor_scalar_mul(out=su[:, ts, 3], in0=f["rs"][:], scalar1=-1.0)
-                nc.vector.scalar_tensor_tensor(
-                    out=sq[:, ts, 3], in0=sq[:, ts, 3], scalar=4.0 * OC, in1=f["rq"][:], op0=ALU.add, op1=ALU.subtract
+        def sum_normed_squares(t):
+            for n in range(HN - 1):
+                unused = work.tile([P, OC], F32, name="unused")
+                nc.scalar.activation(
+                    out=unused[:], in_=normed[t][:, n, :], func=ACT.Square, accum_out=row_squares[:, t, n : n + 1]
                 )
-                return
-            if step == 0:
-                mu = small("mu")
-                nc.vector.tensor_scalar_mul(out=mu[:], in0=su[:, ts, :], scalar1=1.0 / OC)
-                FIN[gi]["mu"] = mu
-            f = FIN[gi]
-            if step == 1:
-                m2 = small("m2")
-                nc.vector.tensor_tensor(out=m2[:], in0=f["mu"][:], in1=f["mu"][:], op=ALU.mult)
-                f["m2"] = m2
-            if step == 2:
-                var = small("var")
-                nc.vector.scalar_tensor_tensor(
-                    out=var[:], in0=sq[:, ts, :], scalar=1.0 / OC, in1=f["m2"][:], op0=ALU.mult, op1=ALU.subtract
-                )
-                f["var"] = var
-            if step == 3:
-                a = small("a")
-                nc.scalar.activation(out=a[:], in_=f["var"][:], func=ACT.Abs_reciprocal_sqrt)
-                f["a"] = a
-            if step == 4:
-                a4 = small("a4")
-                nc.vector.tensor_scalar(out=a4[:], in0=f["a"][:], scalar1=1.0e8, scalar2=0.25, op0=ALU.min, op1=ALU.mult)
-                f["a4"] = a4
-            if step == 5:
-                am = small("am")
-                nc.vector.scalar_tensor_tensor(
-                    out=am[:], in0=f["mu"][:], scalar=-1.0, in1=f["a4"][:], op0=ALU.mult, op1=ALU.mult
-                )
-                f["am"] = am
-                dl = work.tile([P, GROUP, 3], F32, name="dl")
-                nc.vector.tensor_tensor(
-                    out=dl[:], in0=f["a4"][:, :, 0:3], in1=f["a4"][:, :, 3:4].to_broadcast([P, GROUP, 3]), op=ALU.subtract
-                )
-                f["dl"] = dl
-            if step == 6:
-                nk = work.tile([P, GROUP], F32, name="nk")
-                nc.vector.tensor_reduce(out=nk[:], in_=f["am"][:], axis=AX.X, op=ALU.add)
-                f["nk"] = nk
-                ob = work.tile([P, GROUP, OC], F32, name="ob")
-                f["ob"] = ob
 
-        def fin_first(gi, k):
-            f = FIN[gi]
-            f0 = work.tile([P, OC], F32, name="f0")
+        def small(name, shape):
+            return work.tile([P] + shape, F32, name=name)
+
+        def others(g):
+            ts = slice(g * GROUP, (g + 1) * GROUP)
+            f = {"sum3": small("sum3", [GROUP]), "squares3": small("squares3", [GROUP])}
+            nc.vector.tensor_reduce(out=f["sum3"][:], in_=row_sum[:, ts, 0 : HN - 1], axis=AX.X, op=ALU.add)
+            nc.vector.tensor_reduce(out=f["squares3"][:], in_=row_squares[:, ts, 0 : HN - 1], axis=AX.X, op=ALU.add)
+            stats[g] = f
+
+        def last_expert(g):
+            ts = slice(g * GROUP, (g + 1) * GROUP)
+            f = stats[g]
+            nc.vector.tensor_scalar_mul(out=row_sum[:, ts, HN - 1], in0=f["sum3"][:], scalar1=-1.0)
+            nc.vector.scalar_tensor_tensor(
+                out=row_squares[:, ts, HN - 1], in0=row_squares[:, ts, HN - 1], scalar=1.0 * HN * OC, in1=f["squares3"][:],
+                op0=ALU.add, op1=ALU.subtract,
+            )
+
+        def row_mean(g):
+            f = stats[g]
+            f["mean"] = small("mean", [GROUP, HN])
+            nc.vector.tensor_scalar_mul(out=f["mean"][:], in0=row_sum[:, g * GROUP : (g + 1) * GROUP, :], scalar1=1.0 / OC)
+
+        def row_mean_squared(g):
+            f = stats[g]
+            f["mean2"] = small("mean2", [GROUP, HN])
+            nc.vector.tensor_tensor(out=f["mean2"][:], in0=f["mean"][:], in1=f["mean"][:], op=ALU.mult)
+
+        def row_variance(g):
+            f = stats[g]
+            f["var"] = small("var", [GROUP, HN])
+            nc.vector.scalar_tensor_tensor(
+                out=f["var"][:], in0=row_squares[:, g * GROUP : (g + 1) * GROUP, :], scalar=1.0 / OC, in1=f["mean2"][:],
+                op0=ALU.mult, op1=ALU.subtract,
+            )
+
+        def row_rsqrt(g):
+            f = stats[g]
+            f["rsqrt"] = small("row_rsqrt", [GROUP, HN])
+            nc.scalar.activation(out=f["rsqrt"][:], in_=f["var"][:], func=ACT.Abs_reciprocal_sqrt)
+
+        def row_factor(g):
+            f = stats[g]
+            f["a"] = small("a", [GROUP, HN])
+            nc.vector.tensor_scalar(
+                out=f["a"][:], in0=f["rsqrt"][:], scalar1=1.0e8, scalar2=1.0 / HN, op0=ALU.min, op1=ALU.mult
+            )
+
+        def row_terms(g):
+            f = stats[g]
+            f["shift"] = small("shift", [GROUP, HN])
+            nc.vector.scalar_tensor_tensor(
+                out=f["shift"][:], in0=f["mean"][:], scalar=-1.0, in1=f["a"][:], op0=ALU.mult, op1=ALU.mult
+            )
+            f["diff"] = small("diff", [GROUP, HN - 1])
+            nc.vector.tensor_tensor(
+                out=f["diff"][:], in0=f["a"][:, :, 0 : HN - 1],
+                in1=f["a"][:, :, HN - 1 : HN].to_broadcast([P, GROUP, HN - 1]), op=ALU.subtract,
+            )
+
+        def row_shift(g):
+            f = stats[g]
+            f["offset"] = small("offset", [GROUP])
+            nc.vector.tensor_reduce(out=f["offset"][:], in_=f["shift"][:], axis=AX.X, op=ALU.add)
+            f["out"] = small("out_rows", [GROUP, OC])
+
+        def first_term(g, k):
+            f = stats[g]
+            f[("part0", k)] = small("part0", [OC])
             nc.gpsimd.tensor_scalar(
-                out=f0[:], in0=U[gi * GROUP + k][:, 0, :], scalar1=f["dl"][:, k, 0:1], scalar2=f["nk"][:, k : k + 1],
-                op0=ALU.mult, op1=ALU.add,
+                out=f[("part0", k)][:], in0=normed[g * GROUP + k][:, 0, :], scalar1=f["diff"][:, k, 0:1],
+                scalar2=f["offset"][:, k : k + 1], op0=ALU.mult, op1=ALU.add,
             )
-            f[("f0", k)] = f0
 
-        def fin_second(gi, k):
-            f = FIN[gi]
-            f1 = work.tile([P, OC], F32, name="f1")
+        def second_term(g, k):
+            f = stats[g]
+            f[("part1", k)] = small("part1", [OC])
             nc.vector.scalar_tensor_tensor(
-                out=f1[:], in0=U[gi * GROUP + k][:, 1, :], scalar=f["dl"][:, k, 1:2], in1=f[("f0", k)][:],
-                op0=ALU.mult, op1=ALU.add,
+                out=f[("part1", k)][:], in0=normed[g * GROUP + k][:, 1, :], scalar=f["diff"][:, k, 1:2],
+                in1=f[("part0", k)][:], op0=ALU.mult, op1=ALU.add,
             )
-            f[("f1", k)] = f1
 
-        def fin_third(gi, k):
-            f = FIN[gi]
+        def third_term(g, k):
+            f = stats[g]
             nc.vector.scalar_tensor_tensor(
-                out=f["ob"][:, k, :], in0=U.pop(gi * GROUP + k)[:, 2, :], scalar=f["dl"][:, k, 2:3], in1=f[("f1", k)][:],
-                op0=ALU.mult, op1=ALU.add,
+                out=f["out"][:, k, :], in0=normed.pop(g * GROUP + k)[:, 2, :], scalar=f["diff"][:, k, 2:3],
+                in1=f[("part1", k)][:], op0=ALU.mult, op1=ALU.add,
             )
 
-        def fin_store(gi):
-            f = FIN.pop(gi)
-            nc.sync.dma_start(out=out_view[:, gi * GROUP : (gi + 1) * GROUP, :], in_=f["ob"][:])
+        def store(g):
+            nc.sync.dma_start(out=out_view[:, g * GROUP : (g + 1) * GROUP, :], in_=stats.pop(g)["out"][:])
 
-        def ok(t):
+        def live(t):
             return 0 <= t < NT
 
-        def usq_tile(t):
-            for n in range(HN - 1):
-                e_usq(HN * t + n)
+        def since_stats(g, j):
+            return j - (g * GROUP + GROUP - 1 + STATS)
 
-        for j in range(-2, NT + 9):
-            if ok(j + AHEAD) and j + AHEAD >= AHEAD:
-                load(j + AHEAD, 1)
-            for gi in range(NT // GROUP):
-                d = j - (gi * GROUP + GROUP - 1 + 4)
-                if d == 1:
-                    fin(gi, 3)
+        for j in range(-2, NT + STATS + GROUP + 1):
+            if j >= 0 and live(j + AHEAD):
+                load(j + AHEAD)
+            for g in range(NG):
+                if since_stats(g, j) == 1:
+                    row_rsqrt(g)
             for n in range(HN):
-                if ok(j) and l_on_vector(j, n):
-                    leave(HN * j + n)
-            if ok(j - 2):
-                e_centre(j - 2)
-                e_square(j - 2)
-            for gi in range(NT // GROUP):
-                d = j - (gi * GROUP + GROUP - 1 + 4)
-                if 2 <= d < 2 + GROUP:
-                    fin_first(gi, d - 2)
-            if ok(j - 3):
-                e_lack(j - 3)
-            if ok(j - 4):
-                usq_tile(j - 4)
-            if ok(j - 1):
-                for n in range(HN):
-                    weigh(HN * (j - 1) + n)
+                if live(j) and slope_on_vector(j, n):
+                    slope(HN * j + n)
+            if live(j - 2):
+                centre(j - 2)
+                square(j - 2)
+            for g in range(NG):
+                if 2 <= since_stats(g, j) < 2 + GROUP:
+                    first_term(g, since_stats(g, j) - 2)
+            if live(j - 3):
+                fetch_lack(j - 3)
+            if live(j - STATS):
+                sum_normed_squares(j - STATS)
+            if live(j - 1):
+                weigh(j - 1)
             for n in range(HN):
-                if n == 2 and ok(j - 3):
-                    e_u(j - 3)
-                if ok(j):
-                    rectify_psum(HN * j + n)
-                if ok(j + 1):
+                if n == 2 and live(j - 3):
+                    normalise(j - 3)
+                if live(j):
+                    rectify(HN * j + n)
+                if live(j + 1):
                     transposes(HN * (j + 1) + n)
-                    if not l_on_vector(j + 1, n):
-                        leave(HN * (j + 1) + n)
-                if n == 1 and ok(j - 1):
-                    e_sum(j - 1)
-                    e_nm(j - 1)
-                if n == 1 and ok(j - 2):
-                    e_q(j - 2)
-                    e_r(j - 2)
-            small = []
-            for gi in range(NT // GROUP):
-                d = j - (gi * GROUP + GROUP - 1 + 4)
+                    if not slope_on_vector(j + 1, n):
+                        slope(HN * (j + 1) + n)
+                if n == 1 and live(j - 1):
+                    sum_weighted(j - 1)
+                    negative_mean(j - 1)
+                if n == 1 and live(j - 2):
+                    sum_squares(j - 2)
+                    rsqrt(j - 2)
+            steps = []
+            for g in range(NG):
+                d = since_stats(g, j)
                 if 2 <= d < 2 + GROUP:
-                    small.append((fin_second, gi, d - 2))
+                    steps.append((second_term, (g, d - 2)))
                 if d == 0:
-                    small.extend([(fin, gi, step) for step in range(-2, 3)])
+                    steps.extend([(fn, (g,)) for fn in (others, last_expert, row_mean, row_mean_squared, row_variance)])
                 if d == 1:
-                    small.extend([(fin, gi, step) for step in range(4, 7)])
-            for gi in range(NT // GROUP):
-                d = j - (gi * GROUP + GROUP - 1 + 4)
+                    steps.extend([(fn, (g,)) for fn in (row_factor, row_terms, row_shift)])
+            for g in range(NG):
+                d = since_stats(g, j)
                 if 2 <= d < 2 + GROUP:
-                    small.append((fin_third, gi, d - 2))
+                    steps.append((third_term, (g, d - 2)))
+
+            def one_step():
+                if steps:
+                    fn, args = steps.pop(0)
+                    fn(*args)
+
             for i in range(2):
-                if ok(j):
+                if live(j):
                     quantise(2 * j + i)
-                    mx(2 * j + i)
-                if i == 0 and ok(j - 1):
-                    e_nmback(j - 1)
-                if i == 0 and ok(j - 2):
-                    e_rback(j - 2)
-                if small:
-                    fn, gi, arg = small.pop(0)
-                    fn(gi, arg)
+                    multiply(2 * j + i)
+                if i == 0 and live(j - 1):
+                    mean_back(j - 1)
+                if i == 0 and live(j - 2):
+                    rsqrt_back(j - 2)
+                one_step()
                 for n in (2 * i, 2 * i + 1):
-                    if ok(j + 2):
+                    if live(j + 2):
                         flip(HN * (j + 2) + n)
-                    if small:
-                        fn, gi, arg = small.pop(0)
-                        fn(gi, arg)
-            for fn, gi, arg in small:
-                fn(gi, arg)
+                    one_step()
+            while steps:
+                one_step()
             if j == -2:
-                for a in range(8):
-                    w_regroup(a)
+                for a in range(HN * PASSES):
+                    regroup_w(a)
             if j == -1:
                 for n in range(HN):
-                    w_quantise(n)
-            for gi in range(NT // GROUP):
-                if j - (gi * GROUP + GROUP - 1 + 4) == 1 + GROUP:
-                    fin_store(gi)
+                    quantise_w(n)
+            for g in range(NG):
+                if since_stats(g, j) == 1 + GROUP:
+                    store(g)

@@ -48,7 +48,7 @@ def tile_tensormoe_pb_t_kernel(tc, h_pre, W_mo, weights_n, leak_n, out):
         weights_bf = const.tile([P, NT * HN], BF16)
         nc.sync.dma_start(out=weights_bf[:], in_=weights_n.rearrange("(p t) n -> p (t n)", t=NT))
 
-        rows, bank, sloped, rect, quantised, prod, weighted, centred, squares = {}, {}, {}, {}, {}, {}, {}, {}, {}
+        rows, signed, bank, sloped, rect, quantised, prod, weighted, centred, squares = {}, {}, {}, {}, {}, {}, {}, {}, {}, {}
         mean_sum, square_sum, turned, lacking, normed, stats = {}, {}, {}, {}, {}, {}
 
         def new_rows(t):
@@ -112,18 +112,24 @@ def tile_tensormoe_pb_t_kernel(tc, h_pre, W_mo, weights_n, leak_n, out):
 
         def flip(s):
             t, n = divmod(s, HN)
-            x = rows[t][:, n * HM : (n + 1) * HM]
-            nc.vector.tensor_scalar(out=x, in0=x, scalar1=sign[:, n : n + 1], scalar2=None, op0=ALU.mult)
+            if n == 0:
+                signed[t] = work.tile([P, HN * HM], BF16, name="signed", bufs=3)
+            cols = slice(n * HM, (n + 1) * HM)
+            nc.vector.tensor_scalar(
+                out=signed[t][:, cols].rearrange("p (u w e) -> p u w e", u=2, e=2),
+                in0=rows[t][:, cols].rearrange("p (w u e) -> p u w e", u=2, e=2),
+                scalar1=sign[:, n : n + 1], scalar2=None, op0=ALU.mult,
+            )
 
         def transposes(s):
             t, n = divmod(s, HN)
-            words = rows[t][:].bitcast(F32)
+            words = signed[t][:].bitcast(F32)
             bank[s] = bank_pool.tile([P, WORDS], F32, name="bank")
             for u in range(2):
                 for g in range(PASSES):
-                    first = n * WORDS + g * 2 * P
                     at = (u * PASSES + g) * P
-                    nc.tensor.transpose(bank[s][:, at : at + P], words[:, first + u : first + 2 * P : 2], ident[:])
+                    first = n * WORDS + at
+                    nc.tensor.transpose(bank[s][:, at : at + P], words[:, first : first + P], ident[:])
 
         def slope(s):
             t, n = divmod(s, HN)

@@ -18,15 +18,14 @@ NT = B // P
 PASSES = HM // (4 * P)
 WORDS = HM // 2
 GROUP = 4
-NG = NT // GROUP
+FIRST = list(range(0, NT - 4, GROUP)) + [NT - 4, NT - 2, NT - 1, NT]
+NG = len(FIRST) - 1
 FLOPS = 2 * B * HN * HM * OC
 
 AHEAD = 4
+COMBINE = 3
+RUN = 4
 STATS = 4
-
-
-def slope_on_vector(t, n):
-    return n == HN - 1 and t % 4 == 0
 
 
 def tile_tensormoe_pb_t_kernel(tc, h_pre, W_mo, weights_n, leak_n, out):
@@ -35,36 +34,40 @@ def tile_tensormoe_pb_t_kernel(tc, h_pre, W_mo, weights_n, leak_n, out):
         ctx.enter_context(tc.manual_schedule())
         const = ctx.enter_context(tc.tile_pool(name="const", bufs=1))
         work = ctx.enter_context(tc.tile_pool(name="work", bufs=2))
-        bank_pool = ctx.enter_context(tc.psum_pool(name="bank_pool", bufs=HN))
+        bank_pool = ctx.enter_context(tc.psum_pool(name="bank_pool", bufs=3))
         prod_pool = ctx.enter_context(tc.psum_pool(name="prod_pool", bufs=2))
         sum_pool = ctx.enter_context(tc.psum_pool(name="sum_pool", bufs=2))
+        out_pool = ctx.enter_context(tc.psum_pool(name="out_pool", bufs=1))
 
         h_view = h_pre.rearrange("(p t) n m -> p t (n m)", t=NT)
         out_view = out.rearrange("(p t) o -> p t o", t=NT)
-        w_view = W_mo.rearrange("n (g p j) o -> p (n g) (j o)", g=PASSES, p=P, j=4)
+        w_view = W_mo.rearrange("n (g s u r e) o -> r u s (n g) (e o)", g=PASSES, s=P // RUN, u=2, r=RUN, e=2)
 
         leak_bf = const.tile([P, HN], BF16)
         nc.sync.dma_start(out=leak_bf[:], in_=leak_n.partition_broadcast(P))
         weights_bf = const.tile([P, NT * HN], BF16)
         nc.sync.dma_start(out=weights_bf[:], in_=weights_n.rearrange("(p t) n -> p (t n)", t=NT))
 
+        negative = {}
         rows, signed, bank, sloped, rect, quantised, prod, weighted, centred, squares = {}, {}, {}, {}, {}, {}, {}, {}, {}, {}
         mean_sum, square_sum, turned, lacking, normed, stats = {}, {}, {}, {}, {}, {}
 
         def new_rows(t):
-            rows[t] = work.tile([P, HN * HM], BF16, name="rows", bufs=AHEAD + 3)
+            rows[t] = work.tile([P, HN * HM], BF16, name="rows", bufs=AHEAD + 1)
 
         def load(t):
             new_rows(t)
             nc.sync.dma_start(out=rows[t][:], in_=h_view[:, t, :])
 
-        w_raw = const.tile([P, HN * PASSES * 4 * OC], BF16)
+        w_raw = const.tile([P, HN * PASSES, 2, 2 * OC], BF16)
         new_rows(0)
         for n in range(HN):
             nc.sync.dma_start(out=rows[0][:, n * HM : (n + 1) * HM], in_=h_view[:, 0, n * HM : (n + 1) * HM])
-            for a in range(n * PASSES, (n + 1) * PASSES):
-                nc.sync.dma_start(out=w_raw[:, a * 4 * OC : (a + 1) * 4 * OC], in_=w_view[:, a, :])
-        for t in range(1, AHEAD):
+        load(1)
+        for u in range(2):
+            for r in range(RUN):
+                nc.sync.dma_start(out=w_raw[r::RUN, :, u, :], in_=w_view[r, u])
+        for t in range(2, AHEAD):
             load(t)
 
         ident = const.tile([P, P], F32)
@@ -79,6 +82,7 @@ def tile_tensormoe_pb_t_kernel(tc, h_pre, W_mo, weights_n, leak_n, out):
         sign = const.tile([P, HN], F32)
         nc.vector.tensor_scalar(out=sign[:], in0=leak[:], scalar1=1.0, scalar2=-2.0, op0=ALU.is_gt, op1=ALU.mult)
         nc.vector.tensor_scalar_add(out=sign[:], in0=sign[:], scalar1=1.0)
+        nc.vector.memset(sign[:, HN - 1 : HN], 1.0)
         signed_weights = const.tile([P, NT, HN], F32)
         nc.vector.tensor_tensor(
             out=signed_weights[:],
@@ -87,28 +91,23 @@ def tile_tensormoe_pb_t_kernel(tc, h_pre, W_mo, weights_n, leak_n, out):
             op=ALU.mult,
         )
 
-        w_grouped = const.tile([P, HN * PASSES * OC * 4], BF16, align_bytes=64)
         w_codes = const.tile([P, HN * PASSES * OC], U32, align_bytes=64)
         w_scales = const.tile([P, HN * PASSES * OC], U8, align_bytes=64)
-        w_from = w_raw[:].rearrange("p (a j o) -> p a o j", a=HN * PASSES, j=4, o=OC)
-        w_to = w_grouped[:].rearrange("p (a o j) -> p a o j", a=HN * PASSES, j=4, o=OC)
+        w_from = w_raw[:].rearrange("p a u (e o) -> p a o (u e)", e=2, o=OC)
 
-        def regroup_w(a):
-            if a % 2 == 1:
-                nc.scalar.copy(out=w_to[:, a], in_=w_from[:, a])
-            else:
-                nc.vector.tensor_copy(out=w_to[:, a], in_=w_from[:, a])
-
-        def quantise_w(n):
+        def prepare_w(n):
+            grouped = work.tile([P, 2 * HM], BF16, name="rect", bufs=4, align_bytes=64)
+            to = grouped[:].rearrange("p (g o j) -> p g o j", g=PASSES, j=4)
+            nc.scalar.copy(out=to[:, 1], in_=w_from[:, n * PASSES + 1])
+            nc.vector.tensor_copy(out=to[:, 0], in_=w_from[:, n * PASSES])
             cols = slice(n * PASSES * OC, (n + 1) * PASSES * OC)
-            nc.vector.quantize_mx(
-                out=w_codes[:, cols].bitcast(FP8X4),
-                scales=w_scales[:, cols],
-                in_=w_grouped[:, n * PASSES * OC * 4 : (n + 1) * PASSES * OC * 4],
-            )
+            nc.vector.quantize_mx(out=w_codes[:, cols].bitcast(FP8X4), scales=w_scales[:, cols], in_=grouped[:])
 
         row_sum = const.tile([P, NT, HN], F32)
         row_squares = const.tile([P, NT, HN], F32)
+
+        def spread(x):
+            return x.rearrange("p (s u v) -> p u s v", u=2, v=2 * RUN)
 
         def flip(s):
             t, n = divmod(s, HN)
@@ -116,9 +115,35 @@ def tile_tensormoe_pb_t_kernel(tc, h_pre, W_mo, weights_n, leak_n, out):
                 signed[t] = work.tile([P, HN * HM], BF16, name="signed", bufs=3)
             cols = slice(n * HM, (n + 1) * HM)
             nc.vector.tensor_scalar(
-                out=signed[t][:, cols].rearrange("p (u w e) -> p u w e", u=2, e=2),
-                in0=rows[t][:, cols].rearrange("p (w u e) -> p u w e", u=2, e=2),
+                out=signed[t][:, cols].rearrange("p (u s v) -> p u s v", u=2, v=2 * RUN), in0=spread(rows[t][:, cols]),
                 scalar1=sign[:, n : n + 1], scalar2=None, op0=ALU.mult,
+            )
+
+        LAST = slice((HN - 1) * HM, HN * HM)
+
+        def negative_part(t):
+            negative[t] = work.tile([P, HM], BF16, name="negative")
+            nc.vector.tensor_scalar(
+                out=negative[t][:].rearrange("p (u s v) -> p u s v", u=2, v=2 * RUN), in0=spread(rows[t][:, LAST]),
+                scalar1=0.0, scalar2=leak[:, HN - 1 : HN], op0=ALU.min, op1=ALU.mult,
+            )
+
+        def positive_part(t):
+            nc.vector.tensor_scalar(
+                out=signed[t][:, LAST].rearrange("p (u s v) -> p u s v", u=2, v=2 * RUN), in0=spread(rows[t][:, LAST]),
+                scalar1=0.0, scalar2=None, op0=ALU.max,
+            )
+
+        def add_parts(t):
+            nc.vector.tensor_tensor(
+                out=signed[t][:, LAST], in0=signed[t][:, LAST], in1=negative.pop(t)[:], op=ALU.add,
+            )
+
+        def copy_out(s):
+            q = s // 2
+            nc.scalar.copy(
+                out=rect[q][:, HM : 2 * HM].bitcast(F32).rearrange("p (w u) -> p w u", u=2),
+                in_=bank.pop(s)[:].rearrange("p (u w) -> p w u", u=2),
             )
 
         def transposes(s):
@@ -133,17 +158,18 @@ def tile_tensormoe_pb_t_kernel(tc, h_pre, W_mo, weights_n, leak_n, out):
 
         def slope(s):
             t, n = divmod(s, HN)
-            sloped[s] = work.tile([P, HM], BF16, name="sloped", bufs=HN)
+            sloped[s] = work.tile([P, HM], BF16, name="sloped", bufs=3)
             x = bank[s][:].bitcast(BF16)
-            if slope_on_vector(t, n):
-                nc.vector.tensor_scalar(out=sloped[s][:], in0=x, scalar1=leak[:, n : n + 1], scalar2=None, op0=ALU.mult)
-            else:
-                nc.scalar.activation(out=sloped[s][:], in_=x, func=ACT.Copy, scale=leak[:, n : n + 1])
+            nc.scalar.activation(out=sloped[s][:], in_=x, func=ACT.Copy, scale=leak[:, n : n + 1])
+
+        def new_rect(q):
+            rect[q] = work.tile([P, 2 * HM], BF16, name="rect", bufs=4, align_bytes=64)
 
         def rectify(s):
             q = s // 2
-            if s % 2 == 0:
-                rect[q] = work.tile([P, 2 * HM], BF16, name="rect", bufs=3, align_bytes=64)
+            if s % 4 == 0:
+                new_rect(q)
+                new_rect(q + 1)
             nc.vector.tensor_tensor(
                 out=rect[q][:, (s % 2) * HM : (s % 2 + 1) * HM].rearrange("p (w u e) -> p w u e", u=2, e=2),
                 in0=sloped.pop(s)[:].rearrange("p (u w e) -> p w u e", u=2, e=2),
@@ -229,6 +255,13 @@ def tile_tensormoe_pb_t_kernel(tc, h_pre, W_mo, weights_n, leak_n, out):
             squares[t] = work.tile([P, HN, OC], F32, name="squares")
             nc.gpsimd.tensor_tensor(out=squares[t][:], in0=centred[t][:], in1=centred[t][:], op=ALU.mult)
 
+        def square_on_three(t):
+            squares[t] = work.tile([P, HN, OC], F32, name="squares")
+            for n in (0, 1):
+                nc.scalar.activation(out=squares[t][:, n, :], in_=centred[t][:, n, :], func=ACT.Square)
+            nc.gpsimd.tensor_tensor(out=squares[t][:, 2, :], in0=centred[t][:, 2, :], in1=centred[t][:, 2, :], op=ALU.mult)
+            nc.vector.tensor_tensor(out=squares[t][:, 3, :], in0=centred[t][:, 3, :], in1=centred[t][:, 3, :], op=ALU.mult)
+
         def sum_squares(t):
             square_sum[t] = sum_over_experts(squares.pop(t))
 
@@ -257,7 +290,7 @@ def tile_tensormoe_pb_t_kernel(tc, h_pre, W_mo, weights_n, leak_n, out):
             )
 
         def normalise(t):
-            normed[t] = work.tile([P, HN - 1, OC], F32, name="normed", bufs=10)
+            normed[t] = work.tile([P, HN - 1, OC], F32, name="normed", bufs=11)
             for n in range(HN - 1):
                 nc.vector.scalar_tensor_tensor(
                     out=normed[t][:, n, :], in0=square_sum[t][:, OC : 2 * OC], scalar=1.0e8, in1=centred[t][:, n, :],
@@ -273,18 +306,21 @@ def tile_tensormoe_pb_t_kernel(tc, h_pre, W_mo, weights_n, leak_n, out):
                     out=unused[:], in_=normed[t][:, n, :], func=ACT.Square, accum_out=row_squares[:, t, n : n + 1]
                 )
 
+        def size(g):
+            return FIRST[g + 1] - FIRST[g]
+
         def small(name, shape):
-            return work.tile([P] + shape, F32, name=name)
+            return work.tile([P] + shape, F32, name=name, bufs=4)
 
         def others(g):
-            ts = slice(g * GROUP, (g + 1) * GROUP)
-            f = {"sum3": small("sum3", [GROUP]), "squares3": small("squares3", [GROUP])}
+            ts = slice(FIRST[g], FIRST[g + 1])
+            f = {"sum3": small("sum3", [size(g)]), "squares3": small("squares3", [size(g)])}
             nc.vector.tensor_reduce(out=f["sum3"][:], in_=row_sum[:, ts, 0 : HN - 1], axis=AX.X, op=ALU.add)
             nc.vector.tensor_reduce(out=f["squares3"][:], in_=row_squares[:, ts, 0 : HN - 1], axis=AX.X, op=ALU.add)
             stats[g] = f
 
         def last_expert(g):
-            ts = slice(g * GROUP, (g + 1) * GROUP)
+            ts = slice(FIRST[g], FIRST[g + 1])
             f = stats[g]
             nc.vector.tensor_scalar_mul(out=row_sum[:, ts, HN - 1], in0=f["sum3"][:], scalar1=-1.0)
             nc.vector.scalar_tensor_tensor(
@@ -294,160 +330,276 @@ def tile_tensormoe_pb_t_kernel(tc, h_pre, W_mo, weights_n, leak_n, out):
 
         def row_mean(g):
             f = stats[g]
-            f["mean"] = small("mean", [GROUP, HN])
-            nc.vector.tensor_scalar_mul(out=f["mean"][:], in0=row_sum[:, g * GROUP : (g + 1) * GROUP, :], scalar1=1.0 / OC)
+            f["mean"] = small("mean", [size(g), HN])
+            nc.vector.tensor_scalar_mul(out=f["mean"][:], in0=row_sum[:, FIRST[g] : FIRST[g + 1], :], scalar1=1.0 / OC)
 
         def row_mean_squared(g):
             f = stats[g]
-            f["mean2"] = small("mean2", [GROUP, HN])
+            f["mean2"] = small("mean2", [size(g), HN])
             nc.vector.tensor_tensor(out=f["mean2"][:], in0=f["mean"][:], in1=f["mean"][:], op=ALU.mult)
 
         def row_variance(g):
             f = stats[g]
-            f["var"] = small("var", [GROUP, HN])
+            f["var"] = small("var", [size(g), HN])
             nc.vector.scalar_tensor_tensor(
-                out=f["var"][:], in0=row_squares[:, g * GROUP : (g + 1) * GROUP, :], scalar=1.0 / OC, in1=f["mean2"][:],
+                out=f["var"][:], in0=row_squares[:, FIRST[g] : FIRST[g + 1], :], scalar=1.0 / OC, in1=f["mean2"][:],
                 op0=ALU.mult, op1=ALU.subtract,
             )
 
         def row_rsqrt(g):
             f = stats[g]
-            f["rsqrt"] = small("row_rsqrt", [GROUP, HN])
+            f["rsqrt"] = small("row_rsqrt", [size(g), HN])
             nc.scalar.activation(out=f["rsqrt"][:], in_=f["var"][:], func=ACT.Abs_reciprocal_sqrt)
 
         def row_factor(g):
             f = stats[g]
-            f["a"] = small("a", [GROUP, HN])
+            f["a"] = small("a", [size(g), HN])
             nc.vector.tensor_scalar(
                 out=f["a"][:], in0=f["rsqrt"][:], scalar1=1.0e8, scalar2=1.0 / HN, op0=ALU.min, op1=ALU.mult
             )
 
         def row_terms(g):
             f = stats[g]
-            f["shift"] = small("shift", [GROUP, HN])
+            f["shift"] = small("shift", [size(g), HN])
             nc.vector.scalar_tensor_tensor(
                 out=f["shift"][:], in0=f["mean"][:], scalar=-1.0, in1=f["a"][:], op0=ALU.mult, op1=ALU.mult
             )
-            f["diff"] = small("diff", [GROUP, HN - 1])
+            f["diff"] = small("diff", [size(g), HN - 1])
             nc.vector.tensor_tensor(
                 out=f["diff"][:], in0=f["a"][:, :, 0 : HN - 1],
-                in1=f["a"][:, :, HN - 1 : HN].to_broadcast([P, GROUP, HN - 1]), op=ALU.subtract,
+                in1=f["a"][:, :, HN - 1 : HN].to_broadcast([P, size(g), HN - 1]), op=ALU.subtract,
             )
 
         def row_shift(g):
             f = stats[g]
-            f["offset"] = small("offset", [GROUP])
+            f["offset"] = small("offset", [size(g)])
             nc.vector.tensor_reduce(out=f["offset"][:], in_=f["shift"][:], axis=AX.X, op=ALU.add)
-            f["out"] = small("out_rows", [GROUP, OC])
+            f["out"] = small("out_rows", [size(g), OC])
 
-        def first_term(g, k):
+        def diagonals(g, k):
             f = stats[g]
-            f[("part0", k)] = small("part0", [OC])
-            nc.gpsimd.tensor_scalar(
-                out=f[("part0", k)][:], in0=normed[g * GROUP + k][:, 0, :], scalar1=f["diff"][:, k, 0:1],
-                scalar2=f["offset"][:, k : k + 1], op0=ALU.mult, op1=ALU.add,
+            f[("diag", k)] = work.tile([P, HN - 1, P], F32, name="diag", bufs=3)
+            for n in range(HN - 1):
+                nc.gpsimd.tensor_scalar(
+                    out=f[("diag", k)][:, n, :], in0=ident[:], scalar1=f["diff"][:, k, n : n + 1], scalar2=0.0,
+                    op0=ALU.mult, op1=ALU.add,
+                )
+
+        def combine(g, k, n, pool=None):
+            f = stats[g]
+            if n == 0:
+                if pool is None:
+                    f[("sum", k)] = out_pool.tile([P, 2 * OC], F32, name="out_sum")
+                else:
+                    f[("sum", k)] = pool.tile([P, WORDS], F32, name="bank")
+            nc.tensor.matmul(
+                out=f[("sum", k)][:, 0:OC], lhsT=f[("diag", k)][:, n, :], rhs=normed[FIRST[g] + k][:, n, :],
+                start=(n == 0), stop=(n == HN - 2),
             )
 
-        def second_term(g, k):
+        def finish(g, k):
             f = stats[g]
-            f[("part1", k)] = small("part1", [OC])
-            nc.vector.scalar_tensor_tensor(
-                out=f[("part1", k)][:], in0=normed[g * GROUP + k][:, 1, :], scalar=f["diff"][:, k, 1:2],
-                in1=f[("part0", k)][:], op0=ALU.mult, op1=ALU.add,
+            nc.scalar.activation(
+                out=f["out"][:, k, :], in_=f[("sum", k)][:, 0:OC], func=ACT.Identity, bias=f["offset"][:, k : k + 1]
             )
 
-        def third_term(g, k):
+        def output_on_tensor(g, k):
+            for n in range(HN - 1):
+                combine(g, k, n, bank_pool)
+            finish(g, k)
+
+        def output_on_vector(g, k):
             f = stats[g]
-            nc.vector.scalar_tensor_tensor(
-                out=f["out"][:, k, :], in0=normed.pop(g * GROUP + k)[:, 2, :], scalar=f["diff"][:, k, 2:3],
-                in1=f[("part1", k)][:], op0=ALU.mult, op1=ALU.add,
+            u = normed[FIRST[g] + k]
+            nc.vector.tensor_scalar(
+                out=f["out"][:, k, :], in0=u[:, 0, :], scalar1=f["diff"][:, k, 0:1], scalar2=f["offset"][:, k : k + 1],
+                op0=ALU.mult, op1=ALU.add,
             )
+            for n in (1, 2):
+                nc.vector.scalar_tensor_tensor(
+                    out=f["out"][:, k, :], in0=u[:, n, :], scalar=f["diff"][:, k, n : n + 1], in1=f["out"][:, k, :],
+                    op0=ALU.mult, op1=ALU.add,
+                )
+
+        def first_steps(g):
+            for fn in (others, last_expert, row_mean, row_mean_squared, row_variance):
+                fn(g)
+            row_rsqrt(g)
+
+        def last_steps(g):
+            for fn in (row_factor, row_terms, row_shift):
+                fn(g)
 
         def store(g):
-            nc.sync.dma_start(out=out_view[:, g * GROUP : (g + 1) * GROUP, :], in_=stats.pop(g)["out"][:])
+            nc.sync.dma_start(out=out_view[:, FIRST[g] : FIRST[g + 1], :], in_=stats.pop(g)["out"][:])
 
         def live(t):
             return 0 <= t < NT
 
         def since_stats(g, j):
-            return j - (g * GROUP + GROUP - 1 + STATS)
+            return j - (FIRST[g + 1] - 1 + STATS)
 
-        for j in range(-2, NT + STATS + GROUP + 1):
+        turn_of = {}
+        last_turn = 0
+        for g in range(NG):
+            for k in range(size(g)):
+                last_turn = max(last_turn + 1, FIRST[g + 1] - 1 + STATS + COMBINE)
+                turn_of[last_turn] = (g, k)
+
+        def output(fn, j, *args):
+            if j in turn_of:
+                fn(*turn_of[j], *args)
+
+        for j in range(-2, NT):
+            s = HN * j
             if j >= 0 and live(j + AHEAD):
                 load(j + AHEAD)
             for g in range(NG):
                 if since_stats(g, j) == 1:
                     row_rsqrt(g)
-            for n in range(HN):
-                if live(j) and slope_on_vector(j, n):
-                    slope(HN * j + n)
+            if live(j - 1):
+                multiply(2 * j - 2)
+                multiply(2 * j - 1)
+            output(diagonals, j + 1)
+            if live(j):
+                slope(s + 2)
             if live(j - 2):
                 centre(j - 2)
                 square(j - 2)
-            for g in range(NG):
-                if 2 <= since_stats(g, j) < 2 + GROUP:
-                    first_term(g, since_stats(g, j) - 2)
             if live(j - 3):
                 fetch_lack(j - 3)
             if live(j - STATS):
                 sum_normed_squares(j - STATS)
+            if live(j):
+                rectify(s)
+                transposes(s + 3)
+                rectify(s + 1)
+            if live(j + 1):
+                transposes(s + 4)
+            output(combine, j, 0)
             if live(j - 1):
                 weigh(j - 1)
-            for n in range(HN):
-                if n == 2 and live(j - 3):
-                    normalise(j - 3)
-                if live(j):
-                    rectify(HN * j + n)
-                if live(j + 1):
-                    transposes(HN * (j + 1) + n)
-                    if not slope_on_vector(j + 1, n):
-                        slope(HN * (j + 1) + n)
-                if n == 1 and live(j - 1):
-                    sum_weighted(j - 1)
-                    negative_mean(j - 1)
-                if n == 1 and live(j - 2):
-                    sum_squares(j - 2)
-                    rsqrt(j - 2)
+            if live(j):
+                copy_out(s + 3)
+            if live(j - 1):
+                sum_weighted(j - 1)
+            if live(j - 3):
+                normalise(j - 3)
+            if live(j):
+                rectify(s + 2)
+            if live(j + 1):
+                slope(s + 4)
+                transposes(s + 5)
+            if live(j - 1):
+                negative_mean(j - 1)
+            output(combine, j, 1)
+            if live(j + 1):
+                slope(s + 5)
+                transposes(s + 6)
+            if live(j - 2):
+                sum_squares(j - 2)
+            if live(j - 1):
+                mean_back(j - 1)
+            output(combine, j, 2)
+            if live(j - 2):
+                rsqrt(j - 2)
+            output(finish, j)
+            if live(j - 2):
+                rsqrt_back(j - 2)
+
             steps = []
             for g in range(NG):
                 d = since_stats(g, j)
-                if 2 <= d < 2 + GROUP:
-                    steps.append((second_term, (g, d - 2)))
                 if d == 0:
                     steps.extend([(fn, (g,)) for fn in (others, last_expert, row_mean, row_mean_squared, row_variance)])
                 if d == 1:
                     steps.extend([(fn, (g,)) for fn in (row_factor, row_terms, row_shift)])
-            for g in range(NG):
-                d = since_stats(g, j)
-                if 2 <= d < 2 + GROUP:
-                    steps.append((third_term, (g, d - 2)))
 
             def one_step():
                 if steps:
                     fn, args = steps.pop(0)
                     fn(*args)
 
-            for i in range(2):
-                if live(j):
-                    quantise(2 * j + i)
-                    multiply(2 * j + i)
-                if i == 0 and live(j - 1):
-                    mean_back(j - 1)
-                if i == 0 and live(j - 2):
-                    rsqrt_back(j - 2)
+            if live(j):
+                quantise(2 * j)
+            one_step()
+            for n in range(HN - 1):
+                if live(j + 2):
+                    flip(s + 8 + n)
+                    if n == 0:
+                        negative_part(j + 2)
+                    if n == 1:
+                        positive_part(j + 2)
                 one_step()
-                for n in (2 * i, 2 * i + 1):
-                    if live(j + 2):
-                        flip(HN * (j + 2) + n)
-                    one_step()
+            if live(j + 2):
+                add_parts(j + 2)
+            one_step()
+            if live(j):
+                quantise(2 * j + 1)
             while steps:
                 one_step()
-            if j == -2:
-                for a in range(HN * PASSES):
-                    regroup_w(a)
-            if j == -1:
+            if j == 0:
                 for n in range(HN):
-                    quantise_w(n)
-            for g in range(NG):
-                if since_stats(g, j) == 1 + GROUP:
-                    store(g)
+                    prepare_w(n)
+            if j in turn_of and turn_of[j][1] == size(turn_of[j][0]) - 1:
+                store(turn_of[j][0])
+
+        last = NT - 1
+        g4, g2, g1, g0 = NG - 4, NG - 3, NG - 2, NG - 1
+        multiply(2 * last)
+        multiply(2 * last + 1)
+        row_rsqrt(g4)
+        fetch_lack(last - 2)
+        sum_normed_squares(last - 3)
+        diagonals(g4 - 1, 2)
+        centre(last - 1)
+        square(last - 1)
+        diagonals(g4 - 1, 3)
+        normalise(last - 2)
+        last_steps(g4)
+        output_on_tensor(g4 - 1, 2)
+        weigh(last)
+        sum_weighted(last)
+        negative_mean(last)
+        mean_back(last)
+        output_on_tensor(g4 - 1, 3)
+        store(g4 - 1)
+        sum_normed_squares(last - 2)
+        diagonals(g4, 0)
+        diagonals(g4, 1)
+        sum_squares(last - 1)
+        rsqrt(last - 1)
+        rsqrt_back(last - 1)
+        first_steps(g2)
+        centre(last)
+        square_on_three(last)
+        fetch_lack(last - 1)
+        output_on_tensor(g4, 0)
+        normalise(last - 1)
+        sum_squares(last)
+        rsqrt(last)
+        rsqrt_back(last)
+        diagonals(g4, 2)
+        diagonals(g4, 3)
+        sum_normed_squares(last - 1)
+        output_on_tensor(g4, 1)
+        last_steps(g2)
+        fetch_lack(last)
+        normalise(last)
+        output_on_tensor(g4, 2)
+        diagonals(g2, 0)
+        diagonals(g2, 1)
+        first_steps(g1)
+        sum_normed_squares(last)
+        output_on_tensor(g4, 3)
+        store(g4)
+        last_steps(g1)
+        output_on_tensor(g2, 0)
+        first_steps(g0)
+        output_on_vector(g1, 0)
+        store(g1)
+        last_steps(g0)
+        output_on_tensor(g2, 1)
+        store(g2)
+        output_on_vector(g0, 0)
+        store(g0)

@@ -18,12 +18,12 @@ NT = B // P
 PASSES = HM // (4 * P)
 WORDS = HM // 2
 GROUP = 4
-FIRST = list(range(0, NT - 4, GROUP)) + [NT - 4, NT - 2, NT - 1, NT]
+FIRST = list(range(0, NT - 4, GROUP)) + [NT - 4, NT]
 NG = len(FIRST) - 1
 FLOPS = 2 * B * HN * HM * OC
 
 AHEAD = 4
-COMBINE = 3
+COMBINE = 2
 RUN = 4
 STATS = 4
 
@@ -50,7 +50,7 @@ def tile_tensormoe_pb_t_kernel(tc, h_pre, W_mo, weights_n, leak_n, out):
 
         negative = {}
         rows, signed, bank, sloped, rect, quantised, prod, weighted, centred, squares = {}, {}, {}, {}, {}, {}, {}, {}, {}, {}
-        mean_sum, square_sum, turned, lacking, normed, stats = {}, {}, {}, {}, {}, {}
+        out_sum, mean_sum, square_sum, turned, lacking, normed, stats = {}, {}, {}, {}, {}, {}, {}
 
         def new_rows(t):
             rows[t] = work.tile([P, HN * HM], BF16, name="rows", bufs=AHEAD + 1)
@@ -61,13 +61,14 @@ def tile_tensormoe_pb_t_kernel(tc, h_pre, W_mo, weights_n, leak_n, out):
 
         w_raw = const.tile([P, HN * PASSES, 2, 2 * OC], BF16)
         new_rows(0)
-        for n in range(HN):
+        for n in (0, 3, 1, 2):
             nc.sync.dma_start(out=rows[0][:, n * HM : (n + 1) * HM], in_=h_view[:, 0, n * HM : (n + 1) * HM])
         load(1)
+        load(2)
         for u in range(2):
             for r in range(RUN):
                 nc.sync.dma_start(out=w_raw[r::RUN, :, u, :], in_=w_view[r, u])
-        for t in range(2, AHEAD):
+        for t in range(3, AHEAD):
             load(t)
 
         ident = const.tile([P, P], F32)
@@ -277,16 +278,18 @@ def tile_tensormoe_pb_t_kernel(tc, h_pre, W_mo, weights_n, leak_n, out):
 
         def rsqrt_back(t):
             turn_back(square_sum[t], t)
+
+        def sum_lack(t):
             short = lacking.pop(t)
             for half in range(OC // P):
                 nc.tensor.matmul(
-                    out=square_sum[t][:, 0:1], lhsT=short[:, half * P : (half + 1) * P], rhs=one[:],
+                    out=out_sum[t + 2][:, OC : OC + 1], lhsT=short[:, half * P : (half + 1) * P], rhs=one[:],
                     start=(half == 0), stop=(half == OC // P - 1),
                 )
 
         def fetch_lack(t):
             nc.scalar.activation(
-                out=row_squares[:, t, HN - 1 : HN], in_=square_sum[t][:, 0:1], func=ACT.Copy, scale=-1.0 * HN
+                out=row_squares[:, t, HN - 1 : HN], in_=out_sum[t + 2][:, OC : OC + 1], func=ACT.Copy, scale=-1.0 * HN
             )
 
         def normalise(t):
@@ -376,22 +379,22 @@ def tile_tensormoe_pb_t_kernel(tc, h_pre, W_mo, weights_n, leak_n, out):
             nc.vector.tensor_reduce(out=f["offset"][:], in_=f["shift"][:], axis=AX.X, op=ALU.add)
             f["out"] = small("out_rows", [size(g), OC])
 
-        def diagonals(g, k):
+        def diagonals(g, k, name="diag"):
             f = stats[g]
-            f[("diag", k)] = work.tile([P, HN - 1, P], F32, name="diag", bufs=3)
+            f[("diag", k)] = work.tile([P, HN - 1, P], F32, name=name, bufs=1)
             for n in range(HN - 1):
                 nc.gpsimd.tensor_scalar(
                     out=f[("diag", k)][:, n, :], in0=ident[:], scalar1=f["diff"][:, k, n : n + 1], scalar2=0.0,
                     op0=ALU.mult, op1=ALU.add,
                 )
 
-        def combine(g, k, n, pool=None):
+        def new_out(j):
+            out_sum[j] = out_pool.tile([P, 2 * OC], F32, name="out_sum")
+
+        def combine(g, k, n, target=None):
             f = stats[g]
             if n == 0:
-                if pool is None:
-                    f[("sum", k)] = out_pool.tile([P, 2 * OC], F32, name="out_sum")
-                else:
-                    f[("sum", k)] = pool.tile([P, WORDS], F32, name="bank")
+                f[("sum", k)] = bank_pool.tile([P, WORDS], F32, name="bank") if target is None else target
             nc.tensor.matmul(
                 out=f[("sum", k)][:, 0:OC], lhsT=f[("diag", k)][:, n, :], rhs=normed[FIRST[g] + k][:, n, :],
                 start=(n == 0), stop=(n == HN - 2),
@@ -403,23 +406,19 @@ def tile_tensormoe_pb_t_kernel(tc, h_pre, W_mo, weights_n, leak_n, out):
                 out=f["out"][:, k, :], in_=f[("sum", k)][:, 0:OC], func=ACT.Identity, bias=f["offset"][:, k : k + 1]
             )
 
-        def output_on_tensor(g, k):
-            for n in range(HN - 1):
-                combine(g, k, n, bank_pool)
-            finish(g, k)
-
-        def output_on_vector(g, k):
+        def output_on_vector(g):
             f = stats[g]
-            u = normed[FIRST[g] + k]
-            nc.vector.tensor_scalar(
-                out=f["out"][:, k, :], in0=u[:, 0, :], scalar1=f["diff"][:, k, 0:1], scalar2=f["offset"][:, k : k + 1],
-                op0=ALU.mult, op1=ALU.add,
-            )
-            for n in (1, 2):
-                nc.vector.scalar_tensor_tensor(
-                    out=f["out"][:, k, :], in0=u[:, n, :], scalar=f["diff"][:, k, n : n + 1], in1=f["out"][:, k, :],
-                    op0=ALU.mult, op1=ALU.add,
+            for k in range(size(g)):
+                nc.scalar.activation(
+                    out=f["out"][:, k, :], in_=normed[FIRST[g] + k][:, 0, :], func=ACT.Identity, scale=f["diff"][:, k, 0:1],
+                    bias=f["offset"][:, k : k + 1],
                 )
+            for n in (1, 2):
+                for k in range(size(g)):
+                    nc.vector.scalar_tensor_tensor(
+                        out=f["out"][:, k, :], in0=normed[FIRST[g] + k][:, n, :], scalar=f["diff"][:, k, n : n + 1],
+                        in1=f["out"][:, k, :], op0=ALU.mult, op1=ALU.add,
+                    )
 
         def first_steps(g):
             for fn in (others, last_expert, row_mean, row_mean_squared, row_variance):
@@ -460,9 +459,13 @@ def tile_tensormoe_pb_t_kernel(tc, h_pre, W_mo, weights_n, leak_n, out):
             if live(j - 1):
                 multiply(2 * j - 2)
                 multiply(2 * j - 1)
-            output(diagonals, j + 1)
+            new_out(j)
+            output(diagonals, j)
             if live(j):
                 slope(s + 2)
+            output(finish, j - 1)
+            if j - 1 in turn_of and turn_of[j - 1][1] == size(turn_of[j - 1][0]) - 1:
+                store(turn_of[j - 1][0])
             if live(j - 2):
                 centre(j - 2)
                 square(j - 2)
@@ -476,7 +479,7 @@ def tile_tensormoe_pb_t_kernel(tc, h_pre, W_mo, weights_n, leak_n, out):
                 rectify(s + 1)
             if live(j + 1):
                 transposes(s + 4)
-            output(combine, j, 0)
+            output(combine, j, 0, out_sum[j])
             if live(j - 1):
                 weigh(j - 1)
             if live(j):
@@ -492,7 +495,7 @@ def tile_tensormoe_pb_t_kernel(tc, h_pre, W_mo, weights_n, leak_n, out):
                 transposes(s + 5)
             if live(j - 1):
                 negative_mean(j - 1)
-            output(combine, j, 1)
+            output(combine, j, 1, out_sum[j])
             if live(j + 1):
                 slope(s + 5)
                 transposes(s + 6)
@@ -500,12 +503,12 @@ def tile_tensormoe_pb_t_kernel(tc, h_pre, W_mo, weights_n, leak_n, out):
                 sum_squares(j - 2)
             if live(j - 1):
                 mean_back(j - 1)
-            output(combine, j, 2)
+            output(combine, j, 2, out_sum[j])
             if live(j - 2):
                 rsqrt(j - 2)
-            output(finish, j)
-            if live(j - 2):
-                rsqrt_back(j - 2)
+                if j < NT - 1:
+                    rsqrt_back(j - 2)
+                    sum_lack(j - 2)
 
             steps = []
             for g in range(NG):
@@ -522,6 +525,8 @@ def tile_tensormoe_pb_t_kernel(tc, h_pre, W_mo, weights_n, leak_n, out):
 
             if live(j):
                 quantise(2 * j)
+            if j == NT - 1:
+                quantise(2 * j + 1)
             one_step()
             for n in range(HN - 1):
                 if live(j + 2):
@@ -534,72 +539,69 @@ def tile_tensormoe_pb_t_kernel(tc, h_pre, W_mo, weights_n, leak_n, out):
             if live(j + 2):
                 add_parts(j + 2)
             one_step()
-            if live(j):
+            if 0 <= j < NT - 1:
                 quantise(2 * j + 1)
             while steps:
                 one_step()
             if j == 0:
                 for n in range(HN):
                     prepare_w(n)
-            if j in turn_of and turn_of[j][1] == size(turn_of[j][0]) - 1:
-                store(turn_of[j][0])
 
         last = NT - 1
-        g4, g2, g1, g0 = NG - 4, NG - 3, NG - 2, NG - 1
+        ga, gb = NG - 2, NG - 1
+        new_out(NT)
+        new_out(NT + 1)
         multiply(2 * last)
         multiply(2 * last + 1)
-        row_rsqrt(g4)
+        output(finish, last)
+        rsqrt_back(last - 2)
+        sum_lack(last - 2)
+        row_rsqrt(ga)
         fetch_lack(last - 2)
-        sum_normed_squares(last - 3)
-        diagonals(g4 - 1, 2)
+        diagonals(ga - 1, 3)
         centre(last - 1)
         square(last - 1)
-        diagonals(g4 - 1, 3)
-        normalise(last - 2)
-        last_steps(g4)
-        output_on_tensor(g4 - 1, 2)
         weigh(last)
+        normalise(last - 2)
         sum_weighted(last)
         negative_mean(last)
         mean_back(last)
-        output_on_tensor(g4 - 1, 3)
-        store(g4 - 1)
-        sum_normed_squares(last - 2)
-        diagonals(g4, 0)
-        diagonals(g4, 1)
+        sum_normed_squares(last - 3)
+        last_steps(ga)
         sum_squares(last - 1)
         rsqrt(last - 1)
+        combine(ga - 1, 3, 0)
         rsqrt_back(last - 1)
-        first_steps(g2)
+        sum_lack(last - 1)
         centre(last)
         square_on_three(last)
+        combine(ga - 1, 3, 1)
         fetch_lack(last - 1)
-        output_on_tensor(g4, 0)
+        sum_normed_squares(last - 2)
         normalise(last - 1)
+        for k in range(2):
+            diagonals(ga, k, "diag%d" % k)
         sum_squares(last)
         rsqrt(last)
+        combine(ga - 1, 3, 2)
         rsqrt_back(last)
-        diagonals(g4, 2)
-        diagonals(g4, 3)
+        sum_lack(last)
+        finish(ga - 1, 3)
+        store(ga - 1)
         sum_normed_squares(last - 1)
-        output_on_tensor(g4, 1)
-        last_steps(g2)
         fetch_lack(last)
         normalise(last)
-        output_on_tensor(g4, 2)
-        diagonals(g2, 0)
-        diagonals(g2, 1)
-        first_steps(g1)
+        for k in range(2, GROUP):
+            diagonals(ga, k, "diag%d" % k)
         sum_normed_squares(last)
-        output_on_tensor(g4, 3)
-        store(g4)
-        last_steps(g1)
-        output_on_tensor(g2, 0)
-        first_steps(g0)
-        output_on_vector(g1, 0)
-        store(g1)
-        last_steps(g0)
-        output_on_tensor(g2, 1)
-        store(g2)
-        output_on_vector(g0, 0)
-        store(g0)
+        for k in range(GROUP):
+            for n in range(HN - 1):
+                combine(ga, k, n)
+        first_steps(gb)
+        last_steps(gb)
+        finish(ga, 0)
+        output_on_vector(gb)
+        store(gb)
+        for k in range(1, GROUP):
+            finish(ga, k)
+        store(ga)

@@ -23,7 +23,7 @@ NG = len(FIRST) - 1
 FLOPS = 2 * B * HN * HM * OC
 
 AHEAD = 4
-COMBINE = 2
+COMBINE = 3
 RUN = 4
 STATS = 4
 
@@ -104,8 +104,8 @@ def tile_tensormoe_pb_t_kernel(tc, h_pre, W_mo, weights_n, leak_n, out):
             cols = slice(n * PASSES * OC, (n + 1) * PASSES * OC)
             nc.vector.quantize_mx(out=w_codes[:, cols].bitcast(FP8X4), scales=w_scales[:, cols], in_=grouped[:])
 
-        row_sum = const.tile([P, NT, HN], F32)
-        row_squares = const.tile([P, NT, HN], F32)
+        row_sums = const.tile([P, NT, 2, HN], F32)
+        nc.gpsimd.memset(row_sums[:], 0.0)
 
         def spread(x):
             return x.rearrange("p (s u v) -> p u s v", u=2, v=2 * RUN)
@@ -139,6 +139,14 @@ def tile_tensormoe_pb_t_kernel(tc, h_pre, W_mo, weights_n, leak_n, out):
             nc.vector.tensor_tensor(
                 out=signed[t][:, LAST], in0=signed[t][:, LAST], in1=negative.pop(t)[:], op=ALU.add,
             )
+
+        def prepare_rows(t):
+            flip(HN * t)
+            negative_part(t)
+            flip(HN * t + 1)
+            positive_part(t)
+            flip(HN * t + 2)
+            add_parts(t)
 
         def copy_out(s):
             q = s // 2
@@ -243,18 +251,22 @@ def tile_tensormoe_pb_t_kernel(tc, h_pre, W_mo, weights_n, leak_n, out):
         def mean_back(t):
             turn_back(mean_sum[t], t)
 
-        def centre(t):
-            centred[t] = work.tile([P, HN, OC], F32, name="centred", bufs=3)
+        def centre(t, pair):
+            if pair == 0:
+                centred[t] = work.tile([P, HN, OC], F32, name="centred", bufs=3)
+            experts = slice(2 * pair, 2 * pair + 2)
             nc.vector.tensor_tensor(
-                out=centred[t][:],
-                in0=weighted.pop(t)[:],
-                in1=mean_sum.pop(t)[:, OC : 2 * OC].unsqueeze(1).to_broadcast([P, HN, OC]),
+                out=centred[t][:, experts],
+                in0=weighted[t][:, experts],
+                in1=mean_sum[t][:, OC : 2 * OC].unsqueeze(1).to_broadcast([P, 2, OC]),
                 op=ALU.add,
             )
 
-        def square(t):
-            squares[t] = work.tile([P, HN, OC], F32, name="squares")
-            nc.gpsimd.tensor_tensor(out=squares[t][:], in0=centred[t][:], in1=centred[t][:], op=ALU.mult)
+        def square(t, pair):
+            if pair == 0:
+                squares[t] = work.tile([P, HN, OC], F32, name="squares")
+            c = centred[t][:, 2 * pair : 2 * pair + 2]
+            nc.gpsimd.tensor_tensor(out=squares[t][:, 2 * pair : 2 * pair + 2], in0=c, in1=c, op=ALU.mult)
 
         def square_on_three(t):
             squares[t] = work.tile([P, HN, OC], F32, name="squares")
@@ -289,7 +301,8 @@ def tile_tensormoe_pb_t_kernel(tc, h_pre, W_mo, weights_n, leak_n, out):
 
         def fetch_lack(t):
             nc.scalar.activation(
-                out=row_squares[:, t, HN - 1 : HN], in_=out_sum[t + 2][:, OC : OC + 1], func=ACT.Copy, scale=-1.0 * HN
+                out=row_sums[:, t, 1, HN - 1 : HN], in_=out_sum[t + 2][:, OC : OC + 1], func=ACT.Copy, scale=-1.0 * HN,
+                bias=1.0 * HN * OC,
             )
 
         def normalise(t):
@@ -297,7 +310,7 @@ def tile_tensormoe_pb_t_kernel(tc, h_pre, W_mo, weights_n, leak_n, out):
             for n in range(HN - 1):
                 nc.vector.scalar_tensor_tensor(
                     out=normed[t][:, n, :], in0=square_sum[t][:, OC : 2 * OC], scalar=1.0e8, in1=centred[t][:, n, :],
-                    op0=ALU.min, op1=ALU.mult, accum_out=row_sum[:, t, n : n + 1],
+                    op0=ALU.min, op1=ALU.mult, accum_out=row_sums[:, t, 0, n : n + 1],
                 )
             square_sum.pop(t)
             centred.pop(t)
@@ -306,7 +319,7 @@ def tile_tensormoe_pb_t_kernel(tc, h_pre, W_mo, weights_n, leak_n, out):
             for n in range(HN - 1):
                 unused = work.tile([P, OC], F32, name="unused")
                 nc.scalar.activation(
-                    out=unused[:], in_=normed[t][:, n, :], func=ACT.Square, accum_out=row_squares[:, t, n : n + 1]
+                    out=unused[:], in_=normed[t][:, n, :], func=ACT.Square, accum_out=row_sums[:, t, 1, n : n + 1]
                 )
 
         def size(g):
@@ -316,43 +329,31 @@ def tile_tensormoe_pb_t_kernel(tc, h_pre, W_mo, weights_n, leak_n, out):
             return work.tile([P] + shape, F32, name=name, bufs=4)
 
         def others(g):
-            ts = slice(FIRST[g], FIRST[g + 1])
-            f = {"sum3": small("sum3", [size(g)]), "squares3": small("squares3", [size(g)])}
-            nc.vector.tensor_reduce(out=f["sum3"][:], in_=row_sum[:, ts, 0 : HN - 1], axis=AX.X, op=ALU.add)
-            nc.vector.tensor_reduce(out=f["squares3"][:], in_=row_squares[:, ts, 0 : HN - 1], axis=AX.X, op=ALU.add)
-            stats[g] = f
-
-        def last_expert(g):
-            ts = slice(FIRST[g], FIRST[g + 1])
-            f = stats[g]
-            nc.vector.tensor_scalar_mul(out=row_sum[:, ts, HN - 1], in0=f["sum3"][:], scalar1=-1.0)
-            nc.vector.scalar_tensor_tensor(
-                out=row_squares[:, ts, HN - 1], in0=row_squares[:, ts, HN - 1], scalar=1.0 * HN * OC, in1=f["squares3"][:],
-                op0=ALU.add, op1=ALU.subtract,
+            stats[g] = {"others": small("others", [size(g), 2])}
+            nc.vector.tensor_reduce(
+                out=stats[g]["others"][:], in_=row_sums[:, FIRST[g] : FIRST[g + 1], :, 0 : HN - 1], axis=AX.X, op=ALU.add
             )
 
-        def row_mean(g):
-            f = stats[g]
-            f["mean"] = small("mean", [size(g), HN])
-            nc.vector.tensor_scalar_mul(out=f["mean"][:], in0=row_sum[:, FIRST[g] : FIRST[g + 1], :], scalar1=1.0 / OC)
+        def last_expert(g):
+            own = row_sums[:, FIRST[g] : FIRST[g + 1], :, HN - 1]
+            nc.vector.tensor_tensor(out=own, in0=own, in1=stats[g]["others"][:], op=ALU.subtract)
 
-        def row_mean_squared(g):
-            f = stats[g]
-            f["mean2"] = small("mean2", [size(g), HN])
-            nc.vector.tensor_tensor(out=f["mean2"][:], in0=f["mean"][:], in1=f["mean"][:], op=ALU.mult)
+        def row_squared(g):
+            stats[g]["squared"] = small("squared", [size(g), HN])
+            sums = row_sums[:, FIRST[g] : FIRST[g + 1], 0, :]
+            nc.vector.tensor_tensor(out=stats[g]["squared"][:], in0=sums, in1=sums, op=ALU.mult)
 
         def row_variance(g):
-            f = stats[g]
-            f["var"] = small("var", [size(g), HN])
+            stats[g]["var"] = small("var", [size(g), HN])
             nc.vector.scalar_tensor_tensor(
-                out=f["var"][:], in0=row_squares[:, FIRST[g] : FIRST[g + 1], :], scalar=1.0 / OC, in1=f["mean2"][:],
-                op0=ALU.mult, op1=ALU.subtract,
+                out=stats[g]["var"][:], in0=row_sums[:, FIRST[g] : FIRST[g + 1], 1, :], scalar=1.0 * OC,
+                in1=stats[g]["squared"][:], op0=ALU.mult, op1=ALU.subtract,
             )
 
         def row_rsqrt(g):
             f = stats[g]
             f["rsqrt"] = small("row_rsqrt", [size(g), HN])
-            nc.scalar.activation(out=f["rsqrt"][:], in_=f["var"][:], func=ACT.Abs_reciprocal_sqrt)
+            nc.scalar.activation(out=f["rsqrt"][:], in_=f["var"][:], func=ACT.Abs_reciprocal_sqrt, scale=1.0 / (OC * OC))
 
         def row_factor(g):
             f = stats[g]
@@ -365,7 +366,8 @@ def tile_tensormoe_pb_t_kernel(tc, h_pre, W_mo, weights_n, leak_n, out):
             f = stats[g]
             f["shift"] = small("shift", [size(g), HN])
             nc.vector.scalar_tensor_tensor(
-                out=f["shift"][:], in0=f["mean"][:], scalar=-1.0, in1=f["a"][:], op0=ALU.mult, op1=ALU.mult
+                out=f["shift"][:], in0=row_sums[:, FIRST[g] : FIRST[g + 1], 0, :], scalar=-1.0 / OC, in1=f["a"][:],
+                op0=ALU.mult, op1=ALU.mult,
             )
             f["diff"] = small("diff", [size(g), HN - 1])
             nc.vector.tensor_tensor(
@@ -381,7 +383,7 @@ def tile_tensormoe_pb_t_kernel(tc, h_pre, W_mo, weights_n, leak_n, out):
 
         def diagonals(g, k, name="diag"):
             f = stats[g]
-            f[("diag", k)] = work.tile([P, HN - 1, P], F32, name=name, bufs=1)
+            f[("diag", k)] = work.tile([P, HN - 1, P], F32, name=name, bufs=2)
             for n in range(HN - 1):
                 nc.gpsimd.tensor_scalar(
                     out=f[("diag", k)][:, n, :], in0=ident[:], scalar1=f["diff"][:, k, n : n + 1], scalar2=0.0,
@@ -421,7 +423,7 @@ def tile_tensormoe_pb_t_kernel(tc, h_pre, W_mo, weights_n, leak_n, out):
                     )
 
         def first_steps(g):
-            for fn in (others, last_expert, row_mean, row_mean_squared, row_variance):
+            for fn in (others, last_expert, row_squared, row_variance):
                 fn(g)
             row_rsqrt(g)
 
@@ -460,15 +462,16 @@ def tile_tensormoe_pb_t_kernel(tc, h_pre, W_mo, weights_n, leak_n, out):
                 multiply(2 * j - 2)
                 multiply(2 * j - 1)
             new_out(j)
-            output(diagonals, j)
             if live(j):
                 slope(s + 2)
             output(finish, j - 1)
             if j - 1 in turn_of and turn_of[j - 1][1] == size(turn_of[j - 1][0]) - 1:
                 store(turn_of[j - 1][0])
             if live(j - 2):
-                centre(j - 2)
-                square(j - 2)
+                for pair in range(2):
+                    centre(j - 2, pair)
+                    square(j - 2, pair)
+            output(diagonals, j + 1)
             if live(j - 3):
                 fetch_lack(j - 3)
             if live(j - STATS):
@@ -477,6 +480,9 @@ def tile_tensormoe_pb_t_kernel(tc, h_pre, W_mo, weights_n, leak_n, out):
                 rectify(s)
                 transposes(s + 3)
                 rectify(s + 1)
+            if j == 0:
+                rectify(s + 2)
+                prepare_rows(1)
             if live(j + 1):
                 transposes(s + 4)
             output(combine, j, 0, out_sum[j])
@@ -488,7 +494,7 @@ def tile_tensormoe_pb_t_kernel(tc, h_pre, W_mo, weights_n, leak_n, out):
                 sum_weighted(j - 1)
             if live(j - 3):
                 normalise(j - 3)
-            if live(j):
+            if live(j) and j > 0:
                 rectify(s + 2)
             if live(j + 1):
                 slope(s + 4)
@@ -514,7 +520,7 @@ def tile_tensormoe_pb_t_kernel(tc, h_pre, W_mo, weights_n, leak_n, out):
             for g in range(NG):
                 d = since_stats(g, j)
                 if d == 0:
-                    steps.extend([(fn, (g,)) for fn in (others, last_expert, row_mean, row_mean_squared, row_variance)])
+                    steps.extend([(fn, (g,)) for fn in (others, last_expert, row_squared, row_variance)])
                 if d == 1:
                     steps.extend([(fn, (g,)) for fn in (row_factor, row_terms, row_shift)])
 
@@ -529,14 +535,14 @@ def tile_tensormoe_pb_t_kernel(tc, h_pre, W_mo, weights_n, leak_n, out):
                 quantise(2 * j + 1)
             one_step()
             for n in range(HN - 1):
-                if live(j + 2):
+                if live(j + 2) and j != -1:
                     flip(s + 8 + n)
                     if n == 0:
                         negative_part(j + 2)
                     if n == 1:
                         positive_part(j + 2)
                 one_step()
-            if live(j + 2):
+            if live(j + 2) and j != -1:
                 add_parts(j + 2)
             one_step()
             if 0 <= j < NT - 1:
@@ -558,14 +564,18 @@ def tile_tensormoe_pb_t_kernel(tc, h_pre, W_mo, weights_n, leak_n, out):
         sum_lack(last - 2)
         row_rsqrt(ga)
         fetch_lack(last - 2)
+        for pair in range(2):
+            centre(last - 1, pair)
+            square(last - 1, pair)
         diagonals(ga - 1, 3)
-        centre(last - 1)
-        square(last - 1)
+        for n in range(HN - 1):
+            combine(ga - 1, 2, n)
         weigh(last)
         normalise(last - 2)
         sum_weighted(last)
         negative_mean(last)
         mean_back(last)
+        finish(ga - 1, 2)
         sum_normed_squares(last - 3)
         last_steps(ga)
         sum_squares(last - 1)
@@ -573,14 +583,15 @@ def tile_tensormoe_pb_t_kernel(tc, h_pre, W_mo, weights_n, leak_n, out):
         combine(ga - 1, 3, 0)
         rsqrt_back(last - 1)
         sum_lack(last - 1)
-        centre(last)
+        centre(last, 0)
+        centre(last, 1)
         square_on_three(last)
         combine(ga - 1, 3, 1)
         fetch_lack(last - 1)
         sum_normed_squares(last - 2)
         normalise(last - 1)
         for k in range(2):
-            diagonals(ga, k, "diag%d" % k)
+            diagonals(ga, k)
         sum_squares(last)
         rsqrt(last)
         combine(ga - 1, 3, 2)
@@ -592,7 +603,7 @@ def tile_tensormoe_pb_t_kernel(tc, h_pre, W_mo, weights_n, leak_n, out):
         fetch_lack(last)
         normalise(last)
         for k in range(2, GROUP):
-            diagonals(ga, k, "diag%d" % k)
+            diagonals(ga, k)
         sum_normed_squares(last)
         for k in range(GROUP):
             for n in range(HN - 1):

@@ -415,12 +415,16 @@ def tile_tensormoe_pb_t_kernel(tc, h_pre, W_mo, weights_n, leak_n, out):
                     out=f["out"][:, k, :], in_=normed[FIRST[g] + k][:, 0, :], func=ACT.Identity, scale=f["diff"][:, k, 0:1],
                     bias=f["offset"][:, k : k + 1],
                 )
-            for n in (1, 2):
-                for k in range(size(g)):
-                    nc.vector.scalar_tensor_tensor(
-                        out=f["out"][:, k, :], in0=normed[FIRST[g] + k][:, n, :], scalar=f["diff"][:, k, n : n + 1],
-                        in1=f["out"][:, k, :], op0=ALU.mult, op1=ALU.add,
-                    )
+            for first in range(0, size(g), 2):
+                for n in (1, 2):
+                    for k in (first, first + 1):
+                        nc.vector.scalar_tensor_tensor(
+                            out=f["out"][:, k, :], in0=normed[FIRST[g] + k][:, n, :], scalar=f["diff"][:, k, n : n + 1],
+                            in1=f["out"][:, k, :], op0=ALU.mult, op1=ALU.add,
+                        )
+                nc.sync.dma_start(
+                    out=out_view[:, FIRST[g] + first : FIRST[g] + first + 2, :], in_=f["out"][:, first : first + 2, :]
+                )
 
         def first_steps(g):
             for fn in (others, last_expert, row_squared, row_variance):
@@ -504,12 +508,14 @@ def tile_tensormoe_pb_t_kernel(tc, h_pre, W_mo, weights_n, leak_n, out):
             output(combine, j, 1, out_sum[j])
             if live(j + 1):
                 slope(s + 5)
-                transposes(s + 6)
             if live(j - 2):
                 sum_squares(j - 2)
+            if live(j + 1):
+                transposes(s + 6)
             if live(j - 1):
                 mean_back(j - 1)
-            output(combine, j, 2, out_sum[j])
+            if j < NT - 1:
+                output(combine, j, 2, out_sum[j])
             if live(j - 2):
                 rsqrt(j - 2)
                 if j < NT - 1:
@@ -559,34 +565,32 @@ def tile_tensormoe_pb_t_kernel(tc, h_pre, W_mo, weights_n, leak_n, out):
         new_out(NT + 1)
         multiply(2 * last)
         multiply(2 * last + 1)
-        output(finish, last)
+        output(combine, last, 2, out_sum[last])
         rsqrt_back(last - 2)
         sum_lack(last - 2)
         row_rsqrt(ga)
-        fetch_lack(last - 2)
         for pair in range(2):
             centre(last - 1, pair)
             square(last - 1, pair)
         diagonals(ga - 1, 3)
-        for n in range(HN - 1):
-            combine(ga - 1, 2, n)
         weigh(last)
+        output(finish, last)
         normalise(last - 2)
         sum_weighted(last)
         negative_mean(last)
         mean_back(last)
-        finish(ga - 1, 2)
+        fetch_lack(last - 2)
         sum_normed_squares(last - 3)
         last_steps(ga)
         sum_squares(last - 1)
         rsqrt(last - 1)
-        combine(ga - 1, 3, 0)
-        rsqrt_back(last - 1)
-        sum_lack(last - 1)
+        combine(ga - 1, 2, 0)
         centre(last, 0)
         centre(last, 1)
         square_on_three(last)
-        combine(ga - 1, 3, 1)
+        rsqrt_back(last - 1)
+        sum_lack(last - 1)
+        combine(ga - 1, 2, 1)
         fetch_lack(last - 1)
         sum_normed_squares(last - 2)
         normalise(last - 1)
@@ -594,14 +598,15 @@ def tile_tensormoe_pb_t_kernel(tc, h_pre, W_mo, weights_n, leak_n, out):
             diagonals(ga, k)
         sum_squares(last)
         rsqrt(last)
-        combine(ga - 1, 3, 2)
+        combine(ga - 1, 2, 2)
         rsqrt_back(last)
         sum_lack(last)
-        finish(ga - 1, 3)
-        store(ga - 1)
         sum_normed_squares(last - 1)
         fetch_lack(last)
         normalise(last)
+        finish(ga - 1, 2)
+        for n in range(HN - 1):
+            combine(ga - 1, 3, n)
         for k in range(2, GROUP):
             diagonals(ga, k)
         sum_normed_squares(last)
@@ -609,10 +614,10 @@ def tile_tensormoe_pb_t_kernel(tc, h_pre, W_mo, weights_n, leak_n, out):
             for n in range(HN - 1):
                 combine(ga, k, n)
         first_steps(gb)
+        finish(ga - 1, 3)
+        store(ga - 1)
         last_steps(gb)
-        finish(ga, 0)
         output_on_vector(gb)
-        store(gb)
-        for k in range(1, GROUP):
+        for k in range(GROUP):
             finish(ga, k)
         store(ga)

@@ -23,7 +23,7 @@ NG = len(FIRST) - 1
 FLOPS = 2 * B * HN * HM * OC
 
 AHEAD = 4
-COMBINE = 3
+COMBINE = 2
 RUN = 4
 STATS = 4
 
@@ -369,11 +369,6 @@ def tile_tensormoe_pb_t_kernel(tc, h_pre, W_mo, weights_n, leak_n, out):
                 out=f["shift"][:], in0=row_sums[:, FIRST[g] : FIRST[g + 1], 0, :], scalar=-1.0 / OC, in1=f["a"][:],
                 op0=ALU.mult, op1=ALU.mult,
             )
-            f["diff"] = small("diff", [size(g), HN - 1])
-            nc.vector.tensor_tensor(
-                out=f["diff"][:], in0=f["a"][:, :, 0 : HN - 1],
-                in1=f["a"][:, :, HN - 1 : HN].to_broadcast([P, size(g), HN - 1]), op=ALU.subtract,
-            )
 
         def row_shift(g):
             f = stats[g]
@@ -381,12 +376,20 @@ def tile_tensormoe_pb_t_kernel(tc, h_pre, W_mo, weights_n, leak_n, out):
             nc.vector.tensor_reduce(out=f["offset"][:], in_=f["shift"][:], axis=AX.X, op=ALU.add)
             f["out"] = small("out_rows", [size(g), OC])
 
+        def tile_factors(g, k):
+            f = stats[g]
+            f[("diff", k)] = small("diff", [HN - 1])
+            nc.vector.tensor_tensor(
+                out=f[("diff", k)][:], in0=f["a"][:, k, 0 : HN - 1],
+                in1=f["a"][:, k, HN - 1 : HN].to_broadcast([P, HN - 1]), op=ALU.subtract,
+            )
+
         def diagonals(g, k, name="diag"):
             f = stats[g]
             f[("diag", k)] = work.tile([P, HN - 1, P], F32, name=name, bufs=2)
             for n in range(HN - 1):
                 nc.gpsimd.tensor_scalar(
-                    out=f[("diag", k)][:, n, :], in0=ident[:], scalar1=f["diff"][:, k, n : n + 1], scalar2=0.0,
+                    out=f[("diag", k)][:, n, :], in0=ident[:], scalar1=f[("diff", k)][:, n : n + 1], scalar2=0.0,
                     op0=ALU.mult, op1=ALU.add,
                 )
 
@@ -412,14 +415,14 @@ def tile_tensormoe_pb_t_kernel(tc, h_pre, W_mo, weights_n, leak_n, out):
             f = stats[g]
             for k in range(size(g)):
                 nc.scalar.activation(
-                    out=f["out"][:, k, :], in_=normed[FIRST[g] + k][:, 0, :], func=ACT.Identity, scale=f["diff"][:, k, 0:1],
+                    out=f["out"][:, k, :], in_=normed[FIRST[g] + k][:, 0, :], func=ACT.Identity, scale=f[("diff", k)][:, 0:1],
                     bias=f["offset"][:, k : k + 1],
                 )
             for first in range(0, size(g), 2):
                 for n in (1, 2):
                     for k in (first, first + 1):
                         nc.vector.scalar_tensor_tensor(
-                            out=f["out"][:, k, :], in0=normed[FIRST[g] + k][:, n, :], scalar=f["diff"][:, k, n : n + 1],
+                            out=f["out"][:, k, :], in0=normed[FIRST[g] + k][:, n, :], scalar=f[("diff", k)][:, n : n + 1],
                             in1=f["out"][:, k, :], op0=ALU.mult, op1=ALU.add,
                         )
                 nc.sync.dma_start(
@@ -471,11 +474,12 @@ def tile_tensormoe_pb_t_kernel(tc, h_pre, W_mo, weights_n, leak_n, out):
             output(finish, j - 1)
             if j - 1 in turn_of and turn_of[j - 1][1] == size(turn_of[j - 1][0]) - 1:
                 store(turn_of[j - 1][0])
+            output(tile_factors, j)
+            output(diagonals, j)
             if live(j - 2):
                 for pair in range(2):
                     centre(j - 2, pair)
                     square(j - 2, pair)
-            output(diagonals, j + 1)
             if live(j - 3):
                 fetch_lack(j - 3)
             if live(j - STATS):
@@ -508,10 +512,9 @@ def tile_tensormoe_pb_t_kernel(tc, h_pre, W_mo, weights_n, leak_n, out):
             output(combine, j, 1, out_sum[j])
             if live(j + 1):
                 slope(s + 5)
+                transposes(s + 6)
             if live(j - 2):
                 sum_squares(j - 2)
-            if live(j + 1):
-                transposes(s + 6)
             if live(j - 1):
                 mean_back(j - 1)
             if j < NT - 1:
@@ -572,6 +575,7 @@ def tile_tensormoe_pb_t_kernel(tc, h_pre, W_mo, weights_n, leak_n, out):
         for pair in range(2):
             centre(last - 1, pair)
             square(last - 1, pair)
+        tile_factors(ga - 1, 3)
         diagonals(ga - 1, 3)
         weigh(last)
         output(finish, last)
@@ -582,15 +586,17 @@ def tile_tensormoe_pb_t_kernel(tc, h_pre, W_mo, weights_n, leak_n, out):
         fetch_lack(last - 2)
         sum_normed_squares(last - 3)
         last_steps(ga)
+        for k in range(GROUP):
+            tile_factors(ga, k)
         sum_squares(last - 1)
         rsqrt(last - 1)
-        combine(ga - 1, 2, 0)
+        combine(ga - 1, 3, 0)
         centre(last, 0)
         centre(last, 1)
         square_on_three(last)
         rsqrt_back(last - 1)
         sum_lack(last - 1)
-        combine(ga - 1, 2, 1)
+        combine(ga - 1, 3, 1)
         fetch_lack(last - 1)
         sum_normed_squares(last - 2)
         normalise(last - 1)
@@ -598,15 +604,14 @@ def tile_tensormoe_pb_t_kernel(tc, h_pre, W_mo, weights_n, leak_n, out):
             diagonals(ga, k)
         sum_squares(last)
         rsqrt(last)
-        combine(ga - 1, 2, 2)
+        combine(ga - 1, 3, 2)
         rsqrt_back(last)
         sum_lack(last)
         sum_normed_squares(last - 1)
         fetch_lack(last)
         normalise(last)
-        finish(ga - 1, 2)
-        for n in range(HN - 1):
-            combine(ga - 1, 3, n)
+        finish(ga - 1, 3)
+        store(ga - 1)
         for k in range(2, GROUP):
             diagonals(ga, k)
         sum_normed_squares(last)
@@ -614,9 +619,9 @@ def tile_tensormoe_pb_t_kernel(tc, h_pre, W_mo, weights_n, leak_n, out):
             for n in range(HN - 1):
                 combine(ga, k, n)
         first_steps(gb)
-        finish(ga - 1, 3)
-        store(ga - 1)
         last_steps(gb)
+        for k in range(GROUP):
+            tile_factors(gb, k)
         output_on_vector(gb)
         for k in range(GROUP):
             finish(ga, k)

@@ -64,17 +64,18 @@ def tile_tensormoe_pb_t_kernel(tc, h_pre, W_mo, weights_n, leak_n, out):
         for n in (0, 3, 1, 2):
             nc.sync.dma_start(out=rows[0][:, n * HM : (n + 1) * HM], in_=h_view[:, 0, n * HM : (n + 1) * HM])
         load(1)
-        load(2)
         for u in range(2):
             for r in range(RUN):
                 nc.sync.dma_start(out=w_raw[r::RUN, :, u, :], in_=w_view[r, u])
-        for t in range(3, AHEAD):
+        for t in range(2, AHEAD):
             load(t)
 
         ident = const.tile([P, P], F32)
         make_identity(nc, ident[:])
         one = const.tile([P, 1], F32)
         nc.vector.memset(one[:], 1.0)
+        ones = const.tile([P, OC], F32)
+        nc.gpsimd.memset(ones[:], 1.0)
         warm = const.tile([P, 1], F32)
         nc.scalar.activation(out=warm[:], in_=one[:], func=ACT.Abs_reciprocal_sqrt)
 
@@ -94,15 +95,18 @@ def tile_tensormoe_pb_t_kernel(tc, h_pre, W_mo, weights_n, leak_n, out):
 
         w_codes = const.tile([P, HN * PASSES * OC], U32, align_bytes=64)
         w_scales = const.tile([P, HN * PASSES * OC], U8, align_bytes=64)
-        w_from = w_raw[:].rearrange("p a u (e o) -> p a o (u e)", e=2, o=OC)
+        w_from = w_raw[:].rearrange("p a u (e c i) -> p a c (u e) i", e=2, i=4)
+        grouped = {}
 
-        def prepare_w(n):
-            grouped = work.tile([P, 2 * HM], BF16, name="rect", bufs=4, align_bytes=64)
-            to = grouped[:].rearrange("p (g o j) -> p g o j", g=PASSES, j=4)
+        def group_w(n):
+            grouped[n] = work.tile([P, 2 * HM], BF16, name="centred", bufs=3, align_bytes=64)
+            to = grouped[n][:].rearrange("p (g c i j) -> p g c j i", g=PASSES, i=4, j=4)
             nc.scalar.copy(out=to[:, 1], in_=w_from[:, n * PASSES + 1])
             nc.vector.tensor_copy(out=to[:, 0], in_=w_from[:, n * PASSES])
+
+        def quantise_w(n):
             cols = slice(n * PASSES * OC, (n + 1) * PASSES * OC)
-            nc.vector.quantize_mx(out=w_codes[:, cols].bitcast(FP8X4), scales=w_scales[:, cols], in_=grouped[:])
+            nc.vector.quantize_mx(out=w_codes[:, cols].bitcast(FP8X4), scales=w_scales[:, cols], in_=grouped.pop(n)[:])
 
         row_sums = const.tile([P, NT, 2, HN], F32)
         nc.gpsimd.memset(row_sums[:], 0.0)
@@ -253,7 +257,7 @@ def tile_tensormoe_pb_t_kernel(tc, h_pre, W_mo, weights_n, leak_n, out):
 
         def centre(t, pair):
             if pair == 0:
-                centred[t] = work.tile([P, HN, OC], F32, name="centred", bufs=3)
+                centred[t] = work.tile([P, HN, OC], F32, name="centred", bufs=3, align_bytes=64)
             experts = slice(2 * pair, 2 * pair + 2)
             nc.vector.tensor_tensor(
                 out=centred[t][:, experts],
@@ -457,6 +461,10 @@ def tile_tensormoe_pb_t_kernel(tc, h_pre, W_mo, weights_n, leak_n, out):
         def output(fn, j, *args):
             if j in turn_of:
                 fn(*turn_of[j], *args)
+            elif fn is combine and 3 <= j < 9:
+                nc.tensor.matmul(
+                    out=out_sum[j][:, 0:OC], lhsT=ident[:], rhs=ones[:], start=True, stop=True
+                )
 
         for j in range(-2, NT):
             s = HN * j
@@ -540,6 +548,9 @@ def tile_tensormoe_pb_t_kernel(tc, h_pre, W_mo, weights_n, leak_n, out):
 
             if live(j):
                 quantise(2 * j)
+            if j == 0:
+                for n in range(3):
+                    group_w(n)
             if j == NT - 1:
                 quantise(2 * j + 1)
             one_step()
@@ -559,8 +570,10 @@ def tile_tensormoe_pb_t_kernel(tc, h_pre, W_mo, weights_n, leak_n, out):
             while steps:
                 one_step()
             if j == 0:
-                for n in range(HN):
-                    prepare_w(n)
+                quantise_w(0)
+                group_w(3)
+                for n in range(1, HN):
+                    quantise_w(n)
 
         last = NT - 1
         ga, gb = NG - 2, NG - 1

@@ -214,18 +214,22 @@ def tile_tensormoe_pb_t_kernel(tc, h_pre, W_mo, weights_n, leak_n, out):
                         stop=(g == PASSES - 1),
                     )
 
-        def weigh(t):
+        def weigh(t, on_vector=()):
             weighted[t] = work.tile([P, HN, OC], F32, name="weighted", bufs=3)
             for n in range(HN):
-                nc.scalar.activation(
-                    out=weighted[t][:, n, :], in_=prod[2 * t + n // 2][:, n % 2, :], func=ACT.Copy,
-                    scale=signed_weights[:, t, n : n + 1],
-                )
+                out, product, factor = weighted[t][:, n, :], prod[2 * t + n // 2][:, n % 2, :], signed_weights[:, t, n : n + 1]
+                if n in on_vector:
+                    nc.vector.tensor_scalar(out=out, in0=product, scalar1=factor, scalar2=None, op0=ALU.mult)
+                else:
+                    nc.scalar.activation(out=out, in_=product, func=ACT.Copy, scale=factor)
             prod.pop(2 * t)
             prod.pop(2 * t + 1)
 
-        def sum_over_experts(terms):
-            total = sum_pool.tile([P, 2 * OC], F32, name="total")
+        def sum_over_experts(terms, pool=None):
+            if pool is None:
+                total = sum_pool.tile([P, 2 * OC], F32, name="total")
+            else:
+                total = pool.tile([P, WORDS], F32, name="bank")
             for half in range(OC // P):
                 for n in range(HN):
                     nc.tensor.matmul(
@@ -245,8 +249,8 @@ def tile_tensormoe_pb_t_kernel(tc, h_pre, W_mo, weights_n, leak_n, out):
                     total[:, OC + half * P : OC + (half + 1) * P], made[:, half * P : (half + 1) * P], ident[:]
                 )
 
-        def sum_weighted(t):
-            mean_sum[t] = sum_over_experts(weighted[t])
+        def sum_weighted(t, pool=None):
+            mean_sum[t] = sum_over_experts(weighted[t], pool)
 
         def negative_mean(t):
             turned[t] = work.tile([P, OC], F32, name="neg_mean")
@@ -279,8 +283,8 @@ def tile_tensormoe_pb_t_kernel(tc, h_pre, W_mo, weights_n, leak_n, out):
             nc.gpsimd.tensor_tensor(out=squares[t][:, 2, :], in0=centred[t][:, 2, :], in1=centred[t][:, 2, :], op=ALU.mult)
             nc.vector.tensor_tensor(out=squares[t][:, 3, :], in0=centred[t][:, 3, :], in1=centred[t][:, 3, :], op=ALU.mult)
 
-        def sum_squares(t):
-            square_sum[t] = sum_over_experts(squares.pop(t))
+        def sum_squares(t, pool=None):
+            square_sum[t] = sum_over_experts(squares.pop(t), pool)
 
         def rsqrt(t):
             turned[t] = work.tile([P, OC], F32, name="rsqrt")
@@ -418,10 +422,12 @@ def tile_tensormoe_pb_t_kernel(tc, h_pre, W_mo, weights_n, leak_n, out):
         def output_on_vector(g):
             f = stats[g]
             for k in range(size(g)):
-                nc.scalar.activation(
-                    out=f["out"][:, k, :], in_=normed[FIRST[g] + k][:, 0, :], func=ACT.Identity, scale=f[("diff", k)][:, 0:1],
-                    bias=f["offset"][:, k : k + 1],
-                )
+                out, u = f["out"][:, k, :], normed[FIRST[g] + k][:, 0, :]
+                factor, offset = f[("diff", k)][:, 0:1], f["offset"][:, k : k + 1]
+                if k < 2:
+                    nc.vector.tensor_scalar(out=out, in0=u, scalar1=factor, scalar2=offset, op0=ALU.mult, op1=ALU.add)
+                else:
+                    nc.scalar.activation(out=out, in_=u, func=ACT.Identity, scale=factor, bias=offset)
             for first in range(0, size(g), 2):
                 for n in (1, 2):
                     for k in (first, first + 1):
@@ -490,7 +496,7 @@ def tile_tensormoe_pb_t_kernel(tc, h_pre, W_mo, weights_n, leak_n, out):
                     square(j - 2, pair)
             if live(j - 3):
                 fetch_lack(j - 3)
-            if live(j - STATS):
+            if live(j - STATS) and j < NT - 1:
                 sum_normed_squares(j - STATS)
             if live(j):
                 rectify(s)
@@ -506,6 +512,8 @@ def tile_tensormoe_pb_t_kernel(tc, h_pre, W_mo, weights_n, leak_n, out):
                 weigh(j - 1)
             if live(j):
                 copy_out(s + 3)
+            if j == NT - 1:
+                sum_normed_squares(j - STATS)
             if live(j - 1):
                 sum_weighted(j - 1)
             if live(j - 3):
@@ -521,17 +529,16 @@ def tile_tensormoe_pb_t_kernel(tc, h_pre, W_mo, weights_n, leak_n, out):
             if live(j + 1):
                 slope(s + 5)
                 transposes(s + 6)
-            if live(j - 2):
+            if live(j - 2) and j < NT - 1:
                 sum_squares(j - 2)
-            if live(j - 1):
+            if live(j - 1) and j < NT - 1:
                 mean_back(j - 1)
             if j < NT - 1:
                 output(combine, j, 2, out_sum[j])
-            if live(j - 2):
+            if live(j - 2) and j < NT - 1:
                 rsqrt(j - 2)
-                if j < NT - 1:
-                    rsqrt_back(j - 2)
-                    sum_lack(j - 2)
+                rsqrt_back(j - 2)
+                sum_lack(j - 2)
 
             steps = []
             for g in range(NG):
@@ -581,45 +588,48 @@ def tile_tensormoe_pb_t_kernel(tc, h_pre, W_mo, weights_n, leak_n, out):
         new_out(NT + 1)
         multiply(2 * last)
         multiply(2 * last + 1)
+        mean_back(last - 1)
+        sum_squares(last - 2)
         output(combine, last, 2, out_sum[last])
-        rsqrt_back(last - 2)
-        sum_lack(last - 2)
+        tile_factors(ga - 1, 3)
+        diagonals(ga - 1, 3)
+        weigh(last, on_vector=(2, 3))
+        rsqrt(last - 2)
         row_rsqrt(ga)
         for pair in range(2):
             centre(last - 1, pair)
             square(last - 1, pair)
-        tile_factors(ga - 1, 3)
-        diagonals(ga - 1, 3)
-        weigh(last)
         output(finish, last)
+        sum_weighted(last, bank_pool)
+        rsqrt_back(last - 2)
         normalise(last - 2)
-        sum_weighted(last)
         negative_mean(last)
         mean_back(last)
+        sum_lack(last - 2)
         fetch_lack(last - 2)
         sum_normed_squares(last - 3)
-        last_steps(ga)
-        for k in range(GROUP):
-            tile_factors(ga, k)
-        sum_squares(last - 1)
-        rsqrt(last - 1)
-        combine(ga - 1, 3, 0)
         centre(last, 0)
         centre(last, 1)
         square_on_three(last)
+        sum_squares(last - 1)
+        combine(ga - 1, 3, 0)
+        sum_squares(last, bank_pool)
+        rsqrt(last - 1)
+        last_steps(ga)
+        for k in range(GROUP):
+            tile_factors(ga, k)
         rsqrt_back(last - 1)
+        rsqrt(last)
         sum_lack(last - 1)
-        combine(ga - 1, 3, 1)
+        normalise(last - 1)
         fetch_lack(last - 1)
         sum_normed_squares(last - 2)
-        normalise(last - 1)
         for k in range(2):
             diagonals(ga, k)
-        sum_squares(last)
-        rsqrt(last)
-        combine(ga - 1, 3, 2)
+        combine(ga - 1, 3, 1)
         rsqrt_back(last)
         sum_lack(last)
+        combine(ga - 1, 3, 2)
         sum_normed_squares(last - 1)
         fetch_lack(last)
         normalise(last)
@@ -631,11 +641,13 @@ def tile_tensormoe_pb_t_kernel(tc, h_pre, W_mo, weights_n, leak_n, out):
         for k in range(GROUP):
             for n in range(HN - 1):
                 combine(ga, k, n)
+        finish(ga, 0)
         first_steps(gb)
+        finish(ga, 1)
         last_steps(gb)
         for k in range(GROUP):
             tile_factors(gb, k)
         output_on_vector(gb)
-        for k in range(GROUP):
+        for k in (2, 3):
             finish(ga, k)
         store(ga)

from contextlib import ExitStack

import concourse.mybir as mybir
from concourse.masks import make_identity

F32 = mybir.dt.float32
BF16 = mybir.dt.bfloat16
U32 = mybir.dt.uint32
U8 = mybir.dt.uint8
FP8X4 = mybir.dt.float8_e4m3fn_x4
ALU = mybir.AluOpType
ACT = mybir.ActivationFunctionType
AX = mybir.AxisListType

P = 128
B, HN, HM, OC = 4096, 4, 1024, 256
NT = B // P
PASSES = HM // (4 * P)
WORDS = HM // 2
GROUP = 4
FIRST = list(range(0, NT - 4, GROUP)) + [NT - 4, NT]
NG = len(FIRST) - 1
FLOPS = 2 * B * HN * HM * OC

AHEAD = 4
COMBINE = 2
RUN = 4
STATS = 4


def tile_tensormoe_pb_t_kernel(tc, h_pre, W_mo, weights_n, leak_n, out):
    nc = tc.nc
    with ExitStack() as ctx:
        ctx.enter_context(tc.manual_schedule())
        const = ctx.enter_context(tc.tile_pool(name="const", bufs=1))
        work = ctx.enter_context(tc.tile_pool(name="work", bufs=2))
        bank_pool = ctx.enter_context(tc.psum_pool(name="bank_pool", bufs=3))
        prod_pool = ctx.enter_context(tc.psum_pool(name="prod_pool", bufs=2))
        sum_pool = ctx.enter_context(tc.psum_pool(name="sum_pool", bufs=2))
        out_pool = ctx.enter_context(tc.psum_pool(name="out_pool", bufs=1))

        h_view = h_pre.rearrange("(p t) n m -> p t (n m)", t=NT)
        out_view = out.rearrange("(p t) o -> p t o", t=NT)
        w_view = W_mo.rearrange("n (g s u r e) o -> r u s (n g) (e o)", g=PASSES, s=P // RUN, u=2, r=RUN, e=2)

        leak_bf = const.tile([P, HN], BF16)
        nc.sync.dma_start(out=leak_bf[:], in_=leak_n.partition_broadcast(P))
        weights_bf = const.tile([P, NT * HN], BF16)
        nc.sync.dma_start(out=weights_bf[:], in_=weights_n.rearrange("(p t) n -> p (t n)", t=NT))

        negative = {}
        rows, signed, bank, sloped, rect, quantised, prod, weighted, centred, squares = {}, {}, {}, {}, {}, {}, {}, {}, {}, {}
        out_sum, mean_sum, square_sum, turned, lacking, normed, stats = {}, {}, {}, {}, {}, {}, {}

        def new_rows(t):
            rows[t] = work.tile([P, HN * HM], BF16, name="rows", bufs=AHEAD + 1)

        def load(t):
            new_rows(t)
            nc.sync.dma_start(out=rows[t][:], in_=h_view[:, t, :])

        w_raw = const.tile([P, HN * PASSES, 2, 2 * OC], BF16)
        new_rows(0)
        for n in (0, 3, 1, 2):
            nc.sync.dma_start(out=rows[0][:, n * HM : (n + 1) * HM], in_=h_view[:, 0, n * HM : (n + 1) * HM])
        load(1)
        for u in range(2):
            for r in range(RUN):
                nc.sync.dma_start(out=w_raw[r::RUN, :, u, :], in_=w_view[r, u])
        for t in range(2, AHEAD):
            load(t)

        ident = const.tile([P, P], F32)
        make_identity(nc, ident[:])
        one = const.tile([P, 1], F32)
        nc.vector.memset(one[:], 1.0)
        ones = const.tile([P, OC], F32)
        nc.gpsimd.memset(ones[:], 1.0)
        warm = const.tile([P, 1], F32)
        nc.scalar.activation(out=warm[:], in_=one[:], func=ACT.Abs_reciprocal_sqrt)

        leak = const.tile([P, HN], F32)
        nc.vector.tensor_copy(out=leak[:], in_=leak_bf[:])
        sign = const.tile([P, HN], F32)
        nc.vector.tensor_scalar(out=sign[:], in0=leak[:], scalar1=1.0, scalar2=-2.0, op0=ALU.is_gt, op1=ALU.mult)
        nc.vector.tensor_scalar_add(out=sign[:], in0=sign[:], scalar1=1.0)
        nc.vector.memset(sign[:, HN - 1 : HN], 1.0)
        signed_weights = const.tile([P, NT, HN], F32)
        nc.vector.tensor_tensor(
            out=signed_weights[:],
            in0=weights_bf[:].rearrange("p (t n) -> p t n", n=HN),
            in1=sign[:].unsqueeze(1).to_broadcast([P, NT, HN]),
            op=ALU.mult,
        )

        w_codes = const.tile([P, HN * PASSES * OC], U32, align_bytes=64)
        w_scales = const.tile([P, HN * PASSES * OC], U8, align_bytes=64)
        w_from = w_raw[:].rearrange("p a u (e c i) -> p a c (u e) i", e=2, i=4)
        grouped = {}

        def group_w(n):
            grouped[n] = work.tile([P, 2 * HM], BF16, name="centred", bufs=3, align_bytes=64)
            to = grouped[n][:].rearrange("p (g c i j) -> p g c j i", g=PASSES, i=4, j=4)
            nc.scalar.copy(out=to[:, 1], in_=w_from[:, n * PASSES + 1])
            nc.vector.tensor_copy(out=to[:, 0], in_=w_from[:, n * PASSES])

        def quantise_w(n):
            cols = slice(n * PASSES * OC, (n + 1) * PASSES * OC)
            nc.vector.quantize_mx(out=w_codes[:, cols].bitcast(FP8X4), scales=w_scales[:, cols], in_=grouped.pop(n)[:])

        row_sums = const.tile([P, NT, 2, HN], F32)
        nc.gpsimd.memset(row_sums[:], 0.0)

        def spread(x):
            return x.rearrange("p (s u v) -> p u s v", u=2, v=2 * RUN)

        def flip(s):
            t, n = divmod(s, HN)
            if n == 0:
                signed[t] = work.tile([P, HN * HM], BF16, name="signed", bufs=3)
            cols = slice(n * HM, (n + 1) * HM)
            nc.vector.tensor_scalar(
                out=signed[t][:, cols].rearrange("p (u s v) -> p u s v", u=2, v=2 * RUN), in0=spread(rows[t][:, cols]),
                scalar1=sign[:, n : n + 1], scalar2=None, op0=ALU.mult,
            )

        LAST = slice((HN - 1) * HM, HN * HM)

        def negative_part(t):
            negative[t] = work.tile([P, HM], BF16, name="negative")
            nc.vector.tensor_scalar(
                out=negative[t][:].rearrange("p (u s v) -> p u s v", u=2, v=2 * RUN), in0=spread(rows[t][:, LAST]),
                scalar1=0.0, scalar2=leak[:, HN - 1 : HN], op0=ALU.min, op1=ALU.mult,
            )

        def positive_part(t):
            nc.vector.tensor_scalar(
                out=signed[t][:, LAST].rearrange("p (u s v) -> p u s v", u=2, v=2 * RUN), in0=spread(rows[t][:, LAST]),
                scalar1=0.0, scalar2=None, op0=ALU.max,
            )

        def add_parts(t):
            nc.vector.tensor_tensor(
                out=signed[t][:, LAST], in0=signed[t][:, LAST], in1=negative.pop(t)[:], op=ALU.add,
            )

        def prepare_rows(t):
            flip(HN * t)
            negative_part(t)
            flip(HN * t + 1)
            positive_part(t)
            flip(HN * t + 2)
            add_parts(t)

        def copy_out(s):
            q = s // 2
            nc.scalar.copy(
                out=rect[q][:, HM : 2 * HM].bitcast(F32).rearrange("p (w u) -> p w u", u=2),
                in_=bank.pop(s)[:].rearrange("p (u w) -> p w u", u=2),
            )

        def transposes(s):
            t, n = divmod(s, HN)
            words = signed[t][:].bitcast(F32)
            bank[s] = bank_pool.tile([P, WORDS], F32, name="bank")
            for u in range(2):
                for g in range(PASSES):
                    at = (u * PASSES + g) * P
                    first = n * WORDS + at
                    nc.tensor.transpose(bank[s][:, at : at + P], words[:, first : first + P], ident[:])

        def slope(s):
            t, n = divmod(s, HN)
            sloped[s] = work.tile([P, HM], BF16, name="sloped", bufs=3)
            x = bank[s][:].bitcast(BF16)
            nc.scalar.activation(out=sloped[s][:], in_=x, func=ACT.Copy, scale=leak[:, n : n + 1])

        def new_rect(q):
            rect[q] = work.tile([P, 2 * HM], BF16, name="rect", bufs=4, align_bytes=64)

        def rectify(s):
            q = s // 2
            if s % 4 == 0:
                new_rect(q)
                new_rect(q + 1)
            nc.vector.tensor_tensor(
                out=rect[q][:, (s % 2) * HM : (s % 2 + 1) * HM].rearrange("p (w u e) -> p w u e", u=2, e=2),
                in0=sloped.pop(s)[:].rearrange("p (u w e) -> p w u e", u=2, e=2),
                in1=bank.pop(s)[:].bitcast(BF16).rearrange("p (u w e) -> p w u e", u=2, e=2),
                op=ALU.max,
            )

        def quantise(q):
            codes = work.tile([P, HM // 2], U32, name="codes", bufs=4, align_bytes=64)
            scales = work.tile([P, HM // 2], U8, name="scales", bufs=4, align_bytes=64)
            nc.vector.quantize_mx(out=codes[:].bitcast(FP8X4), scales=scales[:], in_=rect.pop(q)[:])
            quantised[q] = (codes, scales)

        def multiply(q):
            codes, scales = quantised.pop(q)
            prod[q] = prod_pool.tile([P, 2, OC], F32, name="prod")
            for i in range(2):
                for g in range(PASSES):
                    h_cols = slice((i * PASSES + g) * P, (i * PASSES + g + 1) * P)
                    a = ((q % 2) * 2 + i) * PASSES + g
                    w_cols = slice(a * OC, (a + 1) * OC)
                    nc.tensor.matmul_mx(
                        out=prod[q][:, i, :],
                        lhsT=codes[:, h_cols].bitcast(FP8X4),
                        lhsT_scale=scales[:, h_cols],
                        rhs=w_codes[:, w_cols].bitcast(FP8X4),
                        rhs_scale=w_scales[:, w_cols],
                        start=(g == 0),
                        stop=(g == PASSES - 1),
                    )

        def weigh(t, on_vector=()):
            weighted[t] = work.tile([P, HN, OC], F32, name="weighted", bufs=3)
            for n in range(HN):
                out, product, factor = weighted[t][:, n, :], prod[2 * t + n // 2][:, n % 2, :], signed_weights[:, t, n : n + 1]
                if n in on_vector:
                    nc.vector.tensor_scalar(out=out, in0=product, scalar1=factor, scalar2=None, op0=ALU.mult)
                else:
                    nc.scalar.activation(out=out, in_=product, func=ACT.Copy, scale=factor)
            prod.pop(2 * t)
            prod.pop(2 * t + 1)

        def sum_over_experts(terms, pool=None):
            if pool is None:
                total = sum_pool.tile([P, 2 * OC], F32, name="total")
            else:
                total = pool.tile([P, WORDS], F32, name="bank")
            for half in range(OC // P):
                for n in range(HN):
                    nc.tensor.matmul(
                        out=total[:, half * P : (half + 1) * P],
                        lhsT=terms[:, n, half * P : (half + 1) * P],
                        rhs=ident[:],
                        start=(n == 0),
                        stop=(n == HN - 1),
                        is_transpose=True,
                    )
            return total

        def turn_back(total, t):
            made = turned.pop(t)
            for half in range(OC // P):
                nc.tensor.transpose(
                    total[:, OC + half * P : OC + (half + 1) * P], made[:, half * P : (half + 1) * P], ident[:]
                )

        def sum_weighted(t, pool=None):
            mean_sum[t] = sum_over_experts(weighted[t], pool)

        def negative_mean(t):
            turned[t] = work.tile([P, OC], F32, name="neg_mean")
            nc.scalar.activation(out=turned[t][:], in_=mean_sum[t][:, 0:OC], func=ACT.Copy, scale=-1.0 / HN)

        def mean_back(t):
            turn_back(mean_sum[t], t)

        def centre(t, pair):
            if pair == 0:
                centred[t] = work.tile([P, HN, OC], F32, name="centred", bufs=3, align_bytes=64)
            experts = slice(2 * pair, 2 * pair + 2)
            nc.vector.tensor_tensor(
                out=centred[t][:, experts],
                in0=weighted[t][:, experts],
                in1=mean_sum[t][:, OC : 2 * OC].unsqueeze(1).to_broadcast([P, 2, OC]),
                op=ALU.add,
            )

        def square(t, pair):
            if pair == 0:
                squares[t] = work.tile([P, HN, OC], F32, name="squares")
            c = centred[t][:, 2 * pair : 2 * pair + 2]
            nc.gpsimd.tensor_tensor(out=squares[t][:, 2 * pair : 2 * pair + 2], in0=c, in1=c, op=ALU.mult)

        def square_on_three(t):
            squares[t] = work.tile([P, HN, OC], F32, name="squares")
            for n in (0, 1):
                nc.scalar.activation(out=squares[t][:, n, :], in_=centred[t][:, n, :], func=ACT.Square)
            nc.gpsimd.tensor_tensor(out=squares[t][:, 2, :], in0=centred[t][:, 2, :], in1=centred[t][:, 2, :], op=ALU.mult)
            nc.vector.tensor_tensor(out=squares[t][:, 3, :], in0=centred[t][:, 3, :], in1=centred[t][:, 3, :], op=ALU.mult)

        def sum_squares(t, pool=None):
            square_sum[t] = sum_over_experts(squares.pop(t), pool)

        def rsqrt(t):
            turned[t] = work.tile([P, OC], F32, name="rsqrt")
            nc.scalar.activation(
                out=turned[t][:], in_=square_sum[t][:, 0:OC], func=ACT.Abs_reciprocal_sqrt, scale=1.0 / HN
            )
            lacking[t] = work.tile([P, OC], F32, name="lacking")
            nc.scalar.activation(
                out=lacking[t][:], in_=square_sum[t][:, 0:OC], func=ACT.Relu, scale=-1.0e16 / HN, bias=one[:]
            )

        def rsqrt_back(t):
            turn_back(square_sum[t], t)

        def sum_lack(t):
            short = lacking.pop(t)
            for half in range(OC // P):
                nc.tensor.matmul(
                    out=out_sum[t + 2][:, OC : OC + 1], lhsT=short[:, half * P : (half + 1) * P], rhs=one[:],
                    start=(half == 0), stop=(half == OC // P - 1),
                )

        def fetch_lack(t):
            nc.scalar.activation(
                out=row_sums[:, t, 1, HN - 1 : HN], in_=out_sum[t + 2][:, OC : OC + 1], func=ACT.Copy, scale=-1.0 * HN,
                bias=1.0 * HN * OC,
            )

        def normalise(t):
            normed[t] = work.tile([P, HN - 1, OC], F32, name="normed", bufs=11)
            for n in range(HN - 1):
                nc.vector.scalar_tensor_tensor(
                    out=normed[t][:, n, :], in0=square_sum[t][:, OC : 2 * OC], scalar=1.0e8, in1=centred[t][:, n, :],
                    op0=ALU.min, op1=ALU.mult, accum_out=row_sums[:, t, 0, n : n + 1],
                )
            square_sum.pop(t)
            centred.pop(t)

        def sum_normed_squares(t):
            for n in range(HN - 1):
                unused = work.tile([P, OC], F32, name="unused")
                nc.scalar.activation(
                    out=unused[:], in_=normed[t][:, n, :], func=ACT.Square, accum_out=row_sums[:, t, 1, n : n + 1]
                )

        def size(g):
            return FIRST[g + 1] - FIRST[g]

        def small(name, shape):
            return work.tile([P] + shape, F32, name=name, bufs=4)

        def others(g):
            stats[g] = {"others": small("others", [size(g), 2])}
            nc.vector.tensor_reduce(
                out=stats[g]["others"][:], in_=row_sums[:, FIRST[g] : FIRST[g + 1], :, 0 : HN - 1], axis=AX.X, op=ALU.add
            )

        def last_expert(g):
            own = row_sums[:, FIRST[g] : FIRST[g + 1], :, HN - 1]
            nc.vector.tensor_tensor(out=own, in0=own, in1=stats[g]["others"][:], op=ALU.subtract)

        def row_squared(g):
            stats[g]["squared"] = small("squared", [size(g), HN])
            sums = row_sums[:, FIRST[g] : FIRST[g + 1], 0, :]
            nc.vector.tensor_tensor(out=stats[g]["squared"][:], in0=sums, in1=sums, op=ALU.mult)

        def row_variance(g):
            stats[g]["var"] = small("var", [size(g), HN])
            nc.vector.scalar_tensor_tensor(
                out=stats[g]["var"][:], in0=row_sums[:, FIRST[g] : FIRST[g + 1], 1, :], scalar=1.0 * OC,
                in1=stats[g]["squared"][:], op0=ALU.mult, op1=ALU.subtract,
            )

        def row_rsqrt(g):
            f = stats[g]
            f["rsqrt"] = small("row_rsqrt", [size(g), HN])
            nc.scalar.activation(out=f["rsqrt"][:], in_=f["var"][:], func=ACT.Abs_reciprocal_sqrt, scale=1.0 / (OC * OC))

        def row_factor(g):
            f = stats[g]
            f["a"] = small("a", [size(g), HN])
            nc.vector.tensor_scalar(
                out=f["a"][:], in0=f["rsqrt"][:], scalar1=1.0e8, scalar2=1.0 / HN, op0=ALU.min, op1=ALU.mult
            )

        def row_terms(g):
            f = stats[g]
            f["shift"] = small("shift", [size(g), HN])
            nc.vector.scalar_tensor_tensor(
                out=f["shift"][:], in0=row_sums[:, FIRST[g] : FIRST[g + 1], 0, :], scalar=-1.0 / OC, in1=f["a"][:],
                op0=ALU.mult, op1=ALU.mult,
            )

        def row_shift(g):
            f = stats[g]
            f["offset"] = small("offset", [size(g)])
            nc.vector.tensor_reduce(out=f["offset"][:], in_=f["shift"][:], axis=AX.X, op=ALU.add)
            f["out"] = small("out_rows", [size(g), OC])

        def tile_factors(g, k):
            f = stats[g]
            f[("diff", k)] = small("diff", [HN - 1])
            nc.vector.tensor_tensor(
                out=f[("diff", k)][:], in0=f["a"][:, k, 0 : HN - 1],
                in1=f["a"][:, k, HN - 1 : HN].to_broadcast([P, HN - 1]), op=ALU.subtract,
            )

        def diagonals(g, k, name="diag"):
            f = stats[g]
            f[("diag", k)] = work.tile([P, HN - 1, P], F32, name=name, bufs=2)
            for n in range(HN - 1):
                nc.gpsimd.tensor_scalar(
                    out=f[("diag", k)][:, n, :], in0=ident[:], scalar1=f[("diff", k)][:, n : n + 1], scalar2=0.0,
                    op0=ALU.mult, op1=ALU.add,
                )

        def new_out(j):
            out_sum[j] = out_pool.tile([P, 2 * OC], F32, name="out_sum")

        def combine(g, k, n, target=None):
            f = stats[g]
            if n == 0:
                f[("sum", k)] = bank_pool.tile([P, WORDS], F32, name="bank") if target is None else target
            nc.tensor.matmul(
                out=f[("sum", k)][:, 0:OC], lhsT=f[("diag", k)][:, n, :], rhs=normed[FIRST[g] + k][:, n, :],
                start=(n == 0), stop=(n == HN - 2),
            )

        def finish(g, k):
            f = stats[g]
            nc.scalar.activation(
                out=f["out"][:, k, :], in_=f[("sum", k)][:, 0:OC], func=ACT.Identity, bias=f["offset"][:, k : k + 1]
            )

        def output_on_vector(g):
            f = stats[g]
            for k in range(size(g)):
                out, u = f["out"][:, k, :], normed[FIRST[g] + k][:, 0, :]
                factor, offset = f[("diff", k)][:, 0:1], f["offset"][:, k : k + 1]
                if k < 2:
                    nc.vector.tensor_scalar(out=out, in0=u, scalar1=factor, scalar2=offset, op0=ALU.mult, op1=ALU.add)
                else:
                    nc.scalar.activation(out=out, in_=u, func=ACT.Identity, scale=factor, bias=offset)
            for first in range(0, size(g), 2):
                for n in (1, 2):
                    for k in (first, first + 1):
                        nc.vector.scalar_tensor_tensor(
                            out=f["out"][:, k, :], in0=normed[FIRST[g] + k][:, n, :], scalar=f[("diff", k)][:, n : n + 1],
                            in1=f["out"][:, k, :], op0=ALU.mult, op1=ALU.add,
                        )
                nc.sync.dma_start(
                    out=out_view[:, FIRST[g] + first : FIRST[g] + first + 2, :], in_=f["out"][:, first : first + 2, :]
                )

        def first_steps(g):
            for fn in (others, last_expert, row_squared, row_variance):
                fn(g)
            row_rsqrt(g)

        def last_steps(g):
            for fn in (row_factor, row_terms, row_shift):
                fn(g)

        def store(g):
            nc.sync.dma_start(out=out_view[:, FIRST[g] : FIRST[g + 1], :], in_=stats.pop(g)["out"][:])

        def live(t):
            return 0 <= t < NT

        def since_stats(g, j):
            return j - (FIRST[g + 1] - 1 + STATS)

        turn_of = {}
        last_turn = 0
        for g in range(NG):
            for k in range(size(g)):
                last_turn = max(last_turn + 1, FIRST[g + 1] - 1 + STATS + COMBINE)
                turn_of[last_turn] = (g, k)

        def output(fn, j, *args):
            if j in turn_of:
                fn(*turn_of[j], *args)
            elif fn is combine and 3 <= j < 9:
                nc.tensor.matmul(
                    out=out_sum[j][:, 0:OC], lhsT=ident[:], rhs=ones[:], start=True, stop=True
                )

        for j in range(-2, NT):
            s = HN * j
            if j >= 0 and live(j + AHEAD):
                load(j + AHEAD)
            for g in range(NG):
                if since_stats(g, j) == 1:
                    row_rsqrt(g)
            if live(j - 1):
                multiply(2 * j - 2)
                multiply(2 * j - 1)
            new_out(j)
            if live(j):
                slope(s + 2)
            output(finish, j - 1)
            if j - 1 in turn_of and turn_of[j - 1][1] == size(turn_of[j - 1][0]) - 1:
                store(turn_of[j - 1][0])
            output(tile_factors, j)
            output(diagonals, j)
            if live(j - 2):
                for pair in range(2):
                    centre(j - 2, pair)
                    square(j - 2, pair)
            if live(j - 3):
                fetch_lack(j - 3)
            if live(j - STATS) and j < NT - 1:
                sum_normed_squares(j - STATS)
            if live(j):
                rectify(s)
                transposes(s + 3)
                rectify(s + 1)
            if j == 0:
                rectify(s + 2)
                prepare_rows(1)
            if live(j + 1):
                transposes(s + 4)
            output(combine, j, 0, out_sum[j])
            if live(j - 1):
                weigh(j - 1)
            if live(j):
                copy_out(s + 3)
            if j == NT - 1:
                sum_normed_squares(j - STATS)
            if live(j - 1):
                sum_weighted(j - 1)
            if live(j - 3):
                normalise(j - 3)
            if live(j) and j > 0:
                rectify(s + 2)
            if live(j + 1):
                slope(s + 4)
                transposes(s + 5)
            if live(j - 1):
                negative_mean(j - 1)
            output(combine, j, 1, out_sum[j])
            if live(j + 1):
                slope(s + 5)
                transposes(s + 6)
            if live(j - 2) and j < NT - 1:
                sum_squares(j - 2)
            if live(j - 1) and j < NT - 1:
                mean_back(j - 1)
            if j < NT - 1:
                output(combine, j, 2, out_sum[j])
            if live(j - 2) and j < NT - 1:
                rsqrt(j - 2)
                rsqrt_back(j - 2)
                sum_lack(j - 2)

            steps = []
            for g in range(NG):
                d = since_stats(g, j)
                if d == 0:
                    steps.extend([(fn, (g,)) for fn in (others, last_expert, row_squared, row_variance)])
                if d == 1:
                    steps.extend([(fn, (g,)) for fn in (row_factor, row_terms, row_shift)])

            def one_step():
                if steps:
                    fn, args = steps.pop(0)
                    fn(*args)

            if live(j):
                quantise(2 * j)
            if j == 0:
                for n in range(3):
                    group_w(n)
            if j == NT - 1:
                quantise(2 * j + 1)
            one_step()
            for n in range(HN - 1):
                if live(j + 2) and j != -1:
                    flip(s + 8 + n)
                    if n == 0:
                        negative_part(j + 2)
                    if n == 1:
                        positive_part(j + 2)
                one_step()
            if live(j + 2) and j != -1:
                add_parts(j + 2)
            one_step()
            if 0 <= j < NT - 1:
                quantise(2 * j + 1)
            while steps:
                one_step()
            if j == 0:
                quantise_w(0)
                group_w(3)
                for n in range(1, HN):
                    quantise_w(n)

        last = NT - 1
        ga, gb = NG - 2, NG - 1
        new_out(NT)
        new_out(NT + 1)
        multiply(2 * last)
        multiply(2 * last + 1)
        mean_back(last - 1)
        sum_squares(last - 2)
        output(combine, last, 2, out_sum[last])
        tile_factors(ga - 1, 3)
        diagonals(ga - 1, 3)
        weigh(last, on_vector=(2, 3))
        rsqrt(last - 2)
        row_rsqrt(ga)
        for pair in range(2):
            centre(last - 1, pair)
            square(last - 1, pair)
        output(finish, last)
        sum_weighted(last, bank_pool)
        rsqrt_back(last - 2)
        normalise(last - 2)
        negative_mean(last)
        mean_back(last)
        sum_lack(last - 2)
        fetch_lack(last - 2)
        sum_normed_squares(last - 3)
        centre(last, 0)
        centre(last, 1)
        square_on_three(last)
        sum_squares(last - 1)
        combine(ga - 1, 3, 0)
        sum_squares(last, bank_pool)
        rsqrt(last - 1)
        last_steps(ga)
        for k in range(GROUP):
            tile_factors(ga, k)
        rsqrt_back(last - 1)
        rsqrt(last)
        sum_lack(last - 1)
        normalise(last - 1)
        fetch_lack(last - 1)
        sum_normed_squares(last - 2)
        for k in range(2):
            diagonals(ga, k)
        combine(ga - 1, 3, 1)
        rsqrt_back(last)
        sum_lack(last)
        combine(ga - 1, 3, 2)
        sum_normed_squares(last - 1)
        fetch_lack(last)
        normalise(last)
        finish(ga - 1, 3)
        store(ga - 1)
        for k in range(2, GROUP):
            diagonals(ga, k)
        sum_normed_squares(last)
        for k in range(GROUP):
            for n in range(HN - 1):
                combine(ga, k, n)
        finish(ga, 0)
        first_steps(gb)
        finish(ga, 1)
        last_steps(gb)
        for k in range(GROUP):
            tile_factors(gb, k)
        output_on_vector(gb)
        for k in (2, 3):
            finish(ga, k)
        store(ga)
